import numpy as np
import ml_dtypes


def mxq(x, axis, fmt="e4m3"):
    dtype, down = {"e4m3": (ml_dtypes.float8_e4m3fn, 7), "e5m2": (ml_dtypes.float8_e5m2, 14)}[fmt]
    v = np.moveaxis(np.asarray(x, np.float32).astype(ml_dtypes.bfloat16).astype(np.float64), axis, -1)
    blocks = v.reshape(v.shape[:-1] + (-1, 32))
    amax = np.abs(blocks).max(-1, keepdims=True)
    byte = np.maximum(np.where(amax > 0, np.frexp(amax)[1] - 1 + 127, 0) - down, 1)
    scale = np.exp2(byte - 127.0)
    codes = (blocks / scale).astype(np.float32).astype(dtype).astype(np.float64)
    return np.moveaxis((codes * scale).reshape(v.shape), -1, axis)


WIDE = False


def mx_kscale(k):
    if not WIDE:
        return np.ones(k)
    levels = np.array([10, -10, 5, -5, 0])
    a = np.random.permutation(np.resize(levels, k // 512 * 4)).reshape(k // 512, 4)
    idx = np.arange(k)
    return np.exp2(a[idx // 512, idx % 128 // 32])


BF16 = ml_dtypes.bfloat16


def bf(x):
    return np.asarray(x, np.float32).astype(BF16)


def f64(x):
    return np.asarray(x).astype(np.float64)


B, I, H = 8192, 256, 256
K = I + H
DT = 1.0
EPS = 1e-6


def softplus(v):
    return np.logaddexp(v, 0.0)


def sigmoid(v):
    return 1.0 / (1.0 + np.exp(-v))


def setup_inputs():
    s = np.concatenate([mx_kscale(K)[:I], np.ones(H)])
    scale = (6.0 / ((1 + 5.0) * K)) ** 0.5
    return {"x": bf(np.random.standard_normal((B, I)) * s[:I]),
            "hidden": bf(np.random.standard_normal((B, H))),
            "W_tau": bf(np.random.uniform(-scale, scale, (H, K)) / s),
            "b_tau": bf(np.random.standard_normal(H) * 0.1),
            "W_r": bf(np.random.uniform(-scale, scale, (H, K)) / s),
            "b_r": bf(np.random.standard_normal(H) * 0.1),
            "W_h": bf(np.random.uniform(-scale, scale, (H, K)) / s),
            "b_h": bf(np.random.standard_normal(H) * 0.1)}


def reference(x, hidden, W_tau, b_tau, W_r, b_r, W_h, b_h):
    x, hidden = f64(x), f64(hidden)
    combined = np.concatenate([x, hidden], axis=1)
    cq = mxq(combined, 1, "e4m3")
    tau = softplus((cq @ mxq(f64(W_tau), 1, "e4m3").T) + f64(b_tau)) + EPS
    r = sigmoid((cq @ mxq(f64(W_r), 1, "e4m3").T) + f64(b_r))
    gated = r * hidden
    cand_in = np.concatenate([x, gated], axis=1)
    h_tilde = np.tanh((mxq(cand_in, 1, "e4m3") @ mxq(f64(W_h), 1, "e4m3").T) + f64(b_h))
    return hidden + DT * (h_tilde - hidden) / tau

@@ -1,0 +1,219 @@
+from contextlib import ExitStack
+
+import concourse.mybir as mybir
+from concourse.masks import make_identity
+
+F32 = mybir.dt.float32
+BF16 = mybir.dt.bfloat16
+U32 = mybir.dt.uint32
+U8 = mybir.dt.uint8
+FP8X4 = mybir.dt.float8_e4m3fn_x4
+ACT = mybir.ActivationFunctionType
+ALU = mybir.AluOpType
+
+P = 128
+B, I, H = 8192, 256, 256
+FLOPS = 3 * 2 * B * (I + H) * H
+ROWS = B // P
+UNITS = 8
+UROWS = ROWS // UNITS
+PAIRS = UROWS // 2
+NCOL = PAIRS * P
+UW = 4 * NCOL
+EPS = 1e-6
+
+PLAN = (("setup",),("wload",0,),("load",0,),("wload",1,),("bload",),("load",1,),("wprep",0,),("tin",0,0,),("tin",0,1,),("tin",0,2,),("tin",0,3,),("tinq",0,),("load",2,),("wprep",1,),("bprep",),("wload",2,),("tin",1,0,),("tin",1,1,),("tin",1,2,),("tin",1,3,),("tinq",1,),("load",3,),("tr",0,0,),("tr",0,1,),("tr",0,2,),("tr",0,3,),("gate",0,),("tr",1,0,),("tr",1,1,),("tr",1,2,),("tr",1,3,),("tin",2,0,),("tin",2,1,),("tin",2,2,),("tin",2,3,),("tinq",2,),("load",4,),("ln",0,),("lnb",0,),("gate",1,),("wprep",2,),("ln",1,),("lnb",1,),("tin",3,0,),("tin",3,1,),("tin",3,2,),("tin",3,3,),("tinq",3,),("load",5,),("tin",4,0,),("tin",4,1,),("tin",4,2,),("tin",4,3,),("tinq",4,),("load",6,),("hb",0,0,"v",),("rho",0,0,),("t2",0,0,"g",1,),("hb",0,1,"v",),("rho",0,1,),("t2",0,1,"g",1,),("hb",0,2,"v",),("rho",0,2,),("t2",0,2,"g",1,),("hb",0,3,"v",),("rho",0,3,),("t2",0,3,"g",1,),("tr",2,0,),("tr",2,1,),("tr",2,2,),("tr",2,3,),("gate",2,),("hb",1,0,"v",),("rho",1,0,),("t2",1,0,"g",1,),("hb",1,1,"v",),("rho",1,1,),("t2",1,1,"g",1,),("hb",1,2,"v",),("rho",1,2,),("t2",1,2,"g",1,),("hb",1,3,"v",),("rho",1,3,),("t2",1,3,"g",1,),("load2",0,),("back",0,0,),("back",0,1,),("back",0,2,),("back",0,3,),("tr",3,0,),("tr",3,1,),("tr",3,2,),("tr",3,3,),("gate",3,),("load2",1,),("back",1,0,),("back",1,1,),("back",1,2,),("back",1,3,),("tr",4,0,),("tr",4,1,),("tr",4,2,),("tr",4,3,),("ln",2,),("lnb",2,),("gate",4,),("tin",5,0,),("tin",5,1,),("tin",5,2,),("tin",5,3,),("tinq",5,),("load",7,),("ln",3,),("lnb",3,),("tin",6,0,),("tin",6,1,),("tin",6,2,),("tin",6,3,),("tinq",6,),("ln",4,),("lnb",4,),("tin",7,0,),("tin",7,1,),("tin",7,2,),("tin",7,3,),("tinq",7,),("hb",2,0,"v",),("rho",2,0,),("t2",2,0,"g",1,),("hb",2,1,"v",),("rho",2,1,),("t2",2,1,"g",1,),("hb",2,2,"v",),("rho",2,2,),("t2",2,2,"g",1,),("hb",2,3,"v",),("rho",2,3,),("t2",2,3,"g",1,),("tr",5,0,),("tr",5,1,),("tr",5,2,),("tr",5,3,),("gate",5,),("hb",3,0,"v",),("rho",3,0,),("t2",3,0,"g",1,),("hb",3,1,"v",),("rho",3,1,),("t2",3,1,"g",1,),("hb",3,2,"v",),("rho",3,2,),("t2",3,2,"g",1,),("hb",3,3,"v",),("rho",3,3,),("t2",3,3,"g",1,),("load2",2,),("back",2,0,),("back",2,1,),("back",2,2,),("back",2,3,),("tr",6,0,),("tr",6,1,),("tr",6,2,),("tr",6,3,),("gate",6,),("hb",4,0,"v",),("rho",4,0,),("t2",4,0,"g",1,),("hb",4,1,"v",),("rho",4,1,),("t2",4,1,"g",1,),("hb",4,2,"v",),("rho",4,2,),("t2",4,2,"g",1,),("hb",4,3,"v",),("rho",4,3,),("t2",4,3,"g",1,),("load2",3,),("back",3,0,),("back",3,1,),("back",3,2,),("back",3,3,),("tr",7,0,),("tr",7,1,),("tr",7,2,),("tr",7,3,),("ln",5,),("lnb",5,),("gate",7,),("load2",4,),("back",4,0,),("back",4,1,),("back",4,2,),("back",4,3,),("ln",6,),("lnb",6,),("ln",7,),("lnb",7,),("hb",5,0,"v",),("rho",5,0,),("t2",5,0,"g",1,),("hb",5,1,"v",),("rho",5,1,),("t2",5,1,"g",1,),("hb",5,2,"v",),("rho",5,2,),("t2",5,2,"g",1,),("hb",5,3,"v",),("rho",5,3,),("t2",5,3,"g",1,),("hb",6,0,"v",),("rho",6,0,),("t2",6,0,"g",1,),("hb",6,1,"v",),("rho",6,1,),("t2",6,1,"g",1,),("hb",6,2,"v",),("rho",6,2,),("t2",6,2,"g",1,),("hb",6,3,"v",),("rho",6,3,),("t2",6,3,"g",1,),("load2",5,),("back",5,0,),("back",5,1,),("back",5,2,),("back",5,3,),("hb",7,0,"v",),("rho",7,0,),("t2",7,0,"g",1,),("hb",7,1,"v",),("rho",7,1,),("t2",7,1,"g",1,),("hb",7,2,"v",),("rho",7,2,),("t2",7,2,"g",1,),("hb",7,3,"v",),("rho",7,3,),("t2",7,3,"g",1,),("load2",6,),("back",6,0,),("back",6,1,),("back",6,2,),("back",6,3,),("load2",7,),("back",7,0,),("back",7,1,),("back",7,2,),("back",7,3,),)
+BUFS = {"th":2,"ht":3,"xn":2,"hn":2,"h2":2,"xg":2,"hg":8,"xc":8,"hc":5,"hh":2,"dg":2,"dc":6,"ee":5,"oo":4}
+
+
+def tile_ltccell_t_kernel(tc, x, hidden, W_tau, b_tau, W_r, b_r, W_h, b_h, out):
+    nc = tc.nc
+    xv = x.rearrange("(p q) k -> p (q k)", q=ROWS)
+    hv = hidden.rearrange("(p q) k -> p (q k)", q=ROWS)
+    ov = out.rearrange("(p q) k -> p (q k)", q=ROWS)
+    weights = (W_tau, W_r, W_h)
+    biases = (b_tau, b_r, b_h)
+
+    with ExitStack() as ctx:
+        const = ctx.enter_context(tc.tile_pool(name="const", bufs=1))
+        work = ctx.enter_context(tc.tile_pool(name="work", bufs=2))
+        psum = ctx.enter_context(tc.psum_pool(name="psum", bufs=8))
+        ctx.enter_context(tc.manual_schedule())
+
+        ident = const.tile([P, P], F32, name="ident")
+        cst = const.tile([P, 2], F32, name="cst")
+        braw = const.tile([P, 3, 16], BF16, name="braw")
+        bias = const.tile([P, 12], F32, name="bias")
+        wc = const.tile([P, 3 * 1024], U32, name="wc", align_bytes=64)
+        ws = const.tile([P, 3 * 1024], U8, name="ws", align_bytes=64)
+
+        xn, hn, h2, hg, xc, xs, hc, hs = {}, {}, {}, {}, {}, {}, {}, {}
+        dc, ds, th, ee, ht, wn, xg = {}, {}, {}, {}, {}, {}, {}
+
+        def transpose_in(src_words, n_pairs, dst_words, evac, pieces=None):
+            sv = src_words.rearrange("p (s m u) -> p s m u", s=n_pairs, m=P, u=2)
+            dv = dst_words.rearrange("p (s m u) -> p s m u", s=n_pairs, m=P, u=2)
+            for sb in pieces or range(n_pairs // 2):
+                bank = psum.tile([P, 2, 2, P], F32, name="tin", tag="bank")
+                for s2 in range(2):
+                    for u in range(2):
+                        nc.tensor.transpose(bank[:, s2, u, :], sv[:, 2 * sb + s2, :, u], ident[:])
+                evac(out=dv[:, 2 * sb : 2 * sb + 2, :, :], in_=bank[:].rearrange("p s u m -> p s m u"))
+
+        def setup():
+            make_identity(nc, ident[:])
+            nc.vector.memset(cst[:, 0:1], 1.0)
+            nc.vector.memset(cst[:, 1:2], EPS)
+
+        def wload(w):
+            wn[w] = work.tile([P, 4096], BF16, name="wn", tag="ee", bufs=BUFS["ee"])
+            z = wn[w][:].bitcast(F32).rearrange("p (a h m) -> p a h m", a=8, h=2, m=P)
+            nc.gpsimd.memset(z[0:64, :, 1, :], 0.0)
+            nc.gpsimd.memset(z[64:128, :, 0, :], 0.0)
+            src = weights[w].rearrange("(j r) k -> j (r k)", r=4).rearrange("j (a k) -> j a k", k=256)
+            dst = wn[w][:].rearrange("p (a h k) -> p a h k", a=8, h=2, k=256)
+            nc.scalar.dma_start(out=dst[0:64, :, 0, :], in_=src)
+            nc.scalar.dma_start(out=dst[64:128, :, 1, :], in_=src)
+
+        def bload():
+            for w in range(3):
+                src = biases[w].rearrange("(j t) -> j t", t=4)
+                nc.scalar.dma_start(out=braw[0:64, w, 0:4], in_=src)
+                nc.scalar.dma_start(out=braw[64:128, w, 0:4], in_=src)
+
+        def bprep():
+            bv = bias[:].rearrange("p (w t) -> p w t", w=3)
+            nc.vector.tensor_copy(out=bv, in_=braw[:, :, 0:4])
+            nc.vector.tensor_scalar(out=bias[:, 4:8], in0=bias[:, 4:8], scalar1=0.5, scalar2=None, op0=ALU.mult)
+
+        def wprep(w):
+            wg = work.tile([P, 2048], F32, name="wg", tag="ht", bufs=BUFS["ht"], align_bytes=64)
+            transpose_in(wn[w][:].bitcast(F32), 8, wg[:], nc.scalar.copy)
+            cols = slice(w * 1024, (w + 1) * 1024)
+            nc.vector.quantize_mx(out=wc[:, cols].bitcast(FP8X4), scales=ws[:, cols], in_=wg[:].bitcast(BF16))
+
+        def load(u):
+            cols = slice(u * UW, (u + 1) * UW)
+            xn[u] = work.tile([P, UW], BF16, name="xn", tag="xn", bufs=BUFS["xn"])
+            nc.sync.dma_start(out=xn[u][:], in_=xv[:, cols])
+            hn[u] = work.tile([P, UW], BF16, name="hn", tag="hn", bufs=BUFS["hn"])
+            nc.sync.dma_start(out=hn[u][:], in_=hv[:, cols])
+
+        def load2(u):
+            h2[u] = work.tile([P, UW], BF16, name="h2", tag="h2", bufs=BUFS["h2"])
+            nc.sync.dma_start(out=h2[u][:], in_=hv[:, u * UW : (u + 1) * UW])
+
+        def tin(u, i):
+            if i == 0:
+                xg[u] = work.tile([P, UW // 2], F32, name="xg", tag="xg", bufs=BUFS["xg"], align_bytes=64)
+                hg[u] = work.tile([P, UW // 2], F32, name="hg", tag="hg", bufs=BUFS["hg"], align_bytes=64)
+            if i < 2:
+                transpose_in(xn[u][:].bitcast(F32), PAIRS, xg[u][:], nc.vector.tensor_copy, (i,))
+            else:
+                transpose_in(hn[u][:].bitcast(F32), PAIRS, hg[u][:], nc.vector.tensor_copy, (i - 2,))
+
+        def tinq(u):
+            xc[u] = work.tile([P, NCOL], U32, name="xc", tag="xc", bufs=BUFS["xc"], align_bytes=64)
+            xs[u] = work.tile([P, NCOL], U8, name="xs", tag="xs", bufs=BUFS["xc"], align_bytes=64)
+            hc[u] = work.tile([P, NCOL], U32, name="hc", tag="hc", bufs=BUFS["hc"], align_bytes=64)
+            hs[u] = work.tile([P, NCOL], U8, name="hs", tag="hs", bufs=BUFS["hc"], align_bytes=64)
+            nc.vector.quantize_mx(out=xc[u][:].bitcast(FP8X4), scales=xs[u][:], in_=xg[u][:].bitcast(BF16))
+            nc.vector.quantize_mx(out=hc[u][:].bitcast(FP8X4), scales=hs[u][:], in_=hg[u][:].bitcast(BF16))
+
+        def mx_pair(w, t, c1, s1, c2, s2):
+            bank = psum.tile([P, NCOL], F32, name="mx", tag="bank")
+            for part, (cc, ss) in enumerate(((c1, s1), (c2, s2))):
+                o = w * 1024 + (2 * t + part) * P
+                nc.tensor.matmul_mx(
+                    out=bank[:],
+                    lhsT=wc[:, o : o + P].bitcast(FP8X4),
+                    lhsT_scale=ws[:, o : o + P],
+                    rhs=cc[:].bitcast(FP8X4),
+                    rhs_scale=ss[:],
+                    start=(part == 0),
+                    stop=(part == 1),
+                )
+            return bank
+
+        def tr(u, t):
+            if t == 0:
+                ee[u] = work.tile([P, UW], F32, name="ee", tag="ee", bufs=BUFS["ee"])
+                th[u] = work.tile([P, UW], F32, name="th", tag="th", bufs=BUFS["th"], align_bytes=64)
+            sl = slice(t * NCOL, (t + 1) * NCOL)
+            bank = mx_pair(0, t, xc[u], xs[u], hc[u], hs[u])
+            nc.scalar.activation(out=ee[u][:, sl], in_=bank[:], func=ACT.Exp, bias=bias[:, t : t + 1], scale=1.0)
+            bank = mx_pair(1, t, xc[u], xs[u], hc[u], hs[u])
+            nc.scalar.activation(out=th[u][:, sl], in_=bank[:], func=ACT.Tanh, bias=bias[:, 4 + t : 5 + t], scale=0.5)
+
+        def gate(u):
+            hh = work.tile([P, UW], BF16, name="hh", tag="hh", bufs=BUFS["hh"])
+            nc.vector.tensor_scalar(out=hh[:], in0=hg[u][:].bitcast(BF16), scalar1=0.5, scalar2=None, op0=ALU.mult)
+            dg = work.tile([P, UW], BF16, name="dg", tag="dg", bufs=BUFS["dg"], align_bytes=64)
+            nc.vector.scalar_tensor_tensor(
+                out=dg[:].rearrange("p (c t) -> p c t", t=4),
+                in0=th[u][:].rearrange("p (t c) -> p c t", t=4),
+                scalar=1.0,
+                in1=hh[:].rearrange("p (c t) -> p c t", t=4),
+                op0=ALU.add,
+                op1=ALU.mult,
+            )
+            dc[u] = work.tile([P, NCOL], U32, name="dc", tag="dc", bufs=BUFS["dc"], align_bytes=64)
+            ds[u] = work.tile([P, NCOL], U8, name="ds", tag="ds", bufs=BUFS["dc"], align_bytes=64)
+            nc.vector.quantize_mx(out=dc[u][:].bitcast(FP8X4), scales=ds[u][:], in_=dg[:])
+
+        def ln(u):
+            nc.scalar.activation(out=ee[u][:], in_=ee[u][:], func=ACT.Ln, bias=cst[:, 0:1], scale=1.0)
+
+        def lnb(u):
+            nc.scalar.activation(out=ee[u][:], in_=ee[u][:], func=ACT.Ln, bias=cst[:, 1:2], scale=1.0)
+
+        def rho(u, t=None):
+            sl = slice(0, UW) if t is None else slice(t * NCOL, (t + 1) * NCOL)
+            nc.scalar.activation(out=ee[u][:, sl], in_=ee[u][:, sl], func=ACT.Exp, scale=-1.0)
+
+        def ars(u, t=None):
+            sl = slice(0, UW) if t is None else slice(t * NCOL, (t + 1) * NCOL)
+            nc.scalar.activation(out=ee[u][:, sl], in_=ee[u][:, sl], func=ACT.Abs_reciprocal_sqrt, bias=cst[:, 1:2], scale=1.0)
+
+        def sq(u, t=None):
+            sl = slice(0, UW) if t is None else slice(t * NCOL, (t + 1) * NCOL)
+            nc.scalar.activation(out=ee[u][:, sl], in_=ee[u][:, sl], func=ACT.Square)
+
+        engines = {"v": nc.vector, "g": nc.gpsimd}
+
+        def hb(u, t, e1):
+            if t == 0:
+                ht[u] = work.tile([P, UW], F32, name="ht", tag="ht", bufs=BUFS["ht"], align_bytes=64)
+            hgt = hg[u][:].bitcast(BF16).rearrange("p (c t) -> p t c", t=4)
+            sl = slice(t * NCOL, (t + 1) * NCOL)
+            bank = mx_pair(2, t, xc[u], xs[u], dc[u], ds[u])
+            nc.scalar.activation(out=ht[u][:, sl], in_=bank[:], func=ACT.Tanh, bias=bias[:, 8 + t : 9 + t], scale=1.0)
+            engines[e1].tensor_tensor(out=ht[u][:, sl], in0=ht[u][:, sl], in1=hgt[:, t, :], op=ALU.subtract)
+
+        def t2(u, t, e2, times=2):
+            sl = slice(t * NCOL, (t + 1) * NCOL)
+            for i in range(times):
+                engines[e2].tensor_tensor(out=ht[u][:, sl], in0=ht[u][:, sl], in1=ee[u][:, sl], op=ALU.mult)
+
+        def back(u, s):
+            tb = psum.tile([P, 4, P], F32, name="tb", tag="bank")
+            for t in range(4):
+                o = t * NCOL + s * P
+                nc.tensor.transpose(tb[:, t, :], ht[u][:, o : o + P], ident[:])
+            oo = work.tile([P, NCOL], F32, name="oo", tag="oo", bufs=BUFS["oo"])
+            nc.vector.tensor_tensor(
+                out=oo[:].rearrange("p (m t) -> p m t", t=4),
+                in0=tb[:].rearrange("p t m -> p m t"),
+                in1=h2[u][:, s * NCOL : (s + 1) * NCOL].rearrange("p (m t) -> p m t", t=4),
+                op=ALU.add,
+            )
+            o = u * UW + s * NCOL
+            nc.sync.dma_start(out=ov[:, o : o + NCOL], in_=oo[:])
+
+        steps = {
+            "setup": setup, "wload": wload, "bload": bload, "bprep": bprep, "wprep": wprep, "load": load,
+            "load2": load2, "tin": tin, "tinq": tinq, "tr": tr, "gate": gate, "ln": ln, "lnb": lnb, "rho": rho, "ars": ars, "sq": sq,
+            "hb": hb, "t2": t2, "back": back,
+        }
+        for step in PLAN:
+            steps[step[0]](*step[1:])

@@ -22,7 +22,7 @@ NCOL = PAIRS * P
 UW = 4 * NCOL
 EPS = 1e-6
 
-PLAN = (("setup",),("wload",0,),("load",0,),("wload",1,),("bload",),("load",1,),("wprep",0,),("tin",0,0,),("tin",0,1,),("tin",0,2,),("tin",0,3,),("tinq",0,),("load",2,),("wprep",1,),("bprep",),("wload",2,),("tin",1,0,),("tin",1,1,),("tin",1,2,),("tin",1,3,),("tinq",1,),("load",3,),("tr",0,0,),("tr",0,1,),("tr",0,2,),("tr",0,3,),("gate",0,),("tr",1,0,),("tr",1,1,),("tr",1,2,),("tr",1,3,),("tin",2,0,),("tin",2,1,),("tin",2,2,),("tin",2,3,),("tinq",2,),("load",4,),("ln",0,),("lnb",0,),("gate",1,),("wprep",2,),("ln",1,),("lnb",1,),("tin",3,0,),("tin",3,1,),("tin",3,2,),("tin",3,3,),("tinq",3,),("load",5,),("tin",4,0,),("tin",4,1,),("tin",4,2,),("tin",4,3,),("tinq",4,),("load",6,),("hb",0,0,"v",),("rho",0,0,),("t2",0,0,"g",1,),("hb",0,1,"v",),("rho",0,1,),("t2",0,1,"g",1,),("hb",0,2,"v",),("rho",0,2,),("t2",0,2,"g",1,),("hb",0,3,"v",),("rho",0,3,),("t2",0,3,"g",1,),("tr",2,0,),("tr",2,1,),("tr",2,2,),("tr",2,3,),("gate",2,),("hb",1,0,"v",),("rho",1,0,),("t2",1,0,"g",1,),("hb",1,1,"v",),("rho",1,1,),("t2",1,1,"g",1,),("hb",1,2,"v",),("rho",1,2,),("t2",1,2,"g",1,),("hb",1,3,"v",),("rho",1,3,),("t2",1,3,"g",1,),("load2",0,),("back",0,0,),("back",0,1,),("back",0,2,),("back",0,3,),("tr",3,0,),("tr",3,1,),("tr",3,2,),("tr",3,3,),("gate",3,),("load2",1,),("back",1,0,),("back",1,1,),("back",1,2,),("back",1,3,),("tr",4,0,),("tr",4,1,),("tr",4,2,),("tr",4,3,),("ln",2,),("lnb",2,),("gate",4,),("tin",5,0,),("tin",5,1,),("tin",5,2,),("tin",5,3,),("tinq",5,),("load",7,),("ln",3,),("lnb",3,),("tin",6,0,),("tin",6,1,),("tin",6,2,),("tin",6,3,),("tinq",6,),("ln",4,),("lnb",4,),("tin",7,0,),("tin",7,1,),("tin",7,2,),("tin",7,3,),("tinq",7,),("hb",2,0,"v",),("rho",2,0,),("t2",2,0,"g",1,),("hb",2,1,"v",),("rho",2,1,),("t2",2,1,"g",1,),("hb",2,2,"v",),("rho",2,2,),("t2",2,2,"g",1,),("hb",2,3,"v",),("rho",2,3,),("t2",2,3,"g",1,),("tr",5,0,),("tr",5,1,),("tr",5,2,),("tr",5,3,),("gate",5,),("hb",3,0,"v",),("rho",3,0,),("t2",3,0,"g",1,),("hb",3,1,"v",),("rho",3,1,),("t2",3,1,"g",1,),("hb",3,2,"v",),("rho",3,2,),("t2",3,2,"g",1,),("hb",3,3,"v",),("rho",3,3,),("t2",3,3,"g",1,),("load2",2,),("back",2,0,),("back",2,1,),("back",2,2,),("back",2,3,),("tr",6,0,),("tr",6,1,),("tr",6,2,),("tr",6,3,),("gate",6,),("hb",4,0,"v",),("rho",4,0,),("t2",4,0,"g",1,),("hb",4,1,"v",),("rho",4,1,),("t2",4,1,"g",1,),("hb",4,2,"v",),("rho",4,2,),("t2",4,2,"g",1,),("hb",4,3,"v",),("rho",4,3,),("t2",4,3,"g",1,),("load2",3,),("back",3,0,),("back",3,1,),("back",3,2,),("back",3,3,),("tr",7,0,),("tr",7,1,),("tr",7,2,),("tr",7,3,),("ln",5,),("lnb",5,),("gate",7,),("load2",4,),("back",4,0,),("back",4,1,),("back",4,2,),("back",4,3,),("ln",6,),("lnb",6,),("ln",7,),("lnb",7,),("hb",5,0,"v",),("rho",5,0,),("t2",5,0,"g",1,),("hb",5,1,"v",),("rho",5,1,),("t2",5,1,"g",1,),("hb",5,2,"v",),("rho",5,2,),("t2",5,2,"g",1,),("hb",5,3,"v",),("rho",5,3,),("t2",5,3,"g",1,),("hb",6,0,"v",),("rho",6,0,),("t2",6,0,"g",1,),("hb",6,1,"v",),("rho",6,1,),("t2",6,1,"g",1,),("hb",6,2,"v",),("rho",6,2,),("t2",6,2,"g",1,),("hb",6,3,"v",),("rho",6,3,),("t2",6,3,"g",1,),("load2",5,),("back",5,0,),("back",5,1,),("back",5,2,),("back",5,3,),("hb",7,0,"v",),("rho",7,0,),("t2",7,0,"g",1,),("hb",7,1,"v",),("rho",7,1,),("t2",7,1,"g",1,),("hb",7,2,"v",),("rho",7,2,),("t2",7,2,"g",1,),("hb",7,3,"v",),("rho",7,3,),("t2",7,3,"g",1,),("load2",6,),("back",6,0,),("back",6,1,),("back",6,2,),("back",6,3,),("load2",7,),("back",7,0,),("back",7,1,),("back",7,2,),("back",7,3,),)
+PLAN = (("setup",),("wload",0,),("load",0,),("wload",1,),("bload",),("load",1,),("wprep",0,),("tin",0,0,),("tin",0,1,),("tin",0,2,),("tin",0,3,),("tinq",0,),("load",2,),("wprep",1,),("bprep",),("wload",2,),("tin",1,0,),("tin",1,1,),("tin",1,2,),("tin",1,3,),("tinq",1,),("load",3,),("tr",0,0,),("tr",0,1,),("tr",0,2,),("tr",0,3,),("gate",0,),("tr",1,0,),("tr",1,1,),("tr",1,2,),("tr",1,3,),("tin",2,0,),("tin",2,1,),("tin",2,2,),("tin",2,3,),("tinq",2,),("load",4,),("ln",0,),("lnb",0,),("gate",1,),("wprep",2,),("ln",1,),("lnb",1,),("tin",3,0,),("tin",3,1,),("tin",3,2,),("tin",3,3,),("tinq",3,),("load",5,),("tin",4,0,),("tin",4,1,),("tin",4,2,),("tin",4,3,),("tinq",4,),("load",6,),("hb",0,0,"v",),("rho",0,0,),("t2",0,0,"v",1,),("hb",0,1,"v",),("rho",0,1,),("t2",0,1,"v",1,),("hb",0,2,"v",),("rho",0,2,),("t2",0,2,"v",1,),("hb",0,3,"v",),("rho",0,3,),("t2",0,3,"v",1,),("tr",2,0,),("tr",2,1,),("tr",2,2,),("tr",2,3,),("gate",2,),("hb",1,0,"v",),("rho",1,0,),("t2",1,0,"v",1,),("hb",1,1,"v",),("rho",1,1,),("t2",1,1,"v",1,),("hb",1,2,"v",),("rho",1,2,),("t2",1,2,"v",1,),("hb",1,3,"v",),("rho",1,3,),("t2",1,3,"v",1,),("load2",0,),("back",0,0,),("back",0,1,),("back",0,2,),("back",0,3,),("tr",3,0,),("tr",3,1,),("tr",3,2,),("tr",3,3,),("gate",3,),("load2",1,),("back",1,0,),("back",1,1,),("back",1,2,),("back",1,3,),("tr",4,0,),("tr",4,1,),("tr",4,2,),("tr",4,3,),("ln",2,),("lnb",2,),("gate",4,),("tin",5,0,),("tin",5,1,),("tin",5,2,),("tin",5,3,),("tinq",5,),("load",7,),("ln",3,),("lnb",3,),("tin",6,0,),("tin",6,1,),("tin",6,2,),("tin",6,3,),("tinq",6,),("ln",4,),("lnb",4,),("tin",7,0,),("tin",7,1,),("tin",7,2,),("tin",7,3,),("tinq",7,),("hb",2,0,"v",),("rho",2,0,),("t2",2,0,"v",1,),("hb",2,1,"v",),("rho",2,1,),("t2",2,1,"v",1,),("hb",2,2,"v",),("rho",2,2,),("t2",2,2,"v",1,),("hb",2,3,"v",),("rho",2,3,),("t2",2,3,"v",1,),("tr",5,0,),("tr",5,1,),("tr",5,2,),("tr",5,3,),("gate",5,),("hb",3,0,"v",),("rho",3,0,),("t2",3,0,"v",1,),("hb",3,1,"v",),("rho",3,1,),("t2",3,1,"v",1,),("hb",3,2,"v",),("rho",3,2,),("t2",3,2,"v",1,),("hb",3,3,"v",),("rho",3,3,),("t2",3,3,"v",1,),("load2",2,),("back",2,0,),("back",2,1,),("back",2,2,),("back",2,3,),("tr",6,0,),("tr",6,1,),("tr",6,2,),("tr",6,3,),("gate",6,),("hb",4,0,"v",),("rho",4,0,),("t2",4,0,"v",1,),("hb",4,1,"v",),("rho",4,1,),("t2",4,1,"v",1,),("hb",4,2,"v",),("rho",4,2,),("t2",4,2,"v",1,),("hb",4,3,"v",),("rho",4,3,),("t2",4,3,"v",1,),("load2",3,),("back",3,0,),("back",3,1,),("back",3,2,),("back",3,3,),("tr",7,0,),("tr",7,1,),("tr",7,2,),("tr",7,3,),("ln",5,),("lnb",5,),("gate",7,),("load2",4,),("back",4,0,),("back",4,1,),("back",4,2,),("back",4,3,),("ln",6,),("lnb",6,),("ln",7,),("lnb",7,),("hb",5,0,"v",),("rho",5,0,),("t2",5,0,"v",1,),("hb",5,1,"v",),("rho",5,1,),("t2",5,1,"v",1,),("hb",5,2,"v",),("rho",5,2,),("t2",5,2,"v",1,),("hb",5,3,"v",),("rho",5,3,),("t2",5,3,"v",1,),("hb",6,0,"v",),("rho",6,0,),("t2",6,0,"v",1,),("hb",6,1,"v",),("rho",6,1,),("t2",6,1,"v",1,),("hb",6,2,"v",),("rho",6,2,),("t2",6,2,"v",1,),("hb",6,3,"v",),("rho",6,3,),("t2",6,3,"v",1,),("load2",5,),("back",5,0,),("back",5,1,),("back",5,2,),("back",5,3,),("hb",7,0,"v",),("rho",7,0,),("t2",7,0,"v",1,),("hb",7,1,"v",),("rho",7,1,),("t2",7,1,"v",1,),("hb",7,2,"v",),("rho",7,2,),("t2",7,2,"v",1,),("hb",7,3,"v",),("rho",7,3,),("t2",7,3,"v",1,),("load2",6,),("back",6,0,),("back",6,1,),("back",6,2,),("back",6,3,),("load2",7,),("back",7,0,),("back",7,1,),("back",7,2,),("back",7,3,),)
 BUFS = {"th":2,"ht":3,"xn":2,"hn":2,"h2":2,"xg":2,"hg":8,"xc":8,"hc":5,"hh":2,"dg":2,"dc":6,"ee":5,"oo":4}
 
 
@@ -181,6 +181,10 @@ def tile_ltccell_t_kernel(tc, x, hidden, W_tau, b_tau, W_r, b_r, W_h, b_h, out):
 
         engines = {"v": nc.vector, "g": nc.gpsimd}
 
+        def qq(u, e, t=None):
+            sl = slice(0, UW) if t is None else slice(t * NCOL, (t + 1) * NCOL)
+            engines[e].tensor_tensor(out=ee[u][:, sl], in0=ee[u][:, sl], in1=ee[u][:, sl], op=ALU.mult)
+
         def hb(u, t, e1):
             if t == 0:
                 ht[u] = work.tile([P, UW], F32, name="ht", tag="ht", bufs=BUFS["ht"], align_bytes=64)
@@ -213,7 +217,7 @@ def tile_ltccell_t_kernel(tc, x, hidden, W_tau, b_tau, W_r, b_r, W_h, b_h, out):
         steps = {
             "setup": setup, "wload": wload, "bload": bload, "bprep": bprep, "wprep": wprep, "load": load,
             "load2": load2, "tin": tin, "tinq": tinq, "tr": tr, "gate": gate, "ln": ln, "lnb": lnb, "rho": rho, "ars": ars, "sq": sq,
-            "hb": hb, "t2": t2, "back": back,
+            "hb": hb, "t2": t2, "back": back, "qq": qq,
         }
         for step in PLAN:
             steps[step[0]](*step[1:])

@@ -22,7 +22,7 @@ NCOL = PAIRS * P
 UW = 4 * NCOL
 EPS = 1e-6
 
-PLAN = (("setup",),("wload",0,),("load",0,),("wload",1,),("bload",),("load",1,),("wprep",0,),("tin",0,0,),("tin",0,1,),("tin",0,2,),("tin",0,3,),("tinq",0,),("load",2,),("wprep",1,),("bprep",),("wload",2,),("tin",1,0,),("tin",1,1,),("tin",1,2,),("tin",1,3,),("tinq",1,),("load",3,),("tr",0,0,),("tr",0,1,),("tr",0,2,),("tr",0,3,),("gate",0,),("tr",1,0,),("tr",1,1,),("tr",1,2,),("tr",1,3,),("tin",2,0,),("tin",2,1,),("tin",2,2,),("tin",2,3,),("tinq",2,),("load",4,),("ln",0,),("lnb",0,),("gate",1,),("wprep",2,),("ln",1,),("lnb",1,),("tin",3,0,),("tin",3,1,),("tin",3,2,),("tin",3,3,),("tinq",3,),("load",5,),("tin",4,0,),("tin",4,1,),("tin",4,2,),("tin",4,3,),("tinq",4,),("load",6,),("hb",0,0,"v",),("rho",0,0,),("t2",0,0,"v",1,),("hb",0,1,"v",),("rho",0,1,),("t2",0,1,"v",1,),("hb",0,2,"v",),("rho",0,2,),("t2",0,2,"v",1,),("hb",0,3,"v",),("rho",0,3,),("t2",0,3,"v",1,),("tr",2,0,),("tr",2,1,),("tr",2,2,),("tr",2,3,),("gate",2,),("hb",1,0,"v",),("rho",1,0,),("t2",1,0,"v",1,),("hb",1,1,"v",),("rho",1,1,),("t2",1,1,"v",1,),("hb",1,2,"v",),("rho",1,2,),("t2",1,2,"v",1,),("hb",1,3,"v",),("rho",1,3,),("t2",1,3,"v",1,),("load2",0,),("back",0,0,),("back",0,1,),("back",0,2,),("back",0,3,),("tr",3,0,),("tr",3,1,),("tr",3,2,),("tr",3,3,),("gate",3,),("load2",1,),("back",1,0,),("back",1,1,),("back",1,2,),("back",1,3,),("tr",4,0,),("tr",4,1,),("tr",4,2,),("tr",4,3,),("ln",2,),("lnb",2,),("gate",4,),("tin",5,0,),("tin",5,1,),("tin",5,2,),("tin",5,3,),("tinq",5,),("load",7,),("ln",3,),("lnb",3,),("tin",6,0,),("tin",6,1,),("tin",6,2,),("tin",6,3,),("tinq",6,),("ln",4,),("lnb",4,),("tin",7,0,),("tin",7,1,),("tin",7,2,),("tin",7,3,),("tinq",7,),("hb",2,0,"v",),("rho",2,0,),("t2",2,0,"v",1,),("hb",2,1,"v",),("rho",2,1,),("t2",2,1,"v",1,),("hb",2,2,"v",),("rho",2,2,),("t2",2,2,"v",1,),("hb",2,3,"v",),("rho",2,3,),("t2",2,3,"v",1,),("tr",5,0,),("tr",5,1,),("tr",5,2,),("tr",5,3,),("gate",5,),("hb",3,0,"v",),("rho",3,0,),("t2",3,0,"v",1,),("hb",3,1,"v",),("rho",3,1,),("t2",3,1,"v",1,),("hb",3,2,"v",),("rho",3,2,),("t2",3,2,"v",1,),("hb",3,3,"v",),("rho",3,3,),("t2",3,3,"v",1,),("load2",2,),("back",2,0,),("back",2,1,),("back",2,2,),("back",2,3,),("tr",6,0,),("tr",6,1,),("tr",6,2,),("tr",6,3,),("gate",6,),("hb",4,0,"v",),("rho",4,0,),("t2",4,0,"v",1,),("hb",4,1,"v",),("rho",4,1,),("t2",4,1,"v",1,),("hb",4,2,"v",),("rho",4,2,),("t2",4,2,"v",1,),("hb",4,3,"v",),("rho",4,3,),("t2",4,3,"v",1,),("load2",3,),("back",3,0,),("back",3,1,),("back",3,2,),("back",3,3,),("tr",7,0,),("tr",7,1,),("tr",7,2,),("tr",7,3,),("ln",5,),("lnb",5,),("gate",7,),("load2",4,),("back",4,0,),("back",4,1,),("back",4,2,),("back",4,3,),("ln",6,),("lnb",6,),("ln",7,),("lnb",7,),("hb",5,0,"v",),("rho",5,0,),("t2",5,0,"v",1,),("hb",5,1,"v",),("rho",5,1,),("t2",5,1,"v",1,),("hb",5,2,"v",),("rho",5,2,),("t2",5,2,"v",1,),("hb",5,3,"v",),("rho",5,3,),("t2",5,3,"v",1,),("hb",6,0,"v",),("rho",6,0,),("t2",6,0,"v",1,),("hb",6,1,"v",),("rho",6,1,),("t2",6,1,"v",1,),("hb",6,2,"v",),("rho",6,2,),("t2",6,2,"v",1,),("hb",6,3,"v",),("rho",6,3,),("t2",6,3,"v",1,),("load2",5,),("back",5,0,),("back",5,1,),("back",5,2,),("back",5,3,),("hb",7,0,"v",),("rho",7,0,),("t2",7,0,"v",1,),("hb",7,1,"v",),("rho",7,1,),("t2",7,1,"v",1,),("hb",7,2,"v",),("rho",7,2,),("t2",7,2,"v",1,),("hb",7,3,"v",),("rho",7,3,),("t2",7,3,"v",1,),("load2",6,),("back",6,0,),("back",6,1,),("back",6,2,),("back",6,3,),("load2",7,),("back",7,0,),("back",7,1,),("back",7,2,),("back",7,3,),)
+PLAN = (("setup",),("wload",0,"v",),("load",0,),("wload",1,"v",),("bload",),("load",1,),("wload",2,"g",),("wprep",0,(0,),),("tin",0,0,),("tin",0,1,),("tin",0,2,),("tin",0,3,),("tinq",0,),("load",2,),("bprep",),("wprep",1,(0,),),("tin",1,0,),("tin",1,1,),("tin",1,2,),("tin",1,3,),("tinq",1,),("load",3,),("tr",0,0,),("tr",0,1,),("tr",0,2,),("tr",0,3,),("tin",2,0,),("tin",2,1,),("tin",2,2,),("tin",2,3,),("tinq",2,),("load",4,),("gate",0,),("tr",1,0,),("tr",1,1,),("tr",1,2,),("tr",1,3,),("tin",3,0,),("tin",3,1,),("tin",3,2,),("tin",3,3,),("tinq",3,),("load",5,),("gate",1,),("tr",2,0,),("tr",2,1,),("tr",2,2,),("tr",2,3,),("tin",4,0,),("tin",4,1,),("tin",4,2,),("tin",4,3,),("tinq",4,),("load",6,),("ln",0,),("lnb",0,),("ln",1,),("lnb",1,),("ln",2,),("lnb",2,),("gate",2,),("wprep",2,(1,),),("tin",5,0,),("tin",5,1,),("tin",5,2,),("tin",5,3,),("tinq",5,),("load",7,),("load2",0,),("load2",1,),("hb",0,0,"v",),("rho",0,0,),("t2",0,0,"v",1,),("hb",0,1,"v",),("rho",0,1,),("t2",0,1,"v",1,),("hb",0,2,"v",),("rho",0,2,),("t2",0,2,"v",1,),("hb",0,3,"v",),("rho",0,3,),("t2",0,3,"v",1,),("tr",3,0,),("tr",3,1,),("tr",3,2,),("tr",3,3,),("gate",3,),("hb",1,0,"v",),("rho",1,0,),("t2",1,0,"v",1,),("hb",1,1,"v",),("rho",1,1,),("t2",1,1,"v",1,),("hb",1,2,"v",),("rho",1,2,),("t2",1,2,"v",1,),("hb",1,3,"v",),("rho",1,3,),("t2",1,3,"v",1,),("back",0,0,),("back",0,1,),("back",0,2,),("back",0,3,),("load2",2,),("tr",4,0,),("tr",4,1,),("tr",4,2,),("tr",4,3,),("gate",4,),("hb",2,0,"v",),("rho",2,0,),("t2",2,0,"v",1,),("hb",2,1,"v",),("rho",2,1,),("t2",2,1,"v",1,),("hb",2,2,"v",),("rho",2,2,),("t2",2,2,"v",1,),("hb",2,3,"v",),("rho",2,3,),("t2",2,3,"v",1,),("back",1,0,),("back",1,1,),("back",1,2,),("back",1,3,),("load2",3,),("tr",5,0,),("tr",5,1,),("tr",5,2,),("tr",5,3,),("ln",3,),("lnb",3,),("ln",4,),("lnb",4,),("ln",5,),("lnb",5,),("gate",5,),("back",2,0,),("back",2,1,),("back",2,2,),("back",2,3,),("load2",4,),("tin",6,0,),("tin",6,1,),("tin",6,2,),("tin",6,3,),("tinq",6,),("tin",7,0,),("tin",7,1,),("tin",7,2,),("tin",7,3,),("tinq",7,),("hb",3,0,"v",),("rho",3,0,),("t2",3,0,"v",1,),("hb",3,1,"v",),("rho",3,1,),("t2",3,1,"v",1,),("hb",3,2,"v",),("rho",3,2,),("t2",3,2,"v",1,),("hb",3,3,"v",),("rho",3,3,),("t2",3,3,"v",1,),("tr",6,0,),("tr",6,1,),("tr",6,2,),("tr",6,3,),("gate",6,),("hb",4,0,"v",),("rho",4,0,),("t2",4,0,"v",1,),("hb",4,1,"v",),("rho",4,1,),("t2",4,1,"v",1,),("hb",4,2,"v",),("rho",4,2,),("t2",4,2,"v",1,),("hb",4,3,"v",),("rho",4,3,),("t2",4,3,"v",1,),("back",3,0,),("back",3,1,),("back",3,2,),("back",3,3,),("load2",5,),("tr",7,0,),("tr",7,1,),("tr",7,2,),("tr",7,3,),("gate",7,),("hb",5,0,"v",),("rho",5,0,),("t2",5,0,"v",1,),("hb",5,1,"v",),("rho",5,1,),("t2",5,1,"v",1,),("hb",5,2,"v",),("rho",5,2,),("t2",5,2,"v",1,),("hb",5,3,"v",),("rho",5,3,),("t2",5,3,"v",1,),("back",4,0,),("back",4,1,),("back",4,2,),("back",4,3,),("load2",6,),("ln",6,),("lnb",6,),("ln",7,),("lnb",7,),("back",5,0,),("back",5,1,),("back",5,2,),("back",5,3,),("load2",7,),("hb",6,0,"v",),("rho",6,0,),("t2",6,0,"v",1,),("hb",6,1,"v",),("rho",6,1,),("t2",6,1,"v",1,),("hb",6,2,"v",),("rho",6,2,),("t2",6,2,"v",1,),("hb",6,3,"v",),("rho",6,3,),("t2",6,3,"v",1,),("hb",7,0,"v",),("rho",7,0,),("t2",7,0,"v",1,),("hb",7,1,"v",),("rho",7,1,),("t2",7,1,"v",1,),("hb",7,2,"v",),("rho",7,2,),("t2",7,2,"v",1,),("hb",7,3,"v",),("rho",7,3,),("t2",7,3,"v",1,),("back",6,0,),("back",6,1,),("back",6,2,),("back",6,3,),("back",7,0,),("back",7,1,),("back",7,2,),("back",7,3,),)
 BUFS = {"th":2,"ht":3,"xn":2,"hn":2,"h2":2,"xg":2,"hg":8,"xc":8,"hc":5,"hh":2,"dg":2,"dc":6,"ee":5,"oo":4}
 
 
@@ -48,7 +48,9 @@ def tile_ltccell_t_kernel(tc, x, hidden, W_tau, b_tau, W_r, b_r, W_h, b_h, out):
         ws = const.tile([P, 3 * 1024], U8, name="ws", align_bytes=64)
 
         xn, hn, h2, hg, xc, xs, hc, hs = {}, {}, {}, {}, {}, {}, {}, {}
-        dc, ds, th, ee, ht, wn, xg = {}, {}, {}, {}, {}, {}, {}
+        dc, ds, th, ee, ht, wn, xg, wg = {}, {}, {}, {}, {}, {}, {}, {}
+
+        engines = {"v": nc.vector, "g": nc.gpsimd}
 
         def transpose_in(src_words, n_pairs, dst_words, evac, pieces=None):
             sv = src_words.rearrange("p (s m u) -> p s m u", s=n_pairs, m=P, u=2)
@@ -65,32 +67,50 @@ def tile_ltccell_t_kernel(tc, x, hidden, W_tau, b_tau, W_r, b_r, W_h, b_h, out):
             nc.vector.memset(cst[:, 0:1], 1.0)
             nc.vector.memset(cst[:, 1:2], EPS)
 
-        def wload(w):
-            wn[w] = work.tile([P, 4096], BF16, name="wn", tag="ee", bufs=BUFS["ee"])
-            z = wn[w][:].bitcast(F32).rearrange("p (a h m) -> p a h m", a=8, h=2, m=P)
-            nc.gpsimd.memset(z[0:64, :, 1, :], 0.0)
-            nc.gpsimd.memset(z[64:128, :, 0, :], 0.0)
-            src = weights[w].rearrange("(j r) k -> j (r k)", r=4).rearrange("j (a k) -> j a k", k=256)
-            dst = wn[w][:].rearrange("p (a h k) -> p a h k", a=8, h=2, k=256)
-            nc.scalar.dma_start(out=dst[0:64, :, 0, :], in_=src)
-            nc.scalar.dma_start(out=dst[64:128, :, 1, :], in_=src)
+        def wload(w, ez):
+            wn[w] = work.tile([P, 2, 768], BF16, name="wn", tag="ee", bufs=BUFS["ee"])
+            src = weights[w].rearrange("(c p) k -> p c k", p=P)
+            nc.sync.dma_start(out=wn[w][:, :, 0:512], in_=src)
+            nc.sync.dma_start(out=wn[w][:, :, 512:768], in_=src[:, :, 0:256])
+            wg[w] = work.tile([P, 2048], F32, name="wg", tag="ht", bufs=BUFS["ht"], align_bytes=64)
+            z = wg[w][:].rearrange("p (a m u) -> p a m u", a=8, m=P, u=2)
+            engines[ez].memset(z[0:64, :, 64:128, :], 0.0)
+            engines[ez].memset(z[64:128, :, 0:64, :], 0.0)
 
         def bload():
             for w in range(3):
                 src = biases[w].rearrange("(j t) -> j t", t=4)
-                nc.scalar.dma_start(out=braw[0:64, w, 0:4], in_=src)
-                nc.scalar.dma_start(out=braw[64:128, w, 0:4], in_=src)
+                nc.sync.dma_start(out=braw[0:64, w, 0:4], in_=src)
+                nc.sync.dma_start(out=braw[64:128, w, 0:4], in_=src)
 
         def bprep():
             bv = bias[:].rearrange("p (w t) -> p w t", w=3)
             nc.vector.tensor_copy(out=bv, in_=braw[:, :, 0:4])
             nc.vector.tensor_scalar(out=bias[:, 4:8], in0=bias[:, 4:8], scalar1=0.5, scalar2=None, op0=ALU.mult)
 
-        def wprep(w):
-            wg = work.tile([P, 2048], F32, name="wg", tag="ht", bufs=BUFS["ht"], align_bytes=64)
-            transpose_in(wn[w][:].bitcast(F32), 8, wg[:], nc.scalar.copy)
+        def wprep(w, evacs):
+            words = wn[w][:].rearrange("p c k -> p (c k)").bitcast(F32).rearrange("p (c k) -> p c k", c=2)
+            dv = wg[w][:].rearrange("p (t a m u) -> p t a m u", t=4, a=2, m=P, u=2)
+            n = 0
+            for order in range(2):
+                bank = psum.tile([P, 2, 2, P], F32, name="wt", tag="bank")
+                for c in range(2):
+                    sv = words[:, c, 128 * order : 128 * order + 256].rearrange("p (m u) -> p m u", u=2)
+                    for u in range(2):
+                        nc.tensor.transpose(bank[:, u, c, :], sv[:, :, u], ident[:])
+                for half in range(2):
+                    rows = slice(64 * half, 64 * half + 64)
+                    part = (order + half) % 2
+                    for c in range(2):
+                        m0 = 64 * half + 32 * c
+                        evac = (nc.scalar.copy, nc.vector.tensor_copy)[evacs[n % len(evacs)]]
+                        n += 1
+                        evac(
+                            out=dv[rows, :, part, m0 : m0 + 32, :],
+                            in_=bank[rows, :, c, :].rearrange("p u (q t) -> p t q u", t=4),
+                        )
             cols = slice(w * 1024, (w + 1) * 1024)
-            nc.vector.quantize_mx(out=wc[:, cols].bitcast(FP8X4), scales=ws[:, cols], in_=wg[:].bitcast(BF16))
+            nc.vector.quantize_mx(out=wc[:, cols].bitcast(FP8X4), scales=ws[:, cols], in_=wg[w][:].bitcast(BF16))
 
         def load(u):
             cols = slice(u * UW, (u + 1) * UW)
@@ -135,15 +155,17 @@ def tile_ltccell_t_kernel(tc, x, hidden, W_tau, b_tau, W_r, b_r, W_h, b_h, out):
                 )
             return bank
 
-        def tr(u, t):
-            if t == 0:
+        def tr(u, t, which=(0, 1)):
+            if u not in ee:
                 ee[u] = work.tile([P, UW], F32, name="ee", tag="ee", bufs=BUFS["ee"])
                 th[u] = work.tile([P, UW], F32, name="th", tag="th", bufs=BUFS["th"], align_bytes=64)
             sl = slice(t * NCOL, (t + 1) * NCOL)
-            bank = mx_pair(0, t, xc[u], xs[u], hc[u], hs[u])
-            nc.scalar.activation(out=ee[u][:, sl], in_=bank[:], func=ACT.Exp, bias=bias[:, t : t + 1], scale=1.0)
-            bank = mx_pair(1, t, xc[u], xs[u], hc[u], hs[u])
-            nc.scalar.activation(out=th[u][:, sl], in_=bank[:], func=ACT.Tanh, bias=bias[:, 4 + t : 5 + t], scale=0.5)
+            if 0 in which:
+                bank = mx_pair(0, t, xc[u], xs[u], hc[u], hs[u])
+                nc.scalar.activation(out=ee[u][:, sl], in_=bank[:], func=ACT.Exp, bias=bias[:, t : t + 1], scale=1.0)
+            if 1 in which:
+                bank = mx_pair(1, t, xc[u], xs[u], hc[u], hs[u])
+                nc.scalar.activation(out=th[u][:, sl], in_=bank[:], func=ACT.Tanh, bias=bias[:, 4 + t : 5 + t], scale=0.5)
 
         def gate(u):
             hh = work.tile([P, UW], BF16, name="hh", tag="hh", bufs=BUFS["hh"])
@@ -178,8 +200,6 @@ def tile_ltccell_t_kernel(tc, x, hidden, W_tau, b_tau, W_r, b_r, W_h, b_h, out):
         def sq(u, t=None):
             sl = slice(0, UW) if t is None else slice(t * NCOL, (t + 1) * NCOL)
             nc.scalar.activation(out=ee[u][:, sl], in_=ee[u][:, sl], func=ACT.Square)
-
-        engines = {"v": nc.vector, "g": nc.gpsimd}
 
         def qq(u, e, t=None):
             sl = slice(0, UW) if t is None else slice(t * NCOL, (t + 1) * NCOL)

@@ -23,7 +23,7 @@ UW = 4 * NCOL
 EPS = 1e-6
 
 PLAN = (("setup",),("wload",0,"v",),("load",0,),("wload",1,"v",),("bload",),("load",1,),("wload",2,"g",),("wprep",0,(0,),),("tin",0,0,),("tin",0,1,),("tin",0,2,),("tin",0,3,),("tinq",0,),("load",2,),("bprep",),("wprep",1,(0,),),("tin",1,0,),("tin",1,1,),("tin",1,2,),("tin",1,3,),("tinq",1,),("load",3,),("tr",0,0,),("tr",0,1,),("tr",0,2,),("tr",0,3,),("tin",2,0,),("tin",2,1,),("tin",2,2,),("tin",2,3,),("tinq",2,),("load",4,),("gate",0,),("tr",1,0,),("tr",1,1,),("tr",1,2,),("tr",1,3,),("tin",3,0,),("tin",3,1,),("tin",3,2,),("tin",3,3,),("tinq",3,),("load",5,),("gate",1,),("tr",2,0,),("tr",2,1,),("tr",2,2,),("tr",2,3,),("tin",4,0,),("tin",4,1,),("tin",4,2,),("tin",4,3,),("tinq",4,),("load",6,),("ln",0,),("lnb",0,),("ln",1,),("lnb",1,),("ln",2,),("lnb",2,),("gate",2,),("wprep",2,(1,),),("tin",5,0,),("tin",5,1,),("tin",5,2,),("tin",5,3,),("tinq",5,),("load",7,),("load2",0,),("load2",1,),("hb",0,0,"v",),("rho",0,0,),("t2",0,0,"v",1,),("hb",0,1,"v",),("rho",0,1,),("t2",0,1,"v",1,),("hb",0,2,"v",),("rho",0,2,),("t2",0,2,"v",1,),("hb",0,3,"v",),("rho",0,3,),("t2",0,3,"v",1,),("tr",3,0,),("tr",3,1,),("tr",3,2,),("tr",3,3,),("gate",3,),("hb",1,0,"v",),("rho",1,0,),("t2",1,0,"v",1,),("hb",1,1,"v",),("rho",1,1,),("t2",1,1,"v",1,),("hb",1,2,"v",),("rho",1,2,),("t2",1,2,"v",1,),("hb",1,3,"v",),("rho",1,3,),("t2",1,3,"v",1,),("back",0,0,),("back",0,1,),("back",0,2,),("back",0,3,),("load2",2,),("tr",4,0,),("tr",4,1,),("tr",4,2,),("tr",4,3,),("gate",4,),("hb",2,0,"v",),("rho",2,0,),("t2",2,0,"v",1,),("hb",2,1,"v",),("rho",2,1,),("t2",2,1,"v",1,),("hb",2,2,"v",),("rho",2,2,),("t2",2,2,"v",1,),("hb",2,3,"v",),("rho",2,3,),("t2",2,3,"v",1,),("back",1,0,),("back",1,1,),("back",1,2,),("back",1,3,),("load2",3,),("tr",5,0,),("tr",5,1,),("tr",5,2,),("tr",5,3,),("ln",3,),("lnb",3,),("ln",4,),("lnb",4,),("ln",5,),("lnb",5,),("gate",5,),("back",2,0,),("back",2,1,),("back",2,2,),("back",2,3,),("load2",4,),("tin",6,0,),("tin",6,1,),("tin",6,2,),("tin",6,3,),("tinq",6,),("tin",7,0,),("tin",7,1,),("tin",7,2,),("tin",7,3,),("tinq",7,),("hb",3,0,"v",),("rho",3,0,),("t2",3,0,"v",1,),("hb",3,1,"v",),("rho",3,1,),("t2",3,1,"v",1,),("hb",3,2,"v",),("rho",3,2,),("t2",3,2,"v",1,),("hb",3,3,"v",),("rho",3,3,),("t2",3,3,"v",1,),("tr",6,0,),("tr",6,1,),("tr",6,2,),("tr",6,3,),("gate",6,),("hb",4,0,"v",),("rho",4,0,),("t2",4,0,"v",1,),("hb",4,1,"v",),("rho",4,1,),("t2",4,1,"v",1,),("hb",4,2,"v",),("rho",4,2,),("t2",4,2,"v",1,),("hb",4,3,"v",),("rho",4,3,),("t2",4,3,"v",1,),("back",3,0,),("back",3,1,),("back",3,2,),("back",3,3,),("load2",5,),("tr",7,0,),("tr",7,1,),("tr",7,2,),("tr",7,3,),("gate",7,),("hb",5,0,"v",),("rho",5,0,),("t2",5,0,"v",1,),("hb",5,1,"v",),("rho",5,1,),("t2",5,1,"v",1,),("hb",5,2,"v",),("rho",5,2,),("t2",5,2,"v",1,),("hb",5,3,"v",),("rho",5,3,),("t2",5,3,"v",1,),("back",4,0,),("back",4,1,),("back",4,2,),("back",4,3,),("load2",6,),("ln",6,),("lnb",6,),("ln",7,),("lnb",7,),("back",5,0,),("back",5,1,),("back",5,2,),("back",5,3,),("load2",7,),("hb",6,0,"v",),("rho",6,0,),("t2",6,0,"v",1,),("hb",6,1,"v",),("rho",6,1,),("t2",6,1,"v",1,),("hb",6,2,"v",),("rho",6,2,),("t2",6,2,"v",1,),("hb",6,3,"v",),("rho",6,3,),("t2",6,3,"v",1,),("hb",7,0,"v",),("rho",7,0,),("t2",7,0,"v",1,),("hb",7,1,"v",),("rho",7,1,),("t2",7,1,"v",1,),("hb",7,2,"v",),("rho",7,2,),("t2",7,2,"v",1,),("hb",7,3,"v",),("rho",7,3,),("t2",7,3,"v",1,),("back",6,0,),("back",6,1,),("back",6,2,),("back",6,3,),("back",7,0,),("back",7,1,),("back",7,2,),("back",7,3,),)
-BUFS = {"th":2,"ht":3,"xn":2,"hn":2,"h2":2,"xg":2,"hg":8,"xc":8,"hc":5,"hh":2,"dg":2,"dc":6,"ee":5,"oo":4}
+BUFS = {"th":2,"ht":3,"xn":2,"hn":2,"h2":2,"xg":2,"hg":8,"xc":8,"hc":5,"hh":2,"dg":2,"dc":6,"ee":5,"oo":4,"mx":4}
 
 
 def tile_ltccell_t_kernel(tc, x, hidden, W_tau, b_tau, W_r, b_r, W_h, b_h, out):
@@ -37,7 +37,8 @@ def tile_ltccell_t_kernel(tc, x, hidden, W_tau, b_tau, W_r, b_r, W_h, b_h, out):
     with ExitStack() as ctx:
         const = ctx.enter_context(tc.tile_pool(name="const", bufs=1))
         work = ctx.enter_context(tc.tile_pool(name="work", bufs=2))
-        psum = ctx.enter_context(tc.psum_pool(name="psum", bufs=8))
+        psum = ctx.enter_context(tc.psum_pool(name="psum", bufs=BUFS["mx"]))
+        psum_t = ctx.enter_context(tc.psum_pool(name="psum_t", bufs=8 - BUFS["mx"]))
         ctx.enter_context(tc.manual_schedule())
 
         ident = const.tile([P, P], F32, name="ident")
@@ -56,7 +57,7 @@ def tile_ltccell_t_kernel(tc, x, hidden, W_tau, b_tau, W_r, b_r, W_h, b_h, out):
             sv = src_words.rearrange("p (s m u) -> p s m u", s=n_pairs, m=P, u=2)
             dv = dst_words.rearrange("p (s m u) -> p s m u", s=n_pairs, m=P, u=2)
             for sb in pieces or range(n_pairs // 2):
-                bank = psum.tile([P, 2, 2, P], F32, name="tin", tag="bank")
+                bank = psum_t.tile([P, 2, 2, P], F32, name="tin", tag="tbank")
                 for s2 in range(2):
                     for u in range(2):
                         nc.tensor.transpose(bank[:, s2, u, :], sv[:, 2 * sb + s2, :, u], ident[:])
@@ -93,7 +94,7 @@ def tile_ltccell_t_kernel(tc, x, hidden, W_tau, b_tau, W_r, b_r, W_h, b_h, out):
             dv = wg[w][:].rearrange("p (t a m u) -> p t a m u", t=4, a=2, m=P, u=2)
             n = 0
             for order in range(2):
-                bank = psum.tile([P, 2, 2, P], F32, name="wt", tag="bank")
+                bank = psum_t.tile([P, 2, 2, P], F32, name="wt", tag="tbank")
                 for c in range(2):
                     sv = words[:, c, 128 * order : 128 * order + 256].rearrange("p (m u) -> p m u", u=2)
                     for u in range(2):
@@ -123,14 +124,15 @@ def tile_ltccell_t_kernel(tc, x, hidden, W_tau, b_tau, W_r, b_r, W_h, b_h, out):
             h2[u] = work.tile([P, UW], BF16, name="h2", tag="h2", bufs=BUFS["h2"])
             nc.sync.dma_start(out=h2[u][:], in_=hv[:, u * UW : (u + 1) * UW])
 
-        def tin(u, i):
+        def tin(u, i, ev=1):
+            evac = (nc.scalar.copy, nc.vector.tensor_copy)[ev]
             if i == 0:
                 xg[u] = work.tile([P, UW // 2], F32, name="xg", tag="xg", bufs=BUFS["xg"], align_bytes=64)
                 hg[u] = work.tile([P, UW // 2], F32, name="hg", tag="hg", bufs=BUFS["hg"], align_bytes=64)
             if i < 2:
-                transpose_in(xn[u][:].bitcast(F32), PAIRS, xg[u][:], nc.vector.tensor_copy, (i,))
+                transpose_in(xn[u][:].bitcast(F32), PAIRS, xg[u][:], evac, (i,))
             else:
-                transpose_in(hn[u][:].bitcast(F32), PAIRS, hg[u][:], nc.vector.tensor_copy, (i - 2,))
+                transpose_in(hn[u][:].bitcast(F32), PAIRS, hg[u][:], evac, (i - 2,))
 
         def tinq(u):
             xc[u] = work.tile([P, NCOL], U32, name="xc", tag="xc", bufs=BUFS["xc"], align_bytes=64)
@@ -220,7 +222,7 @@ def tile_ltccell_t_kernel(tc, x, hidden, W_tau, b_tau, W_r, b_r, W_h, b_h, out):
                 engines[e2].tensor_tensor(out=ht[u][:, sl], in0=ht[u][:, sl], in1=ee[u][:, sl], op=ALU.mult)
 
         def back(u, s):
-            tb = psum.tile([P, 4, P], F32, name="tb", tag="bank")
+            tb = psum_t.tile([P, 4, P], F32, name="tb", tag="tbank")
             for t in range(4):
                 o = t * NCOL + s * P
                 nc.tensor.transpose(tb[:, t, :], ht[u][:, o : o + P], ident[:])

@@ -22,8 +22,8 @@ NCOL = PAIRS * P
 UW = 4 * NCOL
 EPS = 1e-6
 
-PLAN = (("setup",),("wload",0,"v",),("load",0,),("wload",1,"v",),("bload",),("load",1,),("wload",2,"g",),("wprep",0,(0,),),("tin",0,0,),("tin",0,1,),("tin",0,2,),("tin",0,3,),("tinq",0,),("load",2,),("bprep",),("wprep",1,(0,),),("tin",1,0,),("tin",1,1,),("tin",1,2,),("tin",1,3,),("tinq",1,),("load",3,),("tr",0,0,),("tr",0,1,),("tr",0,2,),("tr",0,3,),("tin",2,0,),("tin",2,1,),("tin",2,2,),("tin",2,3,),("tinq",2,),("load",4,),("gate",0,),("tr",1,0,),("tr",1,1,),("tr",1,2,),("tr",1,3,),("tin",3,0,),("tin",3,1,),("tin",3,2,),("tin",3,3,),("tinq",3,),("load",5,),("gate",1,),("tr",2,0,),("tr",2,1,),("tr",2,2,),("tr",2,3,),("tin",4,0,),("tin",4,1,),("tin",4,2,),("tin",4,3,),("tinq",4,),("load",6,),("ln",0,),("lnb",0,),("ln",1,),("lnb",1,),("ln",2,),("lnb",2,),("gate",2,),("wprep",2,(1,),),("tin",5,0,),("tin",5,1,),("tin",5,2,),("tin",5,3,),("tinq",5,),("load",7,),("load2",0,),("load2",1,),("hb",0,0,"v",),("rho",0,0,),("t2",0,0,"v",1,),("hb",0,1,"v",),("rho",0,1,),("t2",0,1,"v",1,),("hb",0,2,"v",),("rho",0,2,),("t2",0,2,"v",1,),("hb",0,3,"v",),("rho",0,3,),("t2",0,3,"v",1,),("tr",3,0,),("tr",3,1,),("tr",3,2,),("tr",3,3,),("gate",3,),("hb",1,0,"v",),("rho",1,0,),("t2",1,0,"v",1,),("hb",1,1,"v",),("rho",1,1,),("t2",1,1,"v",1,),("hb",1,2,"v",),("rho",1,2,),("t2",1,2,"v",1,),("hb",1,3,"v",),("rho",1,3,),("t2",1,3,"v",1,),("back",0,0,),("back",0,1,),("back",0,2,),("back",0,3,),("load2",2,),("tr",4,0,),("tr",4,1,),("tr",4,2,),("tr",4,3,),("gate",4,),("hb",2,0,"v",),("rho",2,0,),("t2",2,0,"v",1,),("hb",2,1,"v",),("rho",2,1,),("t2",2,1,"v",1,),("hb",2,2,"v",),("rho",2,2,),("t2",2,2,"v",1,),("hb",2,3,"v",),("rho",2,3,),("t2",2,3,"v",1,),("back",1,0,),("back",1,1,),("back",1,2,),("back",1,3,),("load2",3,),("tr",5,0,),("tr",5,1,),("tr",5,2,),("tr",5,3,),("ln",3,),("lnb",3,),("ln",4,),("lnb",4,),("ln",5,),("lnb",5,),("gate",5,),("back",2,0,),("back",2,1,),("back",2,2,),("back",2,3,),("load2",4,),("tin",6,0,),("tin",6,1,),("tin",6,2,),("tin",6,3,),("tinq",6,),("tin",7,0,),("tin",7,1,),("tin",7,2,),("tin",7,3,),("tinq",7,),("hb",3,0,"v",),("rho",3,0,),("t2",3,0,"v",1,),("hb",3,1,"v",),("rho",3,1,),("t2",3,1,"v",1,),("hb",3,2,"v",),("rho",3,2,),("t2",3,2,"v",1,),("hb",3,3,"v",),("rho",3,3,),("t2",3,3,"v",1,),("tr",6,0,),("tr",6,1,),("tr",6,2,),("tr",6,3,),("gate",6,),("hb",4,0,"v",),("rho",4,0,),("t2",4,0,"v",1,),("hb",4,1,"v",),("rho",4,1,),("t2",4,1,"v",1,),("hb",4,2,"v",),("rho",4,2,),("t2",4,2,"v",1,),("hb",4,3,"v",),("rho",4,3,),("t2",4,3,"v",1,),("back",3,0,),("back",3,1,),("back",3,2,),("back",3,3,),("load2",5,),("tr",7,0,),("tr",7,1,),("tr",7,2,),("tr",7,3,),("gate",7,),("hb",5,0,"v",),("rho",5,0,),("t2",5,0,"v",1,),("hb",5,1,"v",),("rho",5,1,),("t2",5,1,"v",1,),("hb",5,2,"v",),("rho",5,2,),("t2",5,2,"v",1,),("hb",5,3,"v",),("rho",5,3,),("t2",5,3,"v",1,),("back",4,0,),("back",4,1,),("back",4,2,),("back",4,3,),("load2",6,),("ln",6,),("lnb",6,),("ln",7,),("lnb",7,),("back",5,0,),("back",5,1,),("back",5,2,),("back",5,3,),("load2",7,),("hb",6,0,"v",),("rho",6,0,),("t2",6,0,"v",1,),("hb",6,1,"v",),("rho",6,1,),("t2",6,1,"v",1,),("hb",6,2,"v",),("rho",6,2,),("t2",6,2,"v",1,),("hb",6,3,"v",),("rho",6,3,),("t2",6,3,"v",1,),("hb",7,0,"v",),("rho",7,0,),("t2",7,0,"v",1,),("hb",7,1,"v",),("rho",7,1,),("t2",7,1,"v",1,),("hb",7,2,"v",),("rho",7,2,),("t2",7,2,"v",1,),("hb",7,3,"v",),("rho",7,3,),("t2",7,3,"v",1,),("back",6,0,),("back",6,1,),("back",6,2,),("back",6,3,),("back",7,0,),("back",7,1,),("back",7,2,),("back",7,3,),)
-BUFS = {"th":2,"ht":3,"xn":2,"hn":2,"h2":2,"xg":2,"hg":8,"xc":8,"hc":5,"hh":2,"dg":2,"dc":6,"ee":5,"oo":4,"mx":4}
+PLAN = (("setup",),("wload",0,"v",),("load",0,),("wload",1,"v",),("bload",),("load",1,),("wload",2,"g",),("wprep",0,(0,),),("tin",0,0,),("tin",0,1,),("tin",0,2,),("tin",0,3,),("tinq",0,),("load",2,),("bprep",),("wprep",1,(0,),),("tin",1,0,),("tin",1,1,),("tin",1,2,),("tin",1,3,),("tinq",1,),("load",3,),("tr",0,0,),("tr",0,1,),("tr",0,2,),("tr",0,3,),("tin",2,0,),("tin",2,1,),("tin",2,2,),("tin",2,3,),("tinq",2,),("load",4,),("gh",0,),("gm",0,),("gq",0,),("tr",1,0,),("tr",1,1,),("tr",1,2,),("tr",1,3,),("tin",3,0,),("tin",3,1,),("tin",3,2,),("tin",3,3,),("tinq",3,),("load",5,),("gh",1,),("gm",1,),("gq",1,),("tr",2,0,),("tr",2,1,),("tr",2,2,),("tr",2,3,),("tin",4,0,),("tin",4,1,),("tin",4,2,),("tin",4,3,),("tinq",4,),("load",6,),("ln",0,),("ln",1,),("ln",2,),("gh",2,),("wprep",2,(1,),),("gm",2,),("gq",2,),("tin",5,0,),("tin",5,1,),("tin",5,2,),("tin",5,3,),("tinq",5,),("load",7,),("ars",0,),("qq",0,"g",0,),("qq",0,"g",1,),("qq",0,"g",2,),("qq",0,"g",3,),("ars",1,),("qq",1,"g",0,),("qq",1,"g",1,),("qq",1,"g",2,),("qq",1,"g",3,),("ars",2,),("qq",2,"g",0,),("qq",2,"g",1,),("qq",2,"g",2,),("qq",2,"g",3,),("load2",0,),("load2",1,),("hb",0,0,),("hb",0,1,),("hb",0,2,),("hb",0,3,),("t1",0,0,),("t1",0,1,),("t2",0,0,"v",1,),("t1",0,2,),("t2",0,1,"v",1,),("t1",0,3,),("t2",0,2,"v",1,),("t2",0,3,"v",1,),("tr",3,0,),("tr",3,1,),("tr",3,2,),("tr",3,3,),("hb",1,0,),("hb",1,1,),("hb",1,2,),("hb",1,3,),("gh",3,),("t1",1,0,),("gm",3,),("t1",1,1,),("t2",1,0,"v",1,),("gq",3,),("t1",1,2,),("t2",1,1,"v",1,),("t1",1,3,),("t2",1,2,"v",1,),("t2",1,3,"v",1,),("tr",4,0,),("tr",4,1,),("tr",4,2,),("tr",4,3,),("hb",2,0,),("hb",2,1,),("hb",2,2,),("hb",2,3,),("gh",4,),("t1",2,0,),("gm",4,),("t1",2,1,),("t2",2,0,"v",1,),("gq",4,),("t1",2,2,),("t2",2,1,"v",1,),("t1",2,3,),("t2",2,2,"v",1,),("t2",2,3,"v",1,),("tr",5,0,),("tr",5,1,),("tr",5,2,),("tr",5,3,),("ln",3,),("ln",4,),("ln",5,),("gh",5,),("back",0,0,),("back",0,1,),("back",0,2,),("back",0,3,),("load2",2,),("gm",5,),("tin",6,0,),("tin",6,1,),("tin",6,2,),("tin",6,3,),("tinq",6,),("gq",5,),("back",1,0,),("back",1,1,),("back",1,2,),("back",1,3,),("load2",3,),("tin",7,0,),("tin",7,1,),("tin",7,2,),("tin",7,3,),("tinq",7,),("back",2,0,),("back",2,1,),("back",2,2,),("back",2,3,),("load2",4,),("ars",3,),("qq",3,"g",0,),("qq",3,"g",1,),("qq",3,"g",2,),("qq",3,"g",3,),("ars",4,),("qq",4,"g",0,),("qq",4,"g",1,),("qq",4,"g",2,),("qq",4,"g",3,),("ars",5,),("qq",5,"g",0,),("qq",5,"g",1,),("qq",5,"g",2,),("qq",5,"g",3,),("hb",3,0,),("hb",3,1,),("hb",3,2,),("hb",3,3,),("t1",3,0,),("t1",3,1,),("t2",3,0,"v",1,),("t1",3,2,),("t2",3,1,"v",1,),("t1",3,3,),("t2",3,2,"v",1,),("t2",3,3,"v",1,),("tr",6,0,),("tr",6,1,),("tr",6,2,),("tr",6,3,),("hb",4,0,),("hb",4,1,),("hb",4,2,),("hb",4,3,),("gh",6,),("t1",4,0,),("gm",6,),("t1",4,1,),("t2",4,0,"v",1,),("gq",6,),("t1",4,2,),("t2",4,1,"v",1,),("t1",4,3,),("t2",4,2,"v",1,),("t2",4,3,"v",1,),("tr",7,0,),("tr",7,1,),("tr",7,2,),("tr",7,3,),("hb",5,0,),("hb",5,1,),("hb",5,2,),("hb",5,3,),("gh",7,),("t1",5,0,),("gm",7,),("t1",5,1,),("t2",5,0,"v",1,),("gq",7,),("t1",5,2,),("t2",5,1,"v",1,),("t1",5,3,),("t2",5,2,"v",1,),("t2",5,3,"v",1,),("ln",6,),("ln",7,),("back",3,0,),("back",3,1,),("back",3,2,),("back",3,3,),("load2",5,),("back",4,0,),("back",4,1,),("back",4,2,),("back",4,3,),("load2",6,),("back",5,0,),("back",5,1,),("back",5,2,),("back",5,3,),("load2",7,),("ars",6,),("qq",6,"g",0,),("qq",6,"g",1,),("qq",6,"g",2,),("qq",6,"g",3,),("ars",7,),("qq",7,"g",0,),("qq",7,"g",1,),("qq",7,"g",2,),("qq",7,"g",3,),("hb",6,0,),("hb",6,1,),("hb",6,2,),("hb",6,3,),("t1",6,0,),("t1",6,1,),("t2",6,0,"v",1,),("t1",6,2,),("t2",6,1,"v",1,),("t1",6,3,),("t2",6,2,"v",1,),("t2",6,3,"v",1,),("hb",7,0,),("hb",7,1,),("hb",7,2,),("hb",7,3,),("t1",7,0,),("t1",7,1,),("t2",7,0,"v",1,),("t1",7,2,),("t2",7,1,"v",1,),("t1",7,3,),("t2",7,2,"v",1,),("t2",7,3,"v",1,),("back",6,0,),("back",6,1,),("back",6,2,),("back",6,3,),("back",7,0,),("back",7,1,),("back",7,2,),("back",7,3,),)
+BUFS = {"th":2,"ht":4,"xn":2,"hn":2,"h2":2,"xg":2,"hg":6,"xc":6,"hc":5,"hh":2,"dg":2,"dc":6,"ee":5,"oo":4}
 
 
 def tile_ltccell_t_kernel(tc, x, hidden, W_tau, b_tau, W_r, b_r, W_h, b_h, out):
@@ -37,11 +37,11 @@ def tile_ltccell_t_kernel(tc, x, hidden, W_tau, b_tau, W_r, b_r, W_h, b_h, out):
     with ExitStack() as ctx:
         const = ctx.enter_context(tc.tile_pool(name="const", bufs=1))
         work = ctx.enter_context(tc.tile_pool(name="work", bufs=2))
-        psum = ctx.enter_context(tc.psum_pool(name="psum", bufs=BUFS["mx"]))
-        psum_t = ctx.enter_context(tc.psum_pool(name="psum_t", bufs=8 - BUFS["mx"]))
+        psum = ctx.enter_context(tc.psum_pool(name="psum", bufs=8))
         ctx.enter_context(tc.manual_schedule())
 
         ident = const.tile([P, P], F32, name="ident")
+        identb = const.tile([P, P], BF16, name="identb")
         cst = const.tile([P, 2], F32, name="cst")
         braw = const.tile([P, 3, 16], BF16, name="braw")
         bias = const.tile([P, 12], F32, name="bias")
@@ -49,7 +49,7 @@ def tile_ltccell_t_kernel(tc, x, hidden, W_tau, b_tau, W_r, b_r, W_h, b_h, out):
         ws = const.tile([P, 3 * 1024], U8, name="ws", align_bytes=64)
 
         xn, hn, h2, hg, xc, xs, hc, hs = {}, {}, {}, {}, {}, {}, {}, {}
-        dc, ds, th, ee, ht, wn, xg, wg = {}, {}, {}, {}, {}, {}, {}, {}
+        dc, ds, th, ee, ht, wn, xg, wg, hh, dg = {}, {}, {}, {}, {}, {}, {}, {}, {}, {}
 
         engines = {"v": nc.vector, "g": nc.gpsimd}
 
@@ -57,7 +57,7 @@ def tile_ltccell_t_kernel(tc, x, hidden, W_tau, b_tau, W_r, b_r, W_h, b_h, out):
             sv = src_words.rearrange("p (s m u) -> p s m u", s=n_pairs, m=P, u=2)
             dv = dst_words.rearrange("p (s m u) -> p s m u", s=n_pairs, m=P, u=2)
             for sb in pieces or range(n_pairs // 2):
-                bank = psum_t.tile([P, 2, 2, P], F32, name="tin", tag="tbank")
+                bank = psum.tile([P, 2, 2, P], F32, name="tin", tag="bank")
                 for s2 in range(2):
                     for u in range(2):
                         nc.tensor.transpose(bank[:, s2, u, :], sv[:, 2 * sb + s2, :, u], ident[:])
@@ -65,6 +65,7 @@ def tile_ltccell_t_kernel(tc, x, hidden, W_tau, b_tau, W_r, b_r, W_h, b_h, out):
 
         def setup():
             make_identity(nc, ident[:])
+            make_identity(nc, identb[:])
             nc.vector.memset(cst[:, 0:1], 1.0)
             nc.vector.memset(cst[:, 1:2], EPS)
 
@@ -94,7 +95,7 @@ def tile_ltccell_t_kernel(tc, x, hidden, W_tau, b_tau, W_r, b_r, W_h, b_h, out):
             dv = wg[w][:].rearrange("p (t a m u) -> p t a m u", t=4, a=2, m=P, u=2)
             n = 0
             for order in range(2):
-                bank = psum_t.tile([P, 2, 2, P], F32, name="wt", tag="tbank")
+                bank = psum.tile([P, 2, 2, P], F32, name="wt", tag="bank")
                 for c in range(2):
                     sv = words[:, c, 128 * order : 128 * order + 256].rearrange("p (m u) -> p m u", u=2)
                     for u in range(2):
@@ -124,15 +125,14 @@ def tile_ltccell_t_kernel(tc, x, hidden, W_tau, b_tau, W_r, b_r, W_h, b_h, out):
             h2[u] = work.tile([P, UW], BF16, name="h2", tag="h2", bufs=BUFS["h2"])
             nc.sync.dma_start(out=h2[u][:], in_=hv[:, u * UW : (u + 1) * UW])
 
-        def tin(u, i, ev=1):
-            evac = (nc.scalar.copy, nc.vector.tensor_copy)[ev]
+        def tin(u, i):
             if i == 0:
                 xg[u] = work.tile([P, UW // 2], F32, name="xg", tag="xg", bufs=BUFS["xg"], align_bytes=64)
                 hg[u] = work.tile([P, UW // 2], F32, name="hg", tag="hg", bufs=BUFS["hg"], align_bytes=64)
             if i < 2:
-                transpose_in(xn[u][:].bitcast(F32), PAIRS, xg[u][:], evac, (i,))
+                transpose_in(xn[u][:].bitcast(F32), PAIRS, xg[u][:], nc.vector.tensor_copy, (i,))
             else:
-                transpose_in(hn[u][:].bitcast(F32), PAIRS, hg[u][:], evac, (i - 2,))
+                transpose_in(hn[u][:].bitcast(F32), PAIRS, hg[u][:], nc.vector.tensor_copy, (i - 2,))
 
         def tinq(u):
             xc[u] = work.tile([P, NCOL], U32, name="xc", tag="xc", bufs=BUFS["xc"], align_bytes=64)
@@ -169,21 +169,30 @@ def tile_ltccell_t_kernel(tc, x, hidden, W_tau, b_tau, W_r, b_r, W_h, b_h, out):
                 bank = mx_pair(1, t, xc[u], xs[u], hc[u], hs[u])
                 nc.scalar.activation(out=th[u][:, sl], in_=bank[:], func=ACT.Tanh, bias=bias[:, 4 + t : 5 + t], scale=0.5)
 
-        def gate(u):
-            hh = work.tile([P, UW], BF16, name="hh", tag="hh", bufs=BUFS["hh"])
-            nc.vector.tensor_scalar(out=hh[:], in0=hg[u][:].bitcast(BF16), scalar1=0.5, scalar2=None, op0=ALU.mult)
-            dg = work.tile([P, UW], BF16, name="dg", tag="dg", bufs=BUFS["dg"], align_bytes=64)
+        def gh(u):
+            hh[u] = work.tile([P, UW], BF16, name="hh", tag="hh", bufs=BUFS["hh"])
+            nc.vector.tensor_scalar(out=hh[u][:], in0=hg[u][:].bitcast(BF16), scalar1=0.5, scalar2=None, op0=ALU.mult)
+
+        def gm(u):
+            dg[u] = work.tile([P, UW], BF16, name="dg", tag="dg", bufs=BUFS["dg"], align_bytes=64)
             nc.vector.scalar_tensor_tensor(
-                out=dg[:].rearrange("p (c t) -> p c t", t=4),
+                out=dg[u][:].rearrange("p (c t) -> p c t", t=4),
                 in0=th[u][:].rearrange("p (t c) -> p c t", t=4),
                 scalar=1.0,
-                in1=hh[:].rearrange("p (c t) -> p c t", t=4),
+                in1=hh[u][:].rearrange("p (c t) -> p c t", t=4),
                 op0=ALU.add,
                 op1=ALU.mult,
             )
+
+        def gq(u):
             dc[u] = work.tile([P, NCOL], U32, name="dc", tag="dc", bufs=BUFS["dc"], align_bytes=64)
             ds[u] = work.tile([P, NCOL], U8, name="ds", tag="ds", bufs=BUFS["dc"], align_bytes=64)
-            nc.vector.quantize_mx(out=dc[u][:].bitcast(FP8X4), scales=ds[u][:], in_=dg[:])
+            nc.vector.quantize_mx(out=dc[u][:].bitcast(FP8X4), scales=ds[u][:], in_=dg[u][:])
+
+        def gate(u):
+            gh(u)
+            gm(u)
+            gq(u)
 
         def ln(u):
             nc.scalar.activation(out=ee[u][:], in_=ee[u][:], func=ACT.Ln, bias=cst[:, 0:1], scale=1.0)
@@ -207,14 +216,22 @@ def tile_ltccell_t_kernel(tc, x, hidden, W_tau, b_tau, W_r, b_r, W_h, b_h, out):
             sl = slice(0, UW) if t is None else slice(t * NCOL, (t + 1) * NCOL)
             engines[e].tensor_tensor(out=ee[u][:, sl], in0=ee[u][:, sl], in1=ee[u][:, sl], op=ALU.mult)
 
-        def hb(u, t, e1):
+        def hb(u, t):
             if t == 0:
                 ht[u] = work.tile([P, UW], F32, name="ht", tag="ht", bufs=BUFS["ht"], align_bytes=64)
-            hgt = hg[u][:].bitcast(BF16).rearrange("p (c t) -> p t c", t=4)
             sl = slice(t * NCOL, (t + 1) * NCOL)
             bank = mx_pair(2, t, xc[u], xs[u], dc[u], ds[u])
             nc.scalar.activation(out=ht[u][:, sl], in_=bank[:], func=ACT.Tanh, bias=bias[:, 8 + t : 9 + t], scale=1.0)
-            engines[e1].tensor_tensor(out=ht[u][:, sl], in0=ht[u][:, sl], in1=hgt[:, t, :], op=ALU.subtract)
+
+        def t1(u, t, e1="v", n=1):
+            hgt = hg[u][:].bitcast(BF16).rearrange("p (c t) -> p t c", t=4)
+            sl = slice(t * NCOL, (t + n) * NCOL)
+            engines[e1].tensor_tensor(
+                out=ht[u][:, sl].rearrange("p (t c) -> p t c", t=n),
+                in0=ht[u][:, sl].rearrange("p (t c) -> p t c", t=n),
+                in1=hgt[:, t : t + n, :],
+                op=ALU.subtract,
+            )
 
         def t2(u, t, e2, times=2):
             sl = slice(t * NCOL, (t + 1) * NCOL)
@@ -222,7 +239,7 @@ def tile_ltccell_t_kernel(tc, x, hidden, W_tau, b_tau, W_r, b_r, W_h, b_h, out):
                 engines[e2].tensor_tensor(out=ht[u][:, sl], in0=ht[u][:, sl], in1=ee[u][:, sl], op=ALU.mult)
 
         def back(u, s):
-            tb = psum_t.tile([P, 4, P], F32, name="tb", tag="tbank")
+            tb = psum.tile([P, 4, P], F32, name="tb", tag="bank")
             for t in range(4):
                 o = t * NCOL + s * P
                 nc.tensor.transpose(tb[:, t, :], ht[u][:, o : o + P], ident[:])
@@ -236,10 +253,22 @@ def tile_ltccell_t_kernel(tc, x, hidden, W_tau, b_tau, W_r, b_r, W_h, b_h, out):
             o = u * UW + s * NCOL
             nc.sync.dma_start(out=ov[:, o : o + NCOL], in_=oo[:])
 
+        def backs(u, s):
+            tb = psum.tile([P, 4, P], F32, name="tb", tag="bank")
+            h2v = h2[u][:, s * NCOL : (s + 1) * NCOL].rearrange("p (m t) -> p t m", t=4)
+            for t in range(4):
+                o = t * NCOL + s * P
+                nc.tensor.matmul(out=tb[:, t, :], lhsT=identb[:], rhs=h2v[:, t, :], start=True, stop=False)
+                nc.tensor.matmul(out=tb[:, t, :], lhsT=ht[u][:, o : o + P], rhs=ident[:], is_transpose=True, start=False, stop=True)
+            oo = work.tile([P, NCOL], F32, name="oo", tag="oo", bufs=BUFS["oo"])
+            nc.scalar.copy(out=oo[:].rearrange("p (m t) -> p m t", t=4), in_=tb[:].rearrange("p t m -> p m t"))
+            o = u * UW + s * NCOL
+            nc.sync.dma_start(out=ov[:, o : o + NCOL], in_=oo[:])
+
         steps = {
             "setup": setup, "wload": wload, "bload": bload, "bprep": bprep, "wprep": wprep, "load": load,
             "load2": load2, "tin": tin, "tinq": tinq, "tr": tr, "gate": gate, "ln": ln, "lnb": lnb, "rho": rho, "ars": ars, "sq": sq,
-            "hb": hb, "t2": t2, "back": back, "qq": qq,
+            "hb": hb, "t1": t1, "t2": t2, "gh": gh, "gm": gm, "gq": gq, "back": back, "backs": backs, "qq": qq,
         }
         for step in PLAN:
             steps[step[0]](*step[1:])

@@ -22,8 +22,8 @@ NCOL = PAIRS * P
 UW = 4 * NCOL
 EPS = 1e-6
 
-PLAN = (("setup",),("wload",0,"v",),("load",0,),("wload",1,"v",),("bload",),("load",1,),("wload",2,"g",),("wprep",0,(0,),),("tin",0,0,),("tin",0,1,),("tin",0,2,),("tin",0,3,),("tinq",0,),("load",2,),("bprep",),("wprep",1,(0,),),("tin",1,0,),("tin",1,1,),("tin",1,2,),("tin",1,3,),("tinq",1,),("load",3,),("tr",0,0,),("tr",0,1,),("tr",0,2,),("tr",0,3,),("tin",2,0,),("tin",2,1,),("tin",2,2,),("tin",2,3,),("tinq",2,),("load",4,),("gh",0,),("gm",0,),("gq",0,),("tr",1,0,),("tr",1,1,),("tr",1,2,),("tr",1,3,),("tin",3,0,),("tin",3,1,),("tin",3,2,),("tin",3,3,),("tinq",3,),("load",5,),("gh",1,),("gm",1,),("gq",1,),("tr",2,0,),("tr",2,1,),("tr",2,2,),("tr",2,3,),("tin",4,0,),("tin",4,1,),("tin",4,2,),("tin",4,3,),("tinq",4,),("load",6,),("ln",0,),("ln",1,),("ln",2,),("gh",2,),("wprep",2,(1,),),("gm",2,),("gq",2,),("tin",5,0,),("tin",5,1,),("tin",5,2,),("tin",5,3,),("tinq",5,),("load",7,),("ars",0,),("qq",0,"g",0,),("qq",0,"g",1,),("qq",0,"g",2,),("qq",0,"g",3,),("ars",1,),("qq",1,"g",0,),("qq",1,"g",1,),("qq",1,"g",2,),("qq",1,"g",3,),("ars",2,),("qq",2,"g",0,),("qq",2,"g",1,),("qq",2,"g",2,),("qq",2,"g",3,),("load2",0,),("load2",1,),("hb",0,0,),("hb",0,1,),("hb",0,2,),("hb",0,3,),("t1",0,0,),("t1",0,1,),("t2",0,0,"v",1,),("t1",0,2,),("t2",0,1,"v",1,),("t1",0,3,),("t2",0,2,"v",1,),("t2",0,3,"v",1,),("tr",3,0,),("tr",3,1,),("tr",3,2,),("tr",3,3,),("hb",1,0,),("hb",1,1,),("hb",1,2,),("hb",1,3,),("gh",3,),("t1",1,0,),("gm",3,),("t1",1,1,),("t2",1,0,"v",1,),("gq",3,),("t1",1,2,),("t2",1,1,"v",1,),("t1",1,3,),("t2",1,2,"v",1,),("t2",1,3,"v",1,),("tr",4,0,),("tr",4,1,),("tr",4,2,),("tr",4,3,),("hb",2,0,),("hb",2,1,),("hb",2,2,),("hb",2,3,),("gh",4,),("t1",2,0,),("gm",4,),("t1",2,1,),("t2",2,0,"v",1,),("gq",4,),("t1",2,2,),("t2",2,1,"v",1,),("t1",2,3,),("t2",2,2,"v",1,),("t2",2,3,"v",1,),("tr",5,0,),("tr",5,1,),("tr",5,2,),("tr",5,3,),("ln",3,),("ln",4,),("ln",5,),("gh",5,),("back",0,0,),("back",0,1,),("back",0,2,),("back",0,3,),("load2",2,),("gm",5,),("tin",6,0,),("tin",6,1,),("tin",6,2,),("tin",6,3,),("tinq",6,),("gq",5,),("back",1,0,),("back",1,1,),("back",1,2,),("back",1,3,),("load2",3,),("tin",7,0,),("tin",7,1,),("tin",7,2,),("tin",7,3,),("tinq",7,),("back",2,0,),("back",2,1,),("back",2,2,),("back",2,3,),("load2",4,),("ars",3,),("qq",3,"g",0,),("qq",3,"g",1,),("qq",3,"g",2,),("qq",3,"g",3,),("ars",4,),("qq",4,"g",0,),("qq",4,"g",1,),("qq",4,"g",2,),("qq",4,"g",3,),("ars",5,),("qq",5,"g",0,),("qq",5,"g",1,),("qq",5,"g",2,),("qq",5,"g",3,),("hb",3,0,),("hb",3,1,),("hb",3,2,),("hb",3,3,),("t1",3,0,),("t1",3,1,),("t2",3,0,"v",1,),("t1",3,2,),("t2",3,1,"v",1,),("t1",3,3,),("t2",3,2,"v",1,),("t2",3,3,"v",1,),("tr",6,0,),("tr",6,1,),("tr",6,2,),("tr",6,3,),("hb",4,0,),("hb",4,1,),("hb",4,2,),("hb",4,3,),("gh",6,),("t1",4,0,),("gm",6,),("t1",4,1,),("t2",4,0,"v",1,),("gq",6,),("t1",4,2,),("t2",4,1,"v",1,),("t1",4,3,),("t2",4,2,"v",1,),("t2",4,3,"v",1,),("tr",7,0,),("tr",7,1,),("tr",7,2,),("tr",7,3,),("hb",5,0,),("hb",5,1,),("hb",5,2,),("hb",5,3,),("gh",7,),("t1",5,0,),("gm",7,),("t1",5,1,),("t2",5,0,"v",1,),("gq",7,),("t1",5,2,),("t2",5,1,"v",1,),("t1",5,3,),("t2",5,2,"v",1,),("t2",5,3,"v",1,),("ln",6,),("ln",7,),("back",3,0,),("back",3,1,),("back",3,2,),("back",3,3,),("load2",5,),("back",4,0,),("back",4,1,),("back",4,2,),("back",4,3,),("load2",6,),("back",5,0,),("back",5,1,),("back",5,2,),("back",5,3,),("load2",7,),("ars",6,),("qq",6,"g",0,),("qq",6,"g",1,),("qq",6,"g",2,),("qq",6,"g",3,),("ars",7,),("qq",7,"g",0,),("qq",7,"g",1,),("qq",7,"g",2,),("qq",7,"g",3,),("hb",6,0,),("hb",6,1,),("hb",6,2,),("hb",6,3,),("t1",6,0,),("t1",6,1,),("t2",6,0,"v",1,),("t1",6,2,),("t2",6,1,"v",1,),("t1",6,3,),("t2",6,2,"v",1,),("t2",6,3,"v",1,),("hb",7,0,),("hb",7,1,),("hb",7,2,),("hb",7,3,),("t1",7,0,),("t1",7,1,),("t2",7,0,"v",1,),("t1",7,2,),("t2",7,1,"v",1,),("t1",7,3,),("t2",7,2,"v",1,),("t2",7,3,"v",1,),("back",6,0,),("back",6,1,),("back",6,2,),("back",6,3,),("back",7,0,),("back",7,1,),("back",7,2,),("back",7,3,),)
-BUFS = {"th":2,"ht":4,"xn":2,"hn":2,"h2":2,"xg":2,"hg":6,"xc":6,"hc":5,"hh":2,"dg":2,"dc":6,"ee":5,"oo":4}
+PLAN = (("setup",),("wload",0,"v",),("load",0,),("wload",1,"v",),("bload",),("load",1,),("wload",2,"g",),("wprep",0,(0,),),("tin",0,0,),("tin",0,1,),("tin",0,2,),("tin",0,3,),("tinq",0,),("load",2,),("bprep",),("wprep",1,(0,),),("tin",1,0,),("tin",1,1,),("tin",1,2,),("tin",1,3,),("tinq",1,),("load",3,),("tr",0,0,),("tr",0,1,),("tr",0,2,),("tr",0,3,),("tin",2,0,),("tin",2,1,),("tin",2,2,),("tin",2,3,),("tinq",2,),("load",4,),("gh",0,),("gm",0,),("gq",0,),("tr",1,0,),("tr",1,1,),("tr",1,2,),("tr",1,3,),("tin",3,0,),("tin",3,1,),("tin",3,2,),("tin",3,3,),("tinq",3,),("load",5,),("gh",1,),("gm",1,),("gq",1,),("tr",2,0,),("tr",2,1,),("tr",2,2,),("tr",2,3,),("tin",4,0,),("tin",4,1,),("tin",4,2,),("tin",4,3,),("tinq",4,),("load",6,),("ln",0,),("ln",1,),("lnb",0,),("ln",2,),("lnb",1,),("lnb",2,),("gh",2,),("wprep",2,(1,),),("gm",2,),("gq",2,),("tin",5,0,),("tin",5,1,),("tin",5,2,),("tin",5,3,),("tinq",5,),("load",7,),("load2",0,),("load2",1,),("hb",0,0,),("rho",0,0,),("hb",0,1,),("rho",0,1,),("hb",0,2,),("rho",0,2,),("hb",0,3,),("rho",0,3,),("t1",0,0,),("t1",0,1,),("t2",0,0,"v",1,),("t1",0,2,),("t2",0,1,"v",1,),("t1",0,3,),("t2",0,2,"v",1,),("t2",0,3,"v",1,),("tr",3,0,),("tr",3,1,),("tr",3,2,),("tr",3,3,),("hb",1,0,),("rho",1,0,),("hb",1,1,),("rho",1,1,),("hb",1,2,),("rho",1,2,),("hb",1,3,),("rho",1,3,),("gh",3,),("t1",1,0,),("gm",3,),("t1",1,1,),("t2",1,0,"v",1,),("gq",3,),("t1",1,2,),("t2",1,1,"v",1,),("t1",1,3,),("t2",1,2,"v",1,),("t2",1,3,"v",1,),("back",0,0,),("back",0,1,),("back",0,2,),("back",0,3,),("load2",2,),("tr",4,0,),("tr",4,1,),("tr",4,2,),("tr",4,3,),("hb",2,0,),("rho",2,0,),("hb",2,1,),("rho",2,1,),("hb",2,2,),("rho",2,2,),("hb",2,3,),("rho",2,3,),("gh",4,),("t1",2,0,),("gm",4,),("t1",2,1,),("t2",2,0,"v",1,),("gq",4,),("t1",2,2,),("t2",2,1,"v",1,),("t1",2,3,),("t2",2,2,"v",1,),("t2",2,3,"v",1,),("back",1,0,),("back",1,1,),("back",1,2,),("back",1,3,),("load2",3,),("tr",5,0,),("tr",5,1,),("tr",5,2,),("tr",5,3,),("ln",3,),("ln",4,),("lnb",3,),("ln",5,),("lnb",4,),("lnb",5,),("gh",5,),("back",2,0,),("back",2,1,),("back",2,2,),("back",2,3,),("load2",4,),("gm",5,),("tin",6,0,),("tin",6,1,),("tin",6,2,),("tin",6,3,),("tinq",6,),("gq",5,),("tin",7,0,),("tin",7,1,),("tin",7,2,),("tin",7,3,),("tinq",7,),("hb",3,0,),("rho",3,0,),("hb",3,1,),("rho",3,1,),("hb",3,2,),("rho",3,2,),("hb",3,3,),("rho",3,3,),("t1",3,0,),("t1",3,1,),("t2",3,0,"v",1,),("t1",3,2,),("t2",3,1,"v",1,),("t1",3,3,),("t2",3,2,"v",1,),("t2",3,3,"v",1,),("tr",6,0,),("tr",6,1,),("tr",6,2,),("tr",6,3,),("hb",4,0,),("rho",4,0,),("hb",4,1,),("rho",4,1,),("hb",4,2,),("rho",4,2,),("hb",4,3,),("rho",4,3,),("gh",6,),("t1",4,0,),("gm",6,),("t1",4,1,),("t2",4,0,"v",1,),("gq",6,),("t1",4,2,),("t2",4,1,"v",1,),("t1",4,3,),("t2",4,2,"v",1,),("t2",4,3,"v",1,),("back",3,0,),("back",3,1,),("back",3,2,),("back",3,3,),("load2",5,),("tr",7,0,),("tr",7,1,),("tr",7,2,),("tr",7,3,),("hb",5,0,),("rho",5,0,),("hb",5,1,),("rho",5,1,),("hb",5,2,),("rho",5,2,),("hb",5,3,),("rho",5,3,),("gh",7,),("t1",5,0,),("gm",7,),("t1",5,1,),("t2",5,0,"v",1,),("gq",7,),("t1",5,2,),("t2",5,1,"v",1,),("t1",5,3,),("t2",5,2,"v",1,),("t2",5,3,"v",1,),("back",4,0,),("back",4,1,),("back",4,2,),("back",4,3,),("load2",6,),("ln",6,),("ln",7,),("lnb",6,),("lnb",7,),("back",5,0,),("back",5,1,),("back",5,2,),("back",5,3,),("load2",7,),("hb",6,0,),("rho",6,0,),("hb",6,1,),("rho",6,1,),("hb",6,2,),("rho",6,2,),("hb",6,3,),("rho",6,3,),("t1",6,0,),("t1",6,1,),("t2",6,0,"v",1,),("t1",6,2,),("t2",6,1,"v",1,),("t1",6,3,),("t2",6,2,"v",1,),("t2",6,3,"v",1,),("hb",7,0,),("rho",7,0,),("hb",7,1,),("rho",7,1,),("hb",7,2,),("rho",7,2,),("hb",7,3,),("rho",7,3,),("t1",7,0,),("t1",7,1,),("t2",7,0,"v",1,),("t1",7,2,),("t2",7,1,"v",1,),("t1",7,3,),("t2",7,2,"v",1,),("t2",7,3,"v",1,),("back",6,0,),("back",6,1,),("back",6,2,),("back",6,3,),("back",7,0,),("back",7,1,),("back",7,2,),("back",7,3,),)
+BUFS = {"th":2,"ht":3,"xn":2,"hn":2,"h2":2,"xg":2,"hg":8,"xc":8,"hc":5,"hh":2,"dg":2,"dc":6,"ee":5,"oo":4}
 
 
 def tile_ltccell_t_kernel(tc, x, hidden, W_tau, b_tau, W_r, b_r, W_h, b_h, out):
@@ -125,14 +125,15 @@ def tile_ltccell_t_kernel(tc, x, hidden, W_tau, b_tau, W_r, b_r, W_h, b_h, out):
             h2[u] = work.tile([P, UW], BF16, name="h2", tag="h2", bufs=BUFS["h2"])
             nc.sync.dma_start(out=h2[u][:], in_=hv[:, u * UW : (u + 1) * UW])
 
-        def tin(u, i):
+        def tin(u, i, ev=1):
+            evac = (nc.scalar.copy, nc.vector.tensor_copy)[ev]
             if i == 0:
                 xg[u] = work.tile([P, UW // 2], F32, name="xg", tag="xg", bufs=BUFS["xg"], align_bytes=64)
                 hg[u] = work.tile([P, UW // 2], F32, name="hg", tag="hg", bufs=BUFS["hg"], align_bytes=64)
             if i < 2:
-                transpose_in(xn[u][:].bitcast(F32), PAIRS, xg[u][:], nc.vector.tensor_copy, (i,))
+                transpose_in(xn[u][:].bitcast(F32), PAIRS, xg[u][:], evac, (i,))
             else:
-                transpose_in(hn[u][:].bitcast(F32), PAIRS, hg[u][:], nc.vector.tensor_copy, (i - 2,))
+                transpose_in(hn[u][:].bitcast(F32), PAIRS, hg[u][:], evac, (i - 2,))
 
         def tinq(u):
             xc[u] = work.tile([P, NCOL], U32, name="xc", tag="xc", bufs=BUFS["xc"], align_bytes=64)
@@ -233,8 +234,8 @@ def tile_ltccell_t_kernel(tc, x, hidden, W_tau, b_tau, W_r, b_r, W_h, b_h, out):
                 op=ALU.subtract,
             )
 
-        def t2(u, t, e2, times=2):
-            sl = slice(t * NCOL, (t + 1) * NCOL)
+        def t2(u, t, e2, times=2, n=1):
+            sl = slice(t * NCOL, (t + n) * NCOL)
             for i in range(times):
                 engines[e2].tensor_tensor(out=ht[u][:, sl], in0=ht[u][:, sl], in1=ee[u][:, sl], op=ALU.mult)
 

@@ -12,18 +12,24 @@ ACT = mybir.ActivationFunctionType
 ALU = mybir.AluOpType
 
 P = 128
+HALF = P // 2
+PACK = 4
 B, I, H = 8192, 256, 256
 FLOPS = 3 * 2 * B * (I + H) * H
 ROWS = B // P
 UNITS = 8
-UROWS = ROWS // UNITS
-PAIRS = UROWS // 2
+PAIRS = ROWS // UNITS // 2
 NCOL = PAIRS * P
-UW = 4 * NCOL
+UW = PACK * NCOL
+WCOL = 2 * PACK * P
 EPS = 1e-6
+TAU, GATE, CAND = 0, 1, 2
 
-PLAN = (("setup",),("wload",0,"v",),("load",0,),("wload",1,"v",),("bload",),("load",1,),("wload",2,"g",),("wprep",0,(0,),),("tin",0,0,),("tin",0,1,),("tin",0,2,),("tin",0,3,),("tinq",0,),("load",2,),("bprep",),("wprep",1,(0,),),("tin",1,0,),("tin",1,1,),("tin",1,2,),("tin",1,3,),("tinq",1,),("load",3,),("tr",0,0,),("tr",0,1,),("tr",0,2,),("tr",0,3,),("tin",2,0,),("tin",2,1,),("tin",2,2,),("tin",2,3,),("tinq",2,),("load",4,),("gh",0,),("gm",0,),("gq",0,),("tr",1,0,),("tr",1,1,),("tr",1,2,),("tr",1,3,),("tin",3,0,),("tin",3,1,),("tin",3,2,),("tin",3,3,),("tinq",3,),("load",5,),("gh",1,),("gm",1,),("gq",1,),("tr",2,0,),("tr",2,1,),("tr",2,2,),("tr",2,3,),("tin",4,0,),("tin",4,1,),("tin",4,2,),("tin",4,3,),("tinq",4,),("load",6,),("ln",0,),("ln",1,),("lnb",0,),("ln",2,),("lnb",1,),("lnb",2,),("gh",2,),("wprep",2,(1,),),("gm",2,),("gq",2,),("tin",5,0,),("tin",5,1,),("tin",5,2,),("tin",5,3,),("tinq",5,),("load",7,),("load2",0,),("load2",1,),("hb",0,0,),("rho",0,0,),("hb",0,1,),("rho",0,1,),("hb",0,2,),("rho",0,2,),("hb",0,3,),("rho",0,3,),("t1",0,0,),("t1",0,1,),("t2",0,0,"v",1,),("t1",0,2,),("t2",0,1,"v",1,),("t1",0,3,),("t2",0,2,"v",1,),("t2",0,3,"v",1,),("tr",3,0,),("tr",3,1,),("tr",3,2,),("tr",3,3,),("hb",1,0,),("rho",1,0,),("hb",1,1,),("rho",1,1,),("hb",1,2,),("rho",1,2,),("hb",1,3,),("rho",1,3,),("gh",3,),("t1",1,0,),("gm",3,),("t1",1,1,),("t2",1,0,"v",1,),("gq",3,),("t1",1,2,),("t2",1,1,"v",1,),("t1",1,3,),("t2",1,2,"v",1,),("t2",1,3,"v",1,),("back",0,0,),("back",0,1,),("back",0,2,),("back",0,3,),("load2",2,),("tr",4,0,),("tr",4,1,),("tr",4,2,),("tr",4,3,),("hb",2,0,),("rho",2,0,),("hb",2,1,),("rho",2,1,),("hb",2,2,),("rho",2,2,),("hb",2,3,),("rho",2,3,),("gh",4,),("t1",2,0,),("gm",4,),("t1",2,1,),("t2",2,0,"v",1,),("gq",4,),("t1",2,2,),("t2",2,1,"v",1,),("t1",2,3,),("t2",2,2,"v",1,),("t2",2,3,"v",1,),("back",1,0,),("back",1,1,),("back",1,2,),("back",1,3,),("load2",3,),("tr",5,0,),("tr",5,1,),("tr",5,2,),("tr",5,3,),("ln",3,),("ln",4,),("lnb",3,),("ln",5,),("lnb",4,),("lnb",5,),("gh",5,),("back",2,0,),("back",2,1,),("back",2,2,),("back",2,3,),("load2",4,),("gm",5,),("tin",6,0,),("tin",6,1,),("tin",6,2,),("tin",6,3,),("tinq",6,),("gq",5,),("tin",7,0,),("tin",7,1,),("tin",7,2,),("tin",7,3,),("tinq",7,),("hb",3,0,),("rho",3,0,),("hb",3,1,),("rho",3,1,),("hb",3,2,),("rho",3,2,),("hb",3,3,),("rho",3,3,),("t1",3,0,),("t1",3,1,),("t2",3,0,"v",1,),("t1",3,2,),("t2",3,1,"v",1,),("t1",3,3,),("t2",3,2,"v",1,),("t2",3,3,"v",1,),("tr",6,0,),("tr",6,1,),("tr",6,2,),("tr",6,3,),("hb",4,0,),("rho",4,0,),("hb",4,1,),("rho",4,1,),("hb",4,2,),("rho",4,2,),("hb",4,3,),("rho",4,3,),("gh",6,),("t1",4,0,),("gm",6,),("t1",4,1,),("t2",4,0,"v",1,),("gq",6,),("t1",4,2,),("t2",4,1,"v",1,),("t1",4,3,),("t2",4,2,"v",1,),("t2",4,3,"v",1,),("back",3,0,),("back",3,1,),("back",3,2,),("back",3,3,),("load2",5,),("tr",7,0,),("tr",7,1,),("tr",7,2,),("tr",7,3,),("hb",5,0,),("rho",5,0,),("hb",5,1,),("rho",5,1,),("hb",5,2,),("rho",5,2,),("hb",5,3,),("rho",5,3,),("gh",7,),("t1",5,0,),("gm",7,),("t1",5,1,),("t2",5,0,"v",1,),("gq",7,),("t1",5,2,),("t2",5,1,"v",1,),("t1",5,3,),("t2",5,2,"v",1,),("t2",5,3,"v",1,),("back",4,0,),("back",4,1,),("back",4,2,),("back",4,3,),("load2",6,),("ln",6,),("ln",7,),("lnb",6,),("lnb",7,),("back",5,0,),("back",5,1,),("back",5,2,),("back",5,3,),("load2",7,),("hb",6,0,),("rho",6,0,),("hb",6,1,),("rho",6,1,),("hb",6,2,),("rho",6,2,),("hb",6,3,),("rho",6,3,),("t1",6,0,),("t1",6,1,),("t2",6,0,"v",1,),("t1",6,2,),("t2",6,1,"v",1,),("t1",6,3,),("t2",6,2,"v",1,),("t2",6,3,"v",1,),("hb",7,0,),("rho",7,0,),("hb",7,1,),("rho",7,1,),("hb",7,2,),("rho",7,2,),("hb",7,3,),("rho",7,3,),("t1",7,0,),("t1",7,1,),("t2",7,0,"v",1,),("t1",7,2,),("t2",7,1,"v",1,),("t1",7,3,),("t2",7,2,"v",1,),("t2",7,3,"v",1,),("back",6,0,),("back",6,1,),("back",6,2,),("back",6,3,),("back",7,0,),("back",7,1,),("back",7,2,),("back",7,3,),)
-BUFS = {"th":2,"ht":3,"xn":2,"hn":2,"h2":2,"xg":2,"hg":8,"xc":8,"hc":5,"hh":2,"dg":2,"dc":6,"ee":5,"oo":4}
+GROUPS = ((0, 1, 2), (3, 4, 5), (6, 7))
+LEAD = 2
+SCALAR_END = 6
+
+BUFS = {"th": 2, "ht": 3, "xn": 2, "hn": 2, "h2": 2, "xg": 2, "hg": 8, "xc": 8, "hc": 5, "hh": 2, "dg": 2, "dc": 6, "ee": 5, "oo": 4}
 
 
 def tile_ltccell_t_kernel(tc, x, hidden, W_tau, b_tau, W_r, b_r, W_h, b_h, out):
@@ -44,24 +50,16 @@ def tile_ltccell_t_kernel(tc, x, hidden, W_tau, b_tau, W_r, b_r, W_h, b_h, out):
         identb = const.tile([P, P], BF16, name="identb")
         cst = const.tile([P, 2], F32, name="cst")
         braw = const.tile([P, 3, 16], BF16, name="braw")
-        bias = const.tile([P, 12], F32, name="bias")
-        wc = const.tile([P, 3 * 1024], U32, name="wc", align_bytes=64)
-        ws = const.tile([P, 3 * 1024], U8, name="ws", align_bytes=64)
+        bias = const.tile([P, 3 * PACK], F32, name="bias")
+        wc = const.tile([P, 3 * WCOL], U32, name="wc", align_bytes=64)
+        ws = const.tile([P, 3 * WCOL], U8, name="ws", align_bytes=64)
 
         xn, hn, h2, hg, xc, xs, hc, hs = {}, {}, {}, {}, {}, {}, {}, {}
         dc, ds, th, ee, ht, wn, xg, wg, hh, dg = {}, {}, {}, {}, {}, {}, {}, {}, {}, {}
 
-        engines = {"v": nc.vector, "g": nc.gpsimd}
+        def chunk(t):
+            return slice(t * NCOL, (t + 1) * NCOL)
 
-        def transpose_in(src_words, n_pairs, dst_words, evac, pieces=None):
-            sv = src_words.rearrange("p (s m u) -> p s m u", s=n_pairs, m=P, u=2)
-            dv = dst_words.rearrange("p (s m u) -> p s m u", s=n_pairs, m=P, u=2)
-            for sb in pieces or range(n_pairs // 2):
-                bank = psum.tile([P, 2, 2, P], F32, name="tin", tag="bank")
-                for s2 in range(2):
-                    for u in range(2):
-                        nc.tensor.transpose(bank[:, s2, u, :], sv[:, 2 * sb + s2, :, u], ident[:])
-                evac(out=dv[:, 2 * sb : 2 * sb + 2, :, :], in_=bank[:].rearrange("p s u m -> p s m u"))
 
         def setup():
             make_identity(nc, ident[:])
@@ -69,207 +67,263 @@ def tile_ltccell_t_kernel(tc, x, hidden, W_tau, b_tau, W_r, b_r, W_h, b_h, out):
             nc.vector.memset(cst[:, 0:1], 1.0)
             nc.vector.memset(cst[:, 1:2], EPS)
 
-        def wload(w, ez):
+        def load_weight(w, zero_engine):
             wn[w] = work.tile([P, 2, 768], BF16, name="wn", tag="ee", bufs=BUFS["ee"])
             src = weights[w].rearrange("(c p) k -> p c k", p=P)
             nc.sync.dma_start(out=wn[w][:, :, 0:512], in_=src)
             nc.sync.dma_start(out=wn[w][:, :, 512:768], in_=src[:, :, 0:256])
-            wg[w] = work.tile([P, 2048], F32, name="wg", tag="ht", bufs=BUFS["ht"], align_bytes=64)
-            z = wg[w][:].rearrange("p (a m u) -> p a m u", a=8, m=P, u=2)
-            engines[ez].memset(z[0:64, :, 64:128, :], 0.0)
-            engines[ez].memset(z[64:128, :, 0:64, :], 0.0)
+            wg[w] = work.tile([P, 2 * WCOL], F32, name="wg", tag="ht", bufs=BUFS["ht"], align_bytes=64)
+            z = wg[w][:].rearrange("p (a m u) -> p a m u", a=2 * PACK, m=P, u=2)
+            zero_engine.memset(z[0:HALF, :, HALF:P, :], 0.0)
+            zero_engine.memset(z[HALF:P, :, 0:HALF, :], 0.0)
 
-        def bload():
+        def load_biases():
             for w in range(3):
-                src = biases[w].rearrange("(j t) -> j t", t=4)
-                nc.sync.dma_start(out=braw[0:64, w, 0:4], in_=src)
-                nc.sync.dma_start(out=braw[64:128, w, 0:4], in_=src)
+                src = biases[w].rearrange("(j t) -> j t", t=PACK)
+                nc.sync.dma_start(out=braw[0:HALF, w, 0:PACK], in_=src)
+                nc.sync.dma_start(out=braw[HALF:P, w, 0:PACK], in_=src)
 
-        def bprep():
-            bv = bias[:].rearrange("p (w t) -> p w t", w=3)
-            nc.vector.tensor_copy(out=bv, in_=braw[:, :, 0:4])
-            nc.vector.tensor_scalar(out=bias[:, 4:8], in0=bias[:, 4:8], scalar1=0.5, scalar2=None, op0=ALU.mult)
+        def prepare_biases():
+            nc.vector.tensor_copy(out=bias[:].rearrange("p (w t) -> p w t", w=3), in_=braw[:, :, 0:PACK])
+            gate_bias = bias[:, PACK * GATE : PACK * GATE + PACK]
+            nc.vector.tensor_scalar(out=gate_bias, in0=gate_bias, scalar1=0.5, scalar2=None, op0=ALU.mult)
 
-        def wprep(w, evacs):
+        def prepare_weight(w, copy_out):
             words = wn[w][:].rearrange("p c k -> p (c k)").bitcast(F32).rearrange("p (c k) -> p c k", c=2)
-            dv = wg[w][:].rearrange("p (t a m u) -> p t a m u", t=4, a=2, m=P, u=2)
-            n = 0
+            dv = wg[w][:].rearrange("p (t a m u) -> p t a m u", t=PACK, a=2, m=P, u=2)
             for order in range(2):
                 bank = psum.tile([P, 2, 2, P], F32, name="wt", tag="bank")
                 for c in range(2):
-                    sv = words[:, c, 128 * order : 128 * order + 256].rearrange("p (m u) -> p m u", u=2)
+                    sv = words[:, c, P * order : P * order + 2 * P].rearrange("p (m u) -> p m u", u=2)
                     for u in range(2):
                         nc.tensor.transpose(bank[:, u, c, :], sv[:, :, u], ident[:])
                 for half in range(2):
-                    rows = slice(64 * half, 64 * half + 64)
+                    rows = slice(HALF * half, HALF * half + HALF)
                     part = (order + half) % 2
                     for c in range(2):
-                        m0 = 64 * half + 32 * c
-                        evac = (nc.scalar.copy, nc.vector.tensor_copy)[evacs[n % len(evacs)]]
-                        n += 1
-                        evac(
+                        m0 = HALF * half + 32 * c
+                        copy_out(
                             out=dv[rows, :, part, m0 : m0 + 32, :],
-                            in_=bank[rows, :, c, :].rearrange("p u (q t) -> p t q u", t=4),
+                            in_=bank[rows, :, c, :].rearrange("p u (q t) -> p t q u", t=PACK),
                         )
-            cols = slice(w * 1024, (w + 1) * 1024)
+            cols = slice(w * WCOL, (w + 1) * WCOL)
             nc.vector.quantize_mx(out=wc[:, cols].bitcast(FP8X4), scales=ws[:, cols], in_=wg[w][:].bitcast(BF16))
 
-        def load(u):
+
+        def load_inputs(u):
+            if u >= UNITS:
+                return
             cols = slice(u * UW, (u + 1) * UW)
             xn[u] = work.tile([P, UW], BF16, name="xn", tag="xn", bufs=BUFS["xn"])
             nc.sync.dma_start(out=xn[u][:], in_=xv[:, cols])
             hn[u] = work.tile([P, UW], BF16, name="hn", tag="hn", bufs=BUFS["hn"])
             nc.sync.dma_start(out=hn[u][:], in_=hv[:, cols])
 
-        def load2(u):
+        def load_hidden_again(u):
+            if u >= UNITS:
+                return
             h2[u] = work.tile([P, UW], BF16, name="h2", tag="h2", bufs=BUFS["h2"])
             nc.sync.dma_start(out=h2[u][:], in_=hv[:, u * UW : (u + 1) * UW])
 
-        def tin(u, i, ev=1):
-            evac = (nc.scalar.copy, nc.vector.tensor_copy)[ev]
-            if i == 0:
-                xg[u] = work.tile([P, UW // 2], F32, name="xg", tag="xg", bufs=BUFS["xg"], align_bytes=64)
-                hg[u] = work.tile([P, UW // 2], F32, name="hg", tag="hg", bufs=BUFS["hg"], align_bytes=64)
-            if i < 2:
-                transpose_in(xn[u][:].bitcast(F32), PAIRS, xg[u][:], evac, (i,))
-            else:
-                transpose_in(hn[u][:].bitcast(F32), PAIRS, hg[u][:], evac, (i - 2,))
+        def transpose_rows(natural, transposed):
+            sv = natural[:].bitcast(F32).rearrange("p (s m u) -> p s m u", s=PAIRS, m=P, u=2)
+            dv = transposed[:].rearrange("p (s m u) -> p s m u", s=PAIRS, m=P, u=2)
+            for s in range(0, PAIRS, 2):
+                bank = psum.tile([P, 2, 2, P], F32, name="tin", tag="bank")
+                for s2 in range(2):
+                    for u in range(2):
+                        nc.tensor.transpose(bank[:, s2, u, :], sv[:, s + s2, :, u], ident[:])
+                nc.vector.tensor_copy(out=dv[:, s : s + 2, :, :], in_=bank[:].rearrange("p s u m -> p s m u"))
 
-        def tinq(u):
+        def bring_in(u):
+            if u >= UNITS or u in xc:
+                return
+            xg[u] = work.tile([P, UW // 2], F32, name="xg", tag="xg", bufs=BUFS["xg"], align_bytes=64)
+            hg[u] = work.tile([P, UW // 2], F32, name="hg", tag="hg", bufs=BUFS["hg"], align_bytes=64)
+            transpose_rows(xn[u], xg[u])
+            transpose_rows(hn[u], hg[u])
             xc[u] = work.tile([P, NCOL], U32, name="xc", tag="xc", bufs=BUFS["xc"], align_bytes=64)
             xs[u] = work.tile([P, NCOL], U8, name="xs", tag="xs", bufs=BUFS["xc"], align_bytes=64)
             hc[u] = work.tile([P, NCOL], U32, name="hc", tag="hc", bufs=BUFS["hc"], align_bytes=64)
             hs[u] = work.tile([P, NCOL], U8, name="hs", tag="hs", bufs=BUFS["hc"], align_bytes=64)
             nc.vector.quantize_mx(out=xc[u][:].bitcast(FP8X4), scales=xs[u][:], in_=xg[u][:].bitcast(BF16))
             nc.vector.quantize_mx(out=hc[u][:].bitcast(FP8X4), scales=hs[u][:], in_=hg[u][:].bitcast(BF16))
+            load_inputs(u + LEAD)
 
-        def mx_pair(w, t, c1, s1, c2, s2):
+
+        def mx_group(w, t, second_codes, second_scales, u):
             bank = psum.tile([P, NCOL], F32, name="mx", tag="bank")
-            for part, (cc, ss) in enumerate(((c1, s1), (c2, s2))):
-                o = w * 1024 + (2 * t + part) * P
+            for part, (codes, scales) in enumerate(((xc[u], xs[u]), (second_codes, second_scales))):
+                o = w * WCOL + (2 * t + part) * P
                 nc.tensor.matmul_mx(
                     out=bank[:],
                     lhsT=wc[:, o : o + P].bitcast(FP8X4),
                     lhsT_scale=ws[:, o : o + P],
-                    rhs=cc[:].bitcast(FP8X4),
-                    rhs_scale=ss[:],
+                    rhs=codes[:].bitcast(FP8X4),
+                    rhs_scale=scales[:],
                     start=(part == 0),
                     stop=(part == 1),
                 )
             return bank
 
-        def tr(u, t, which=(0, 1)):
-            if u not in ee:
-                ee[u] = work.tile([P, UW], F32, name="ee", tag="ee", bufs=BUFS["ee"])
-                th[u] = work.tile([P, UW], F32, name="th", tag="th", bufs=BUFS["th"], align_bytes=64)
-            sl = slice(t * NCOL, (t + 1) * NCOL)
-            if 0 in which:
-                bank = mx_pair(0, t, xc[u], xs[u], hc[u], hs[u])
-                nc.scalar.activation(out=ee[u][:, sl], in_=bank[:], func=ACT.Exp, bias=bias[:, t : t + 1], scale=1.0)
-            if 1 in which:
-                bank = mx_pair(1, t, xc[u], xs[u], hc[u], hs[u])
-                nc.scalar.activation(out=th[u][:, sl], in_=bank[:], func=ACT.Tanh, bias=bias[:, 4 + t : 5 + t], scale=0.5)
+        def bias_of(w, t):
+            return bias[:, PACK * w + t : PACK * w + t + 1]
 
-        def gh(u):
+        def tau_and_gate(u):
+            ee[u] = work.tile([P, UW], F32, name="ee", tag="ee", bufs=BUFS["ee"])
+            th[u] = work.tile([P, UW], F32, name="th", tag="th", bufs=BUFS["th"], align_bytes=64)
+            for t in range(PACK):
+                bank = mx_group(TAU, t, hc[u], hs[u], u)
+                nc.scalar.activation(out=ee[u][:, chunk(t)], in_=bank[:], func=ACT.Exp, bias=bias_of(TAU, t), scale=1.0)
+                bank = mx_group(GATE, t, hc[u], hs[u], u)
+                nc.scalar.activation(out=th[u][:, chunk(t)], in_=bank[:], func=ACT.Tanh, bias=bias_of(GATE, t), scale=0.5)
+
+        def halve_hidden(u):
             hh[u] = work.tile([P, UW], BF16, name="hh", tag="hh", bufs=BUFS["hh"])
             nc.vector.tensor_scalar(out=hh[u][:], in0=hg[u][:].bitcast(BF16), scalar1=0.5, scalar2=None, op0=ALU.mult)
 
-        def gm(u):
+        def gate_hidden(u):
             dg[u] = work.tile([P, UW], BF16, name="dg", tag="dg", bufs=BUFS["dg"], align_bytes=64)
             nc.vector.scalar_tensor_tensor(
-                out=dg[u][:].rearrange("p (c t) -> p c t", t=4),
-                in0=th[u][:].rearrange("p (t c) -> p c t", t=4),
+                out=dg[u][:].rearrange("p (c t) -> p c t", t=PACK),
+                in0=th[u][:].rearrange("p (t c) -> p c t", t=PACK),
                 scalar=1.0,
-                in1=hh[u][:].rearrange("p (c t) -> p c t", t=4),
+                in1=hh[u][:].rearrange("p (c t) -> p c t", t=PACK),
                 op0=ALU.add,
                 op1=ALU.mult,
             )
 
-        def gq(u):
+        def quantise_gated(u):
             dc[u] = work.tile([P, NCOL], U32, name="dc", tag="dc", bufs=BUFS["dc"], align_bytes=64)
             ds[u] = work.tile([P, NCOL], U8, name="ds", tag="ds", bufs=BUFS["dc"], align_bytes=64)
             nc.vector.quantize_mx(out=dc[u][:].bitcast(FP8X4), scales=ds[u][:], in_=dg[u][:])
 
-        def gate(u):
-            gh(u)
-            gm(u)
-            gq(u)
-
-        def ln(u):
+        def softplus(u):
             nc.scalar.activation(out=ee[u][:], in_=ee[u][:], func=ACT.Ln, bias=cst[:, 0:1], scale=1.0)
 
-        def lnb(u):
+        def log_tau(u):
             nc.scalar.activation(out=ee[u][:], in_=ee[u][:], func=ACT.Ln, bias=cst[:, 1:2], scale=1.0)
 
-        def rho(u, t=None):
-            sl = slice(0, UW) if t is None else slice(t * NCOL, (t + 1) * NCOL)
-            nc.scalar.activation(out=ee[u][:, sl], in_=ee[u][:, sl], func=ACT.Exp, scale=-1.0)
+        def candidate(u):
+            ht[u] = work.tile([P, UW], F32, name="ht", tag="ht", bufs=BUFS["ht"], align_bytes=64)
+            for t in range(PACK):
+                bank = mx_group(CAND, t, dc[u], ds[u], u)
+                nc.scalar.activation(out=ht[u][:, chunk(t)], in_=bank[:], func=ACT.Tanh, bias=bias_of(CAND, t), scale=1.0)
+                nc.scalar.activation(out=ee[u][:, chunk(t)], in_=ee[u][:, chunk(t)], func=ACT.Exp, scale=-1.0)
 
-        def ars(u, t=None):
-            sl = slice(0, UW) if t is None else slice(t * NCOL, (t + 1) * NCOL)
-            nc.scalar.activation(out=ee[u][:, sl], in_=ee[u][:, sl], func=ACT.Abs_reciprocal_sqrt, bias=cst[:, 1:2], scale=1.0)
+        def subtract_hidden(u, t):
+            plane = hg[u][:].bitcast(BF16).rearrange("p (c t) -> p t c", t=PACK)[:, t : t + 1, :]
+            part = ht[u][:, chunk(t)].rearrange("p (t c) -> p t c", t=1)
+            nc.vector.tensor_tensor(out=part, in0=part, in1=plane, op=ALU.subtract)
 
-        def sq(u, t=None):
-            sl = slice(0, UW) if t is None else slice(t * NCOL, (t + 1) * NCOL)
-            nc.scalar.activation(out=ee[u][:, sl], in_=ee[u][:, sl], func=ACT.Square)
+        def divide_by_tau(u, t):
+            nc.vector.tensor_tensor(out=ht[u][:, chunk(t)], in0=ht[u][:, chunk(t)], in1=ee[u][:, chunk(t)], op=ALU.mult)
 
-        def qq(u, e, t=None):
-            sl = slice(0, UW) if t is None else slice(t * NCOL, (t + 1) * NCOL)
-            engines[e].tensor_tensor(out=ee[u][:, sl], in0=ee[u][:, sl], in1=ee[u][:, sl], op=ALU.mult)
+        def candidate_and_gating(u, g):
+            if u is None:
+                if g is not None:
+                    halve_hidden(g)
+                    gate_hidden(g)
+                    quantise_gated(g)
+                return
+            candidate(u)
+            if g is not None:
+                halve_hidden(g)
+            subtract_hidden(u, 0)
+            if g is not None:
+                gate_hidden(g)
+            subtract_hidden(u, 1)
+            divide_by_tau(u, 0)
+            if g is not None:
+                quantise_gated(g)
+            for t in range(2, PACK):
+                subtract_hidden(u, t)
+                divide_by_tau(u, t - 1)
+            divide_by_tau(u, PACK - 1)
 
-        def hb(u, t):
-            if t == 0:
-                ht[u] = work.tile([P, UW], F32, name="ht", tag="ht", bufs=BUFS["ht"], align_bytes=64)
-            sl = slice(t * NCOL, (t + 1) * NCOL)
-            bank = mx_pair(2, t, xc[u], xs[u], dc[u], ds[u])
-            nc.scalar.activation(out=ht[u][:, sl], in_=bank[:], func=ACT.Tanh, bias=bias[:, 8 + t : 9 + t], scale=1.0)
 
-        def t1(u, t, e1="v", n=1):
-            hgt = hg[u][:].bitcast(BF16).rearrange("p (c t) -> p t c", t=4)
-            sl = slice(t * NCOL, (t + n) * NCOL)
-            engines[e1].tensor_tensor(
-                out=ht[u][:, sl].rearrange("p (t c) -> p t c", t=n),
-                in0=ht[u][:, sl].rearrange("p (t c) -> p t c", t=n),
-                in1=hgt[:, t : t + n, :],
-                op=ALU.subtract,
-            )
+        def give_back(u):
+            for s in range(PAIRS):
+                bank = psum.tile([P, PACK, P], F32, name="tb", tag="bank")
+                again = h2[u][:, chunk(s)]
+                result = work.tile([P, NCOL], F32, name="oo", tag="oo", bufs=BUFS["oo"])
+                if u == SCALAR_END:
+                    planes = again.rearrange("p (m t) -> p t m", t=PACK)
+                    for t in range(PACK):
+                        o = t * NCOL + s * P
+                        nc.tensor.matmul(out=bank[:, t, :], lhsT=identb[:], rhs=planes[:, t, :], start=True, stop=False)
+                        nc.tensor.matmul(
+                            out=bank[:, t, :], lhsT=ht[u][:, o : o + P], rhs=ident[:], is_transpose=True, start=False, stop=True
+                        )
+                    nc.scalar.copy(out=result[:].rearrange("p (m t) -> p m t", t=PACK), in_=bank[:].rearrange("p t m -> p m t"))
+                else:
+                    for t in range(PACK):
+                        o = t * NCOL + s * P
+                        nc.tensor.transpose(bank[:, t, :], ht[u][:, o : o + P], ident[:])
+                    nc.vector.tensor_tensor(
+                        out=result[:].rearrange("p (m t) -> p m t", t=PACK),
+                        in0=bank[:].rearrange("p t m -> p m t"),
+                        in1=again.rearrange("p (m t) -> p m t", t=PACK),
+                        op=ALU.add,
+                    )
+                o = u * UW + s * NCOL
+                nc.sync.dma_start(out=ov[:, o : o + NCOL], in_=result[:])
+            load_hidden_again(u + LEAD)
 
-        def t2(u, t, e2, times=2, n=1):
-            sl = slice(t * NCOL, (t + n) * NCOL)
-            for i in range(times):
-                engines[e2].tensor_tensor(out=ht[u][:, sl], in0=ht[u][:, sl], in1=ee[u][:, sl], op=ALU.mult)
 
-        def back(u, s):
-            tb = psum.tile([P, 4, P], F32, name="tb", tag="bank")
-            for t in range(4):
-                o = t * NCOL + s * P
-                nc.tensor.transpose(tb[:, t, :], ht[u][:, o : o + P], ident[:])
-            oo = work.tile([P, NCOL], F32, name="oo", tag="oo", bufs=BUFS["oo"])
-            nc.vector.tensor_tensor(
-                out=oo[:].rearrange("p (m t) -> p m t", t=4),
-                in0=tb[:].rearrange("p t m -> p m t"),
-                in1=h2[u][:, s * NCOL : (s + 1) * NCOL].rearrange("p (m t) -> p m t", t=4),
-                op=ALU.add,
-            )
-            o = u * UW + s * NCOL
-            nc.sync.dma_start(out=ov[:, o : o + NCOL], in_=oo[:])
+        setup()
+        load_weight(TAU, nc.vector)
+        load_inputs(0)
+        load_weight(GATE, nc.vector)
+        load_biases()
+        load_inputs(1)
+        load_weight(CAND, nc.gpsimd)
+        prepare_weight(TAU, nc.scalar.copy)
+        bring_in(0)
+        prepare_biases()
+        prepare_weight(GATE, nc.scalar.copy)
 
-        def backs(u, s):
-            tb = psum.tile([P, 4, P], F32, name="tb", tag="bank")
-            h2v = h2[u][:, s * NCOL : (s + 1) * NCOL].rearrange("p (m t) -> p t m", t=4)
-            for t in range(4):
-                o = t * NCOL + s * P
-                nc.tensor.matmul(out=tb[:, t, :], lhsT=identb[:], rhs=h2v[:, t, :], start=True, stop=False)
-                nc.tensor.matmul(out=tb[:, t, :], lhsT=ht[u][:, o : o + P], rhs=ident[:], is_transpose=True, start=False, stop=True)
-            oo = work.tile([P, NCOL], F32, name="oo", tag="oo", bufs=BUFS["oo"])
-            nc.scalar.copy(out=oo[:].rearrange("p (m t) -> p m t", t=4), in_=tb[:].rearrange("p t m -> p m t"))
-            o = u * UW + s * NCOL
-            nc.sync.dma_start(out=ov[:, o : o + NCOL], in_=oo[:])
+        for k in range(len(GROUPS) + 1):
+            now = GROUPS[k] if k < len(GROUPS) else ()
+            before = GROUPS[k - 1] if k > 0 else ()
+            after = GROUPS[k + 1] if k + 1 < len(GROUPS) else ()
+            if k == 1:
+                for u in range(LEAD):
+                    load_hidden_again(u)
 
-        steps = {
-            "setup": setup, "wload": wload, "bload": bload, "bprep": bprep, "wprep": wprep, "load": load,
-            "load2": load2, "tin": tin, "tinq": tinq, "tr": tr, "gate": gate, "ln": ln, "lnb": lnb, "rho": rho, "ars": ars, "sq": sq,
-            "hb": hb, "t1": t1, "t2": t2, "gh": gh, "gm": gm, "gq": gq, "back": back, "backs": backs, "qq": qq,
-        }
-        for step in PLAN:
-            steps[step[0]](*step[1:])
+            blocks = max(len(now), len(before))
+            for i in range(blocks):
+                candidate_and_gating(
+                    before[i] if i < len(before) else None,
+                    now[i - 1] if 1 <= i <= len(now) else None,
+                )
+                if 1 <= i <= len(before):
+                    give_back(before[i - 1])
+                if k == 0 and i == 0:
+                    for u in range(1, LEAD):
+                        bring_in(u)
+                if i < len(now):
+                    tau_and_gate(now[i])
+                if k == 0:
+                    bring_in(now[i] + LEAD)
+
+            for i in range(len(now) + 1 if now else 0):
+                if i < len(now):
+                    softplus(now[i])
+                if i >= 1:
+                    log_tau(now[i - 1])
+            left = now[blocks - 1] if len(now) == blocks else None
+            if left is not None:
+                halve_hidden(left)
+            if k == 0:
+                prepare_weight(CAND, nc.vector.tensor_copy)
+            if before:
+                give_back(before[-1])
+            if left is not None:
+                gate_hidden(left)
+            if after:
+                bring_in(after[0])
+            if left is not None:
+                quantise_gated(left)
+            for u in after[1:]:
+                bring_in(u)

@@ -29,7 +29,7 @@ GROUPS = ((0, 1, 2), (3, 4, 5), (6, 7))
 LEAD = 2
 SCALAR_END = 6
 
-BUFS = {"th": 2, "ht": 3, "xn": 2, "hn": 2, "h2": 2, "xg": 2, "hg": 8, "xc": 8, "hc": 5, "hh": 2, "dg": 2, "dc": 6, "ee": 5, "oo": 4}
+BUFS = {"th": 2, "ht": 3, "xn": 2, "hn": 2, "h2": 2, "xg": 2, "hg": 8, "xc": 8, "hc": 5, "dg": 2, "dc": 6, "ee": 5, "oo": 4}
 
 
 def tile_ltccell_t_kernel(tc, x, hidden, W_tau, b_tau, W_r, b_r, W_h, b_h, out):
@@ -55,7 +55,7 @@ def tile_ltccell_t_kernel(tc, x, hidden, W_tau, b_tau, W_r, b_r, W_h, b_h, out):
         ws = const.tile([P, 3 * WCOL], U8, name="ws", align_bytes=64)
 
         xn, hn, h2, hg, xc, xs, hc, hs = {}, {}, {}, {}, {}, {}, {}, {}
-        dc, ds, th, ee, ht, wn, xg, wg, hh, dg = {}, {}, {}, {}, {}, {}, {}, {}, {}, {}
+        dc, ds, th, ee, ht, wn, xg, wg, dg = {}, {}, {}, {}, {}, {}, {}, {}, {}
 
         def chunk(t):
             return slice(t * NCOL, (t + 1) * NCOL)
@@ -87,6 +87,10 @@ def tile_ltccell_t_kernel(tc, x, hidden, W_tau, b_tau, W_r, b_r, W_h, b_h, out):
             nc.vector.tensor_copy(out=bias[:].rearrange("p (w t) -> p w t", w=3), in_=braw[:, :, 0:PACK])
             gate_bias = bias[:, PACK * GATE : PACK * GATE + PACK]
             nc.vector.tensor_scalar(out=gate_bias, in0=gate_bias, scalar1=0.5, scalar2=None, op0=ALU.mult)
+
+        def halve_hidden_columns():
+            part = wn[CAND][:, :, 256:512]
+            nc.vector.tensor_scalar(out=part, in0=part, scalar1=0.5, scalar2=None, op0=ALU.mult)
 
         def prepare_weight(w, copy_out):
             words = wn[w][:].rearrange("p c k -> p (c k)").bitcast(F32).rearrange("p (c k) -> p c k", c=2)
@@ -178,17 +182,13 @@ def tile_ltccell_t_kernel(tc, x, hidden, W_tau, b_tau, W_r, b_r, W_h, b_h, out):
                 bank = mx_group(GATE, t, hc[u], hs[u], u)
                 nc.scalar.activation(out=th[u][:, chunk(t)], in_=bank[:], func=ACT.Tanh, bias=bias_of(GATE, t), scale=0.5)
 
-        def halve_hidden(u):
-            hh[u] = work.tile([P, UW], BF16, name="hh", tag="hh", bufs=BUFS["hh"])
-            nc.vector.tensor_scalar(out=hh[u][:], in0=hg[u][:].bitcast(BF16), scalar1=0.5, scalar2=None, op0=ALU.mult)
-
         def gate_hidden(u):
             dg[u] = work.tile([P, UW], BF16, name="dg", tag="dg", bufs=BUFS["dg"], align_bytes=64)
             nc.vector.scalar_tensor_tensor(
                 out=dg[u][:].rearrange("p (c t) -> p c t", t=PACK),
                 in0=th[u][:].rearrange("p (t c) -> p c t", t=PACK),
                 scalar=1.0,
-                in1=hh[u][:].rearrange("p (c t) -> p c t", t=PACK),
+                in1=hg[u][:].bitcast(BF16).rearrange("p (c t) -> p c t", t=PACK),
                 op0=ALU.add,
                 op1=ALU.mult,
             )
@@ -222,13 +222,10 @@ def tile_ltccell_t_kernel(tc, x, hidden, W_tau, b_tau, W_r, b_r, W_h, b_h, out):
         def candidate_and_gating(u, g):
             if u is None:
                 if g is not None:
-                    halve_hidden(g)
                     gate_hidden(g)
                     quantise_gated(g)
                 return
             candidate(u)
-            if g is not None:
-                halve_hidden(g)
             subtract_hidden(u, 0)
             if g is not None:
                 gate_hidden(g)
@@ -313,9 +310,8 @@ def tile_ltccell_t_kernel(tc, x, hidden, W_tau, b_tau, W_r, b_r, W_h, b_h, out):
                 if i >= 1:
                     log_tau(now[i - 1])
             left = now[blocks - 1] if len(now) == blocks else None
-            if left is not None:
-                halve_hidden(left)
             if k == 0:
+                halve_hidden_columns()
                 prepare_weight(CAND, nc.vector.tensor_copy)
             if before:
                 give_back(before[-1])

@@ -25,11 +25,9 @@ WCOL = 2 * PACK * P
 EPS = 1e-6
 TAU, GATE, CAND = 0, 1, 2
 
-GROUPS = ((0, 1, 2), (3, 4, 5), (6, 7))
+GROUPS = ((0, 1, 2), (3, 4, 5, 6, 7))
 LEAD = 2
-SCALAR_END = 6
-
-BUFS = {"th": 2, "ht": 3, "xn": 2, "hn": 2, "h2": 2, "xg": 2, "hg": 8, "xc": 8, "hc": 5, "dg": 2, "dc": 6, "ee": 5, "oo": 4}
+BUFS = {"th": 2, "ht": 6, "xh": 2, "h2": 3, "xg": 1, "hg": 8, "xc": 7, "hc": 4, "dg": 2, "dc": 5, "ee": 5, "oo": 1}
 
 
 def tile_ltccell_t_kernel(tc, x, hidden, W_tau, b_tau, W_r, b_r, W_h, b_h, out):
@@ -47,7 +45,7 @@ def tile_ltccell_t_kernel(tc, x, hidden, W_tau, b_tau, W_r, b_r, W_h, b_h, out):
         ctx.enter_context(tc.manual_schedule())
 
         ident = const.tile([P, P], F32, name="ident")
-        identb = const.tile([P, P], BF16, name="identb")
+        negid = const.tile([P, P], BF16, name="negid")
         cst = const.tile([P, 2], F32, name="cst")
         braw = const.tile([P, 3, 16], BF16, name="braw")
         bias = const.tile([P, 3 * PACK], F32, name="bias")
@@ -55,7 +53,7 @@ def tile_ltccell_t_kernel(tc, x, hidden, W_tau, b_tau, W_r, b_r, W_h, b_h, out):
         ws = const.tile([P, 3 * WCOL], U8, name="ws", align_bytes=64)
 
         xn, hn, h2, hg, xc, xs, hc, hs = {}, {}, {}, {}, {}, {}, {}, {}
-        dc, ds, th, ee, ht, wn, xg, wg, dg = {}, {}, {}, {}, {}, {}, {}, {}, {}
+        dc, ds, th, ee, ht, wn, xg, wg, dg, lt = {}, {}, {}, {}, {}, {}, {}, {}, {}, {}
 
         def chunk(t):
             return slice(t * NCOL, (t + 1) * NCOL)
@@ -63,12 +61,15 @@ def tile_ltccell_t_kernel(tc, x, hidden, W_tau, b_tau, W_r, b_r, W_h, b_h, out):
 
         def setup():
             make_identity(nc, ident[:])
-            make_identity(nc, identb[:])
             nc.vector.memset(cst[:, 0:1], 1.0)
             nc.vector.memset(cst[:, 1:2], EPS)
 
+        def prep_negid():
+            make_identity(nc, negid[:])
+            nc.vector.tensor_scalar(out=negid[:], in0=negid[:], scalar1=-1.0, scalar2=None, op0=ALU.mult)
+
         def load_weight(w, zero_engine):
-            wn[w] = work.tile([P, 2, 768], BF16, name="wn", tag="ee", bufs=BUFS["ee"])
+            wn[w] = work.tile([P, 2, 768], BF16, name="wn", tag="h2", bufs=BUFS["h2"])
             src = weights[w].rearrange("(c p) k -> p c k", p=P)
             nc.sync.dma_start(out=wn[w][:, :, 0:512], in_=src)
             nc.sync.dma_start(out=wn[w][:, :, 512:768], in_=src[:, :, 0:256])
@@ -92,7 +93,7 @@ def tile_ltccell_t_kernel(tc, x, hidden, W_tau, b_tau, W_r, b_r, W_h, b_h, out):
             part = wn[CAND][:, :, 256:512]
             nc.vector.tensor_scalar(out=part, in0=part, scalar1=0.5, scalar2=None, op0=ALU.mult)
 
-        def prepare_weight(w, copy_out):
+        def prepare_weight(w, copies):
             words = wn[w][:].rearrange("p c k -> p (c k)").bitcast(F32).rearrange("p (c k) -> p c k", c=2)
             dv = wg[w][:].rearrange("p (t a m u) -> p t a m u", t=PACK, a=2, m=P, u=2)
             for order in range(2):
@@ -106,10 +107,12 @@ def tile_ltccell_t_kernel(tc, x, hidden, W_tau, b_tau, W_r, b_r, W_h, b_h, out):
                     part = (order + half) % 2
                     for c in range(2):
                         m0 = HALF * half + 32 * c
-                        copy_out(
+                        copies[order](
                             out=dv[rows, :, part, m0 : m0 + 32, :],
                             in_=bank[rows, :, c, :].rearrange("p u (q t) -> p t q u", t=PACK),
                         )
+
+        def quant_w(w):
             cols = slice(w * WCOL, (w + 1) * WCOL)
             nc.vector.quantize_mx(out=wc[:, cols].bitcast(FP8X4), scales=ws[:, cols], in_=wg[w][:].bitcast(BF16))
 
@@ -118,10 +121,10 @@ def tile_ltccell_t_kernel(tc, x, hidden, W_tau, b_tau, W_r, b_r, W_h, b_h, out):
             if u >= UNITS:
                 return
             cols = slice(u * UW, (u + 1) * UW)
-            xn[u] = work.tile([P, UW], BF16, name="xn", tag="xn", bufs=BUFS["xn"])
-            nc.sync.dma_start(out=xn[u][:], in_=xv[:, cols])
-            hn[u] = work.tile([P, UW], BF16, name="hn", tag="hn", bufs=BUFS["hn"])
-            nc.sync.dma_start(out=hn[u][:], in_=hv[:, cols])
+            both = work.tile([P, 2, UW], BF16, name="xh", tag="xh", bufs=BUFS["xh"], align_bytes=64)
+            xn[u], hn[u] = both[:, 0, :], both[:, 1, :]
+            nc.sync.dma_start(out=xn[u], in_=xv[:, cols])
+            nc.sync.dma_start(out=hn[u], in_=hv[:, cols])
 
         def load_hidden_again(u):
             if u >= UNITS:
@@ -129,31 +132,40 @@ def tile_ltccell_t_kernel(tc, x, hidden, W_tau, b_tau, W_r, b_r, W_h, b_h, out):
             h2[u] = work.tile([P, UW], BF16, name="h2", tag="h2", bufs=BUFS["h2"])
             nc.sync.dma_start(out=h2[u][:], in_=hv[:, u * UW : (u + 1) * UW])
 
-        def transpose_rows(natural, transposed):
-            sv = natural[:].bitcast(F32).rearrange("p (s m u) -> p s m u", s=PAIRS, m=P, u=2)
+        def transpose_rows(natural, transposed, copy):
+            sv = natural.bitcast(F32).rearrange("p (s m u) -> p s m u", s=PAIRS, m=P, u=2)
             dv = transposed[:].rearrange("p (s m u) -> p s m u", s=PAIRS, m=P, u=2)
+            banks = []
             for s in range(0, PAIRS, 2):
                 bank = psum.tile([P, 2, 2, P], F32, name="tin", tag="bank")
+                banks.append(bank)
                 for s2 in range(2):
                     for u in range(2):
                         nc.tensor.transpose(bank[:, s2, u, :], sv[:, s + s2, :, u], ident[:])
-                nc.vector.tensor_copy(out=dv[:, s : s + 2, :, :], in_=bank[:].rearrange("p s u m -> p s m u"))
+            for s in range(0, PAIRS, 2):
+                copy(out=dv[:, s : s + 2, :, :], in_=banks[s // 2][:].rearrange("p s u m -> p s m u"))
 
-        def bring_in(u):
-            if u >= UNITS or u in xc:
-                return
+        def bring_x(u, copy=nc.vector.tensor_copy):
             xg[u] = work.tile([P, UW // 2], F32, name="xg", tag="xg", bufs=BUFS["xg"], align_bytes=64)
-            hg[u] = work.tile([P, UW // 2], F32, name="hg", tag="hg", bufs=BUFS["hg"], align_bytes=64)
-            transpose_rows(xn[u], xg[u])
-            transpose_rows(hn[u], hg[u])
             xc[u] = work.tile([P, NCOL], U32, name="xc", tag="xc", bufs=BUFS["xc"], align_bytes=64)
             xs[u] = work.tile([P, NCOL], U8, name="xs", tag="xs", bufs=BUFS["xc"], align_bytes=64)
+            transpose_rows(xn[u], xg[u], copy)
+
+        def bring_h(u, copy=nc.vector.tensor_copy):
+            hg[u] = work.tile([P, UW // 2], F32, name="hg", tag="hg", bufs=BUFS["hg"], align_bytes=64)
             hc[u] = work.tile([P, NCOL], U32, name="hc", tag="hc", bufs=BUFS["hc"], align_bytes=64)
             hs[u] = work.tile([P, NCOL], U8, name="hs", tag="hs", bufs=BUFS["hc"], align_bytes=64)
-            nc.vector.quantize_mx(out=xc[u][:].bitcast(FP8X4), scales=xs[u][:], in_=xg[u][:].bitcast(BF16))
-            nc.vector.quantize_mx(out=hc[u][:].bitcast(FP8X4), scales=hs[u][:], in_=hg[u][:].bitcast(BF16))
+            transpose_rows(hn[u], hg[u], copy)
             load_inputs(u + LEAD)
 
+        def quant_x(u):
+            nc.vector.quantize_mx(out=xc[u][:].bitcast(FP8X4), scales=xs[u][:], in_=xg[u][:].bitcast(BF16))
+
+        def quant_h(u):
+            nc.vector.quantize_mx(out=hc[u][:].bitcast(FP8X4), scales=hs[u][:], in_=hg[u][:].bitcast(BF16))
+
+        def bring(u):
+            return [lambda: bring_x(u), (lambda: quant_x(u),), lambda: bring_h(u), (lambda: quant_h(u),)]
 
         def mx_group(w, t, second_codes, second_scales, u):
             bank = psum.tile([P, NCOL], F32, name="mx", tag="bank")
@@ -173,22 +185,31 @@ def tile_ltccell_t_kernel(tc, x, hidden, W_tau, b_tau, W_r, b_r, W_h, b_h, out):
         def bias_of(w, t):
             return bias[:, PACK * w + t : PACK * w + t + 1]
 
-        def tau_and_gate(u):
-            ee[u] = work.tile([P, UW], F32, name="ee", tag="ee", bufs=BUFS["ee"])
-            th[u] = work.tile([P, UW], F32, name="th", tag="th", bufs=BUFS["th"], align_bytes=64)
-            for t in range(PACK):
-                bank = mx_group(TAU, t, hc[u], hs[u], u)
-                nc.scalar.activation(out=ee[u][:, chunk(t)], in_=bank[:], func=ACT.Exp, bias=bias_of(TAU, t), scale=1.0)
-                bank = mx_group(GATE, t, hc[u], hs[u], u)
-                nc.scalar.activation(out=th[u][:, chunk(t)], in_=bank[:], func=ACT.Tanh, bias=bias_of(GATE, t), scale=0.5)
+        def tau_job(u, t):
+            if t == 0:
+                ee[u] = work.tile([P, UW], F32, name="ee", tag="ee", bufs=BUFS["ee"])
+            bank = mx_group(TAU, t, hc[u], hs[u], u)
+            nc.scalar.activation(out=ee[u][:, chunk(t)], in_=bank[:], func=ACT.Exp, bias=bias_of(TAU, t), scale=1.0)
 
-        def gate_hidden(u):
-            dg[u] = work.tile([P, UW], BF16, name="dg", tag="dg", bufs=BUFS["dg"], align_bytes=64)
+        def gate_job(u, t):
+            if t == 0:
+                th[u] = work.tile([P, UW], F32, name="th", tag="th", bufs=BUFS["th"], align_bytes=64)
+            bank = mx_group(GATE, t, hc[u], hs[u], u)
+            nc.scalar.activation(out=th[u][:, chunk(t)], in_=bank[:], func=ACT.Tanh, bias=bias_of(GATE, t), scale=0.5)
+
+        def jobs(f, u, n=PACK):
+            return [(lambda f=f, u=u, t=t: f(u, t)) for t in range(n)]
+
+        def gate_hidden(u, i):
+            if i == 0:
+                dg[u] = work.tile([P, UW], BF16, name="dg", tag="dg", bufs=BUFS["dg"], align_bytes=64)
+            c = slice(i * P, (i + 1) * P)
+            w = slice(i * NCOL, (i + 1) * NCOL)
             nc.vector.scalar_tensor_tensor(
-                out=dg[u][:].rearrange("p (c t) -> p c t", t=PACK),
-                in0=th[u][:].rearrange("p (t c) -> p c t", t=PACK),
+                out=dg[u][:, w].rearrange("p (c t) -> p c t", t=PACK),
+                in0=th[u][:].rearrange("p (t c) -> p c t", t=PACK)[:, c, :],
                 scalar=1.0,
-                in1=hg[u][:].bitcast(BF16).rearrange("p (c t) -> p c t", t=PACK),
+                in1=hg[u][:].bitcast(BF16)[:, w].rearrange("p (c t) -> p c t", t=PACK),
                 op0=ALU.add,
                 op1=ALU.mult,
             )
@@ -198,128 +219,174 @@ def tile_ltccell_t_kernel(tc, x, hidden, W_tau, b_tau, W_r, b_r, W_h, b_h, out):
             ds[u] = work.tile([P, NCOL], U8, name="ds", tag="ds", bufs=BUFS["dc"], align_bytes=64)
             nc.vector.quantize_mx(out=dc[u][:].bitcast(FP8X4), scales=ds[u][:], in_=dg[u][:])
 
+        def gating(u):
+            return jobs(gate_hidden, u) + [(lambda: quantise_gated(u),)]
+
         def softplus(u):
             nc.scalar.activation(out=ee[u][:], in_=ee[u][:], func=ACT.Ln, bias=cst[:, 0:1], scale=1.0)
 
-        def log_tau(u):
-            nc.scalar.activation(out=ee[u][:], in_=ee[u][:], func=ACT.Ln, bias=cst[:, 1:2], scale=1.0)
+        def root_plain(u):
+            nc.scalar.activation(out=ee[u][:], in_=ee[u][:], func=ACT.Abs_reciprocal_sqrt, bias=cst[:, 1:2], scale=1.0)
 
-        def candidate(u):
-            ht[u] = work.tile([P, UW], F32, name="ht", tag="ht", bufs=BUFS["ht"], align_bytes=64)
+        def invert_plain(u):
+            nc.scalar.activation(out=ee[u][:], in_=ee[u][:], func=ACT.Exp, scale=-1.0)
+
+        def root_tau(u, s):
+            if s == 0:
+                lt[u] = work.tile([P, UW], F32, name="lt", tag="th", bufs=BUFS["th"], align_bytes=64)
+            bank = psum.tile([P, PACK, P], F32, name="tl", tag="bank")
             for t in range(PACK):
-                bank = mx_group(CAND, t, dc[u], ds[u], u)
-                nc.scalar.activation(out=ht[u][:, chunk(t)], in_=bank[:], func=ACT.Tanh, bias=bias_of(CAND, t), scale=1.0)
-                nc.scalar.activation(out=ee[u][:, chunk(t)], in_=ee[u][:, chunk(t)], func=ACT.Exp, scale=-1.0)
+                o = t * NCOL + s * P
+                nc.tensor.transpose(bank[:, t, :], ee[u][:, o : o + P], ident[:])
+            nc.scalar.activation(
+                out=lt[u][:, chunk(s)].rearrange("p (m t) -> p m t", t=PACK),
+                in_=bank[:].rearrange("p t m -> p m t"),
+                func=ACT.Abs_reciprocal_sqrt,
+                bias=cst[:, 1:2],
+                scale=1.0,
+            )
 
-        def subtract_hidden(u, t):
+        def square_root(u, s):
+            nc.scalar.activation(out=lt[u][:, chunk(s)], in_=lt[u][:, chunk(s)], func=ACT.Square)
+
+        def cand_job(u, t):
+            if t == 0:
+                tag = "ht" if u < 6 else "xh"
+                ht[u] = work.tile([P, UW], F32, name="ht", tag=tag, bufs=BUFS[tag], align_bytes=64)
+            bank = mx_group(CAND, t, dc[u], ds[u], u)
+            nc.scalar.activation(out=ht[u][:, chunk(t)], in_=bank[:], func=ACT.Tanh, bias=bias_of(CAND, t), scale=1.0)
+
+        def sub(u, t):
             plane = hg[u][:].bitcast(BF16).rearrange("p (c t) -> p t c", t=PACK)[:, t : t + 1, :]
             part = ht[u][:, chunk(t)].rearrange("p (t c) -> p t c", t=1)
             nc.vector.tensor_tensor(out=part, in0=part, in1=plane, op=ALU.subtract)
 
-        def divide_by_tau(u, t):
+        def mul(u, t):
             nc.vector.tensor_tensor(out=ht[u][:, chunk(t)], in0=ht[u][:, chunk(t)], in1=ee[u][:, chunk(t)], op=ALU.mult)
 
-        def candidate_and_gating(u, g):
-            if u is None:
-                if g is not None:
-                    gate_hidden(g)
-                    quantise_gated(g)
-                return
-            candidate(u)
-            subtract_hidden(u, 0)
-            if g is not None:
-                gate_hidden(g)
-            subtract_hidden(u, 1)
-            divide_by_tau(u, 0)
-            if g is not None:
-                quantise_gated(g)
-            for t in range(2, PACK):
-                subtract_hidden(u, t)
-                divide_by_tau(u, t - 1)
-            divide_by_tau(u, PACK - 1)
-
-
-        def give_back(u):
-            for s in range(PAIRS):
+        def give_back(u, s0):
+            banks = []
+            for s in (s0, s0 + 1):
                 bank = psum.tile([P, PACK, P], F32, name="tb", tag="bank")
-                again = h2[u][:, chunk(s)]
-                result = work.tile([P, NCOL], F32, name="oo", tag="oo", bufs=BUFS["oo"])
-                if u == SCALAR_END:
-                    planes = again.rearrange("p (m t) -> p t m", t=PACK)
-                    for t in range(PACK):
-                        o = t * NCOL + s * P
-                        nc.tensor.matmul(out=bank[:, t, :], lhsT=identb[:], rhs=planes[:, t, :], start=True, stop=False)
-                        nc.tensor.matmul(
-                            out=bank[:, t, :], lhsT=ht[u][:, o : o + P], rhs=ident[:], is_transpose=True, start=False, stop=True
-                        )
-                    nc.scalar.copy(out=result[:].rearrange("p (m t) -> p m t", t=PACK), in_=bank[:].rearrange("p t m -> p m t"))
-                else:
-                    for t in range(PACK):
-                        o = t * NCOL + s * P
-                        nc.tensor.transpose(bank[:, t, :], ht[u][:, o : o + P], ident[:])
-                    nc.vector.tensor_tensor(
-                        out=result[:].rearrange("p (m t) -> p m t", t=PACK),
-                        in0=bank[:].rearrange("p t m -> p m t"),
-                        in1=again.rearrange("p (m t) -> p m t", t=PACK),
-                        op=ALU.add,
-                    )
-                o = u * UW + s * NCOL
-                nc.sync.dma_start(out=ov[:, o : o + NCOL], in_=result[:])
-            load_hidden_again(u + LEAD)
+                banks.append(bank)
+                for t in range(PACK):
+                    o = t * NCOL + s * P
+                    nc.tensor.transpose(bank[:, t, :], ht[u][:, o : o + P], ident[:])
+            result = work.tile([P, 2 * NCOL], F32, name="oo", tag="hg", bufs=BUFS["hg"], align_bytes=64)
+            for i in range(2):
+                w = slice(i * NCOL, (i + 1) * NCOL)
+                nc.vector.tensor_tensor(
+                    out=result[:, w].rearrange("p (m t) -> p m t", t=PACK),
+                    in0=banks[i][:].rearrange("p t m -> p m t"),
+                    in1=h2[u][:, chunk(s0 + i)].rearrange("p (m t) -> p m t", t=PACK),
+                    op=ALU.add,
+                )
+            o = u * UW + s0 * NCOL
+            nc.sync.dma_start(out=ov[:, o : o + 2 * NCOL], in_=result[:])
+            if s0 + 2 == PAIRS:
+                load_hidden_again(u + 3)
+
+        def difference(u, s):
+            bank = psum.tile([P, PACK, P], F32, name="tb", tag="bank")
+            planes = h2[u][:, chunk(s)].rearrange("p (m t) -> p t m", t=PACK)
+            for t in range(PACK):
+                o = t * NCOL + s * P
+                nc.tensor.matmul(out=bank[:, t, :], lhsT=negid[:], rhs=planes[:, t, :], start=True, stop=False)
+                nc.tensor.matmul(
+                    out=bank[:, t, :], lhsT=ht[u][:, o : o + P], rhs=ident[:], is_transpose=True, start=False, stop=True
+                )
+            part = lt[u][:, chunk(s)].rearrange("p (m t) -> p m t", t=PACK)
+            nc.vector.tensor_tensor(out=part, in0=bank[:].rearrange("p t m -> p m t"), in1=part, op=ALU.mult)
+
+        def add_store(u, s0, n):
+            w = slice(s0 * NCOL, (s0 + n) * NCOL)
+            nc.vector.tensor_tensor(out=lt[u][:, w], in0=lt[u][:, w], in1=h2[u][:, w], op=ALU.add)
+            o = u * UW
+            nc.sync.dma_start(out=ov[:, o + s0 * NCOL : o + (s0 + n) * NCOL], in_=lt[u][:, w])
+            if s0 + n == PAIRS:
+                load_hidden_again(u + 3)
+
+        late = []
+
+        def run(f):
+            if isinstance(f, tuple):
+                late.append(f[0])
+                return
+            f()
+            for g in late:
+                g()
+            late.clear()
+
+        def weave(main, side):
+            done = 0
+            for i, f in enumerate(main):
+                f()
+                upto = (i + 1) * len(side) // len(main)
+                for g in side[done:upto]:
+                    run(g)
+                done = upto
+            run(lambda: None)
 
 
         setup()
         load_weight(TAU, nc.vector)
         load_inputs(0)
-        load_weight(GATE, nc.vector)
         load_biases()
-        load_inputs(1)
+        load_weight(GATE, nc.gpsimd)
         load_weight(CAND, nc.gpsimd)
-        prepare_weight(TAU, nc.scalar.copy)
-        bring_in(0)
+        load_inputs(1)
+        S, V = nc.scalar.copy, nc.vector.tensor_copy
+        G1, G2 = GROUPS
+        def nslot(u):
+            return jobs(tau_job, u) + jobs(gate_job, u)
+        def cslot(u):
+            return jobs(cand_job, u)
+        def fin1(u):
+            return [lambda: sub(u, 0), lambda: sub(u, 1), lambda: mul(u, 0), lambda: sub(u, 2), lambda: mul(u, 1), lambda: mul(u, 0), lambda: sub(u, 3), lambda: mul(u, 2), lambda: mul(u, 1), lambda: mul(u, 3), lambda: mul(u, 2), lambda: mul(u, 3)]
+        def fin2(u):
+            return [lambda: give_back(u, 0), lambda: give_back(u, 2)]
+        prepare_weight(TAU, (S, V))
         prepare_biases()
-        prepare_weight(GATE, nc.scalar.copy)
+        bring_x(0, S)
+        quant_w(TAU)
+        bring_h(0, S)
+        quant_x(0)
+        quant_h(0)
+        prepare_weight(GATE, (S, V))
+        weave(jobs(tau_job, 0), [lambda: quant_w(GATE)] + bring(1)[:2])
+        weave(jobs(gate_job, 0), bring(1)[2:])
+        halve_hidden_columns()
+        prep_negid()
+        prepare_weight(CAND, (S, S))
+        for u in range(3):
+            load_hidden_again(u)
+        weave(nslot(1), bring(2) + gating(0))
+        weave(nslot(2), gating(1))
+        main = [lambda u=u: softplus(u) for u in G1] + [lambda u=u: root_plain(u) for u in G1]
 
-        for k in range(len(GROUPS) + 1):
-            now = GROUPS[k] if k < len(GROUPS) else ()
-            before = GROUPS[k - 1] if k > 0 else ()
-            after = GROUPS[k + 1] if k + 1 < len(GROUPS) else ()
-            if k == 1:
-                for u in range(LEAD):
-                    load_hidden_again(u)
+        weave(main, bring(3) + [lambda: quant_w(CAND)] + bring(4) + bring(5) + bring(6))
+        weave(cslot(0), gating(G1[-1]))
+        weave(nslot(3), fin1(0) + bring(7))
+        weave(cslot(1), gating(3))
+        weave(nslot(4), fin1(1))
+        weave(cslot(2), gating(4))
+        weave(nslot(5), fin1(2))
+        weave(nslot(6), gating(5))
+        weave(jobs(cand_job, 3) + jobs(cand_job, 4), gating(6))
+        weave(nslot(7), [])
+        weave(jobs(cand_job, 5), gating(7))
+        weave(jobs(cand_job, 6), [])
+        weave(jobs(cand_job, 7), [])
 
-            blocks = max(len(now), len(before))
-            for i in range(blocks):
-                candidate_and_gating(
-                    before[i] if i < len(before) else None,
-                    now[i - 1] if 1 <= i <= len(now) else None,
-                )
-                if 1 <= i <= len(before):
-                    give_back(before[i - 1])
-                if k == 0 and i == 0:
-                    for u in range(1, LEAD):
-                        bring_in(u)
-                if i < len(now):
-                    tau_and_gate(now[i])
-                if k == 0:
-                    bring_in(now[i] + LEAD)
 
-            for i in range(len(now) + 1 if now else 0):
-                if i < len(now):
-                    softplus(now[i])
-                if i >= 1:
-                    log_tau(now[i - 1])
-            left = now[blocks - 1] if len(now) == blocks else None
-            if k == 0:
-                halve_hidden_columns()
-                prepare_weight(CAND, nc.vector.tensor_copy)
-            if before:
-                give_back(before[-1])
-            if left is not None:
-                gate_hidden(left)
-            if after:
-                bring_in(after[0])
-            if left is not None:
-                quantise_gated(left)
-            for u in after[1:]:
-                bring_in(u)
+        weave([lambda u=u: softplus(u) for u in G2], fin2(0) + fin2(1) + fin2(2))
+        steps = [(u, s) for u in G2 for s in range(PAIRS)]
+        for i in range(len(steps) + 3):
+            if i < len(steps):
+                root_tau(*steps[i])
+            if 1 <= i <= len(steps):
+                square_root(*steps[i - 1])
+            if 2 <= i <= len(steps) + 1:
+                difference(*steps[i - 2])
+            if i >= 3:
+                add_store(*steps[i - 3], 1)

@@ -231,23 +231,26 @@ def tile_ltccell_t_kernel(tc, x, hidden, W_tau, b_tau, W_r, b_r, W_h, b_h, out):
         def invert_plain(u):
             nc.scalar.activation(out=ee[u][:], in_=ee[u][:], func=ACT.Exp, scale=-1.0)
 
-        def root_tau(u, s):
-            if s == 0:
-                lt[u] = work.tile([P, UW], F32, name="lt", tag="th", bufs=BUFS["th"], align_bytes=64)
-            bank = psum.tile([P, PACK, P], F32, name="tl", tag="bank")
-            for t in range(PACK):
-                o = t * NCOL + s * P
-                nc.tensor.transpose(bank[:, t, :], ee[u][:, o : o + P], ident[:])
-            nc.scalar.activation(
-                out=lt[u][:, chunk(s)].rearrange("p (m t) -> p m t", t=PACK),
-                in_=bank[:].rearrange("p t m -> p m t"),
-                func=ACT.Abs_reciprocal_sqrt,
-                bias=cst[:, 1:2],
-                scale=1.0,
-            )
-
-        def square_root(u, s):
-            nc.scalar.activation(out=lt[u][:, chunk(s)], in_=lt[u][:, chunk(s)], func=ACT.Square)
+        def root_tau(u, s0):
+            if s0 == 0:
+                lt[u] = work.tile([P, UW], F32, name="lt", tag="ht", bufs=BUFS["ht"], align_bytes=64)
+            banks = []
+            for s in (s0, s0 + 1):
+                bank = psum.tile([P, PACK, P], F32, name="tl", tag="bank")
+                banks.append(bank)
+                for t in range(PACK):
+                    o = t * NCOL + s * P
+                    nc.tensor.transpose(bank[:, t, :], ee[u][:, o : o + P], ident[:])
+            for i in range(2):
+                nc.scalar.activation(
+                    out=lt[u][:, chunk(s0 + i)].rearrange("p (m t) -> p m t", t=PACK),
+                    in_=banks[i][:].rearrange("p t m -> p m t"),
+                    func=ACT.Abs_reciprocal_sqrt,
+                    bias=cst[:, 1:2],
+                    scale=1.0,
+                )
+            for s in (s0, s0 + 1):
+                nc.scalar.activation(out=lt[u][:, chunk(s)], in_=lt[u][:, chunk(s)], func=ACT.Square)
 
         def cand_job(u, t):
             if t == 0:
@@ -286,24 +289,33 @@ def tile_ltccell_t_kernel(tc, x, hidden, W_tau, b_tau, W_r, b_r, W_h, b_h, out):
             if s0 + 2 == PAIRS:
                 load_hidden_again(u + 3)
 
-        def difference(u, s):
-            bank = psum.tile([P, PACK, P], F32, name="tb", tag="bank")
-            planes = h2[u][:, chunk(s)].rearrange("p (m t) -> p t m", t=PACK)
-            for t in range(PACK):
-                o = t * NCOL + s * P
-                nc.tensor.matmul(out=bank[:, t, :], lhsT=negid[:], rhs=planes[:, t, :], start=True, stop=False)
+        def finish(u, s0):
+            banks = []
+            for s in (s0, s0 + 1):
+                bank = psum.tile([P, PACK, P], F32, name="td", tag="bank")
+                banks.append(bank)
                 nc.tensor.matmul(
-                    out=bank[:, t, :], lhsT=ht[u][:, o : o + P], rhs=ident[:], is_transpose=True, start=False, stop=True
+                    out=bank[:],
+                    lhsT=negid[:],
+                    rhs=h2[u][:, chunk(s)].rearrange("p (m t) -> p t m", t=PACK),
+                    start=True,
+                    stop=False,
                 )
-            part = lt[u][:, chunk(s)].rearrange("p (m t) -> p m t", t=PACK)
-            nc.vector.tensor_tensor(out=part, in0=bank[:].rearrange("p t m -> p m t"), in1=part, op=ALU.mult)
-
-        def add_store(u, s0, n):
-            w = slice(s0 * NCOL, (s0 + n) * NCOL)
-            nc.vector.tensor_tensor(out=lt[u][:, w], in0=lt[u][:, w], in1=h2[u][:, w], op=ALU.add)
-            o = u * UW
-            nc.sync.dma_start(out=ov[:, o + s0 * NCOL : o + (s0 + n) * NCOL], in_=lt[u][:, w])
-            if s0 + n == PAIRS:
+            for i in range(2):
+                for t in range(PACK):
+                    o = t * NCOL + (s0 + i) * P
+                    nc.tensor.matmul(
+                        out=banks[i][:, t, :], lhsT=ht[u][:, o : o + P], rhs=ident[:], is_transpose=True, start=False, stop=(t == PACK - 1)
+                    )
+            for i in range(2):
+                part = lt[u][:, chunk(s0 + i)].rearrange("p (m t) -> p m t", t=PACK)
+                nc.vector.tensor_tensor(out=part, in0=banks[i][:].rearrange("p t m -> p m t"), in1=part, op=ALU.mult)
+            for i in range(2):
+                w = chunk(s0 + i)
+                nc.vector.tensor_tensor(out=lt[u][:, w], in0=lt[u][:, w], in1=h2[u][:, w], op=ALU.add)
+            o = u * UW + s0 * NCOL
+            nc.sync.dma_start(out=ov[:, o : o + 2 * NCOL], in_=lt[u][:, s0 * NCOL : (s0 + 2) * NCOL])
+            if s0 + 2 == PAIRS:
                 load_hidden_again(u + 3)
 
         late = []
@@ -380,13 +392,9 @@ def tile_ltccell_t_kernel(tc, x, hidden, W_tau, b_tau, W_r, b_r, W_h, b_h, out):
 
 
         weave([lambda u=u: softplus(u) for u in G2], fin2(0) + fin2(1) + fin2(2))
-        steps = [(u, s) for u in G2 for s in range(PAIRS)]
-        for i in range(len(steps) + 3):
-            if i < len(steps):
-                root_tau(*steps[i])
-            if 1 <= i <= len(steps):
-                square_root(*steps[i - 1])
-            if 2 <= i <= len(steps) + 1:
-                difference(*steps[i - 2])
-            if i >= 3:
-                add_store(*steps[i - 3], 1)
+        steps = [(u, s0) for u in G2 for s0 in (0, 2)]
+        root_tau(*steps[0])
+        for i in range(len(steps)):
+            if i + 1 < len(steps):
+                root_tau(*steps[i + 1])
+            finish(*steps[i])

@@ -27,7 +27,7 @@ TAU, GATE, CAND = 0, 1, 2
 
 GROUPS = ((0, 1, 2), (3, 4, 5, 6, 7))
 LEAD = 2
-BUFS = {"th": 2, "ht": 6, "xh": 2, "h2": 3, "xg": 1, "hg": 8, "xc": 7, "hc": 4, "dg": 2, "dc": 5, "ee": 5, "oo": 1}
+BUFS = {"th": 2, "ht": 6, "xh": 2, "h2": 3, "xg": 1, "hg": 8, "xc": 7, "hc": 4, "dg": 1, "dc": 5, "ee": 6}
 
 
 def tile_ltccell_t_kernel(tc, x, hidden, W_tau, b_tau, W_r, b_r, W_h, b_h, out):
@@ -54,6 +54,7 @@ def tile_ltccell_t_kernel(tc, x, hidden, W_tau, b_tau, W_r, b_r, W_h, b_h, out):
 
         xn, hn, h2, hg, xc, xs, hc, hs = {}, {}, {}, {}, {}, {}, {}, {}
         dc, ds, th, ee, ht, wn, xg, wg, dg, lt = {}, {}, {}, {}, {}, {}, {}, {}, {}, {}
+        tau_bank, diff_bank = {}, {}
 
         def chunk(t):
             return slice(t * NCOL, (t + 1) * NCOL)
@@ -66,7 +67,7 @@ def tile_ltccell_t_kernel(tc, x, hidden, W_tau, b_tau, W_r, b_r, W_h, b_h, out):
 
         def prep_negid():
             make_identity(nc, negid[:])
-            nc.vector.tensor_scalar(out=negid[:], in0=negid[:], scalar1=-1.0, scalar2=None, op0=ALU.mult)
+            nc.gpsimd.tensor_scalar(out=negid[:], in0=negid[:], scalar1=-1.0, scalar2=0.0, op0=ALU.mult, op1=ALU.add)
 
         def load_weight(w, zero_engine):
             wn[w] = work.tile([P, 2, 768], BF16, name="wn", tag="h2", bufs=BUFS["h2"])
@@ -91,7 +92,7 @@ def tile_ltccell_t_kernel(tc, x, hidden, W_tau, b_tau, W_r, b_r, W_h, b_h, out):
 
         def halve_hidden_columns():
             part = wn[CAND][:, :, 256:512]
-            nc.vector.tensor_scalar(out=part, in0=part, scalar1=0.5, scalar2=None, op0=ALU.mult)
+            nc.gpsimd.tensor_scalar(out=part, in0=part, scalar1=0.5, scalar2=0.0, op0=ALU.mult, op1=ALU.add)
 
         def prepare_weight(w, copies):
             words = wn[w][:].rearrange("p c k -> p (c k)").bitcast(F32).rearrange("p (c k) -> p c k", c=2)
@@ -203,13 +204,12 @@ def tile_ltccell_t_kernel(tc, x, hidden, W_tau, b_tau, W_r, b_r, W_h, b_h, out):
         def gate_hidden(u, i):
             if i == 0:
                 dg[u] = work.tile([P, UW], BF16, name="dg", tag="dg", bufs=BUFS["dg"], align_bytes=64)
-            c = slice(i * P, (i + 1) * P)
-            w = slice(i * NCOL, (i + 1) * NCOL)
+            c = slice(i * 2 * P, (i + 1) * 2 * P)
             nc.vector.scalar_tensor_tensor(
-                out=dg[u][:, w].rearrange("p (c t) -> p c t", t=PACK),
+                out=dg[u][:].rearrange("p (c t) -> p c t", t=PACK)[:, c, :],
                 in0=th[u][:].rearrange("p (t c) -> p c t", t=PACK)[:, c, :],
                 scalar=1.0,
-                in1=hg[u][:].bitcast(BF16)[:, w].rearrange("p (c t) -> p c t", t=PACK),
+                in1=hg[u][:].bitcast(BF16).rearrange("p (c t) -> p c t", t=PACK)[:, c, :],
                 op0=ALU.add,
                 op1=ALU.mult,
             )
@@ -220,7 +220,7 @@ def tile_ltccell_t_kernel(tc, x, hidden, W_tau, b_tau, W_r, b_r, W_h, b_h, out):
             nc.vector.quantize_mx(out=dc[u][:].bitcast(FP8X4), scales=ds[u][:], in_=dg[u][:])
 
         def gating(u):
-            return jobs(gate_hidden, u) + [(lambda: quantise_gated(u),)]
+            return jobs(gate_hidden, u, 2) + [(lambda: quantise_gated(u),)]
 
         def softplus(u):
             nc.scalar.activation(out=ee[u][:], in_=ee[u][:], func=ACT.Ln, bias=cst[:, 0:1], scale=1.0)
@@ -231,20 +231,22 @@ def tile_ltccell_t_kernel(tc, x, hidden, W_tau, b_tau, W_r, b_r, W_h, b_h, out):
         def invert_plain(u):
             nc.scalar.activation(out=ee[u][:], in_=ee[u][:], func=ACT.Exp, scale=-1.0)
 
-        def root_tau(u, s0):
-            if s0 == 0:
-                lt[u] = work.tile([P, UW], F32, name="lt", tag="ht", bufs=BUFS["ht"], align_bytes=64)
-            banks = []
+
+        def turn_tau(u, s0):
             for s in (s0, s0 + 1):
                 bank = psum.tile([P, PACK, P], F32, name="tl", tag="bank")
-                banks.append(bank)
+                tau_bank[u, s] = bank
                 for t in range(PACK):
                     o = t * NCOL + s * P
                     nc.tensor.transpose(bank[:, t, :], ee[u][:, o : o + P], ident[:])
-            for i in range(2):
+
+        def invert_tau(u, s0):
+            if s0 == 0:
+                lt[u] = work.tile([P, UW], F32, name="lt", tag="ht", bufs=BUFS["ht"], align_bytes=64)
+            for s in (s0, s0 + 1):
                 nc.scalar.activation(
-                    out=lt[u][:, chunk(s0 + i)].rearrange("p (m t) -> p m t", t=PACK),
-                    in_=banks[i][:].rearrange("p t m -> p m t"),
+                    out=lt[u][:, chunk(s)].rearrange("p (m t) -> p m t", t=PACK),
+                    in_=tau_bank[u, s][:].rearrange("p t m -> p m t"),
                     func=ACT.Abs_reciprocal_sqrt,
                     bias=cst[:, 1:2],
                     scale=1.0,
@@ -259,13 +261,14 @@ def tile_ltccell_t_kernel(tc, x, hidden, W_tau, b_tau, W_r, b_r, W_h, b_h, out):
             bank = mx_group(CAND, t, dc[u], ds[u], u)
             nc.scalar.activation(out=ht[u][:, chunk(t)], in_=bank[:], func=ACT.Tanh, bias=bias_of(CAND, t), scale=1.0)
 
-        def sub(u, t):
-            plane = hg[u][:].bitcast(BF16).rearrange("p (c t) -> p t c", t=PACK)[:, t : t + 1, :]
-            part = ht[u][:, chunk(t)].rearrange("p (t c) -> p t c", t=1)
-            nc.vector.tensor_tensor(out=part, in0=part, in1=plane, op=ALU.subtract)
+        def sub(u, i):
+            planes = hg[u][:].bitcast(BF16).rearrange("p (c t) -> p t c", t=PACK)[:, 2 * i : 2 * i + 2, :]
+            part = ht[u][:].rearrange("p (t c) -> p t c", t=PACK)[:, 2 * i : 2 * i + 2, :]
+            nc.vector.tensor_tensor(out=part, in0=part, in1=planes, op=ALU.subtract)
 
-        def mul(u, t):
-            nc.vector.tensor_tensor(out=ht[u][:, chunk(t)], in0=ht[u][:, chunk(t)], in1=ee[u][:, chunk(t)], op=ALU.mult)
+        def mul(u, i):
+            w = slice(i * 2 * NCOL, (i + 1) * 2 * NCOL)
+            nc.vector.tensor_tensor(out=ht[u][:, w], in0=ht[u][:, w], in1=ee[u][:, w], op=ALU.mult)
 
         def give_back(u, s0):
             banks = []
@@ -289,11 +292,10 @@ def tile_ltccell_t_kernel(tc, x, hidden, W_tau, b_tau, W_r, b_r, W_h, b_h, out):
             if s0 + 2 == PAIRS:
                 load_hidden_again(u + 3)
 
-        def finish(u, s0):
-            banks = []
+        def difference(u, s0):
             for s in (s0, s0 + 1):
                 bank = psum.tile([P, PACK, P], F32, name="td", tag="bank")
-                banks.append(bank)
+                diff_bank[u, s] = bank
                 nc.tensor.matmul(
                     out=bank[:],
                     lhsT=negid[:],
@@ -301,17 +303,24 @@ def tile_ltccell_t_kernel(tc, x, hidden, W_tau, b_tau, W_r, b_r, W_h, b_h, out):
                     start=True,
                     stop=False,
                 )
-            for i in range(2):
+            for s in (s0, s0 + 1):
                 for t in range(PACK):
-                    o = t * NCOL + (s0 + i) * P
+                    o = t * NCOL + s * P
                     nc.tensor.matmul(
-                        out=banks[i][:, t, :], lhsT=ht[u][:, o : o + P], rhs=ident[:], is_transpose=True, start=False, stop=(t == PACK - 1)
+                        out=diff_bank[u, s][:, t, :],
+                        lhsT=ht[u][:, o : o + P],
+                        rhs=ident[:],
+                        is_transpose=True,
+                        start=False,
+                        stop=(t == PACK - 1),
                     )
-            for i in range(2):
-                part = lt[u][:, chunk(s0 + i)].rearrange("p (m t) -> p m t", t=PACK)
-                nc.vector.tensor_tensor(out=part, in0=banks[i][:].rearrange("p t m -> p m t"), in1=part, op=ALU.mult)
-            for i in range(2):
-                w = chunk(s0 + i)
+
+        def finish(u, s0):
+            for s in (s0, s0 + 1):
+                part = lt[u][:, chunk(s)].rearrange("p (m t) -> p m t", t=PACK)
+                nc.vector.tensor_tensor(out=part, in0=diff_bank[u, s][:].rearrange("p t m -> p m t"), in1=part, op=ALU.mult)
+            for s in (s0, s0 + 1):
+                w = chunk(s)
                 nc.vector.tensor_tensor(out=lt[u][:, w], in0=lt[u][:, w], in1=h2[u][:, w], op=ALU.add)
             o = u * UW + s0 * NCOL
             nc.sync.dma_start(out=ov[:, o : o + 2 * NCOL], in_=lt[u][:, s0 * NCOL : (s0 + 2) * NCOL])
@@ -347,6 +356,8 @@ def tile_ltccell_t_kernel(tc, x, hidden, W_tau, b_tau, W_r, b_r, W_h, b_h, out):
         load_weight(GATE, nc.gpsimd)
         load_weight(CAND, nc.gpsimd)
         load_inputs(1)
+        halve_hidden_columns()
+        prep_negid()
         S, V = nc.scalar.copy, nc.vector.tensor_copy
         G1, G2 = GROUPS
         def nslot(u):
@@ -354,7 +365,7 @@ def tile_ltccell_t_kernel(tc, x, hidden, W_tau, b_tau, W_r, b_r, W_h, b_h, out):
         def cslot(u):
             return jobs(cand_job, u)
         def fin1(u):
-            return [lambda: sub(u, 0), lambda: sub(u, 1), lambda: mul(u, 0), lambda: sub(u, 2), lambda: mul(u, 1), lambda: mul(u, 0), lambda: sub(u, 3), lambda: mul(u, 2), lambda: mul(u, 1), lambda: mul(u, 3), lambda: mul(u, 2), lambda: mul(u, 3)]
+            return [lambda: sub(u, 0), lambda: sub(u, 1), lambda: mul(u, 0), lambda: mul(u, 1), lambda: mul(u, 0), lambda: mul(u, 1)]
         def fin2(u):
             return [lambda: give_back(u, 0), lambda: give_back(u, 2)]
         prepare_weight(TAU, (S, V))
@@ -367,8 +378,6 @@ def tile_ltccell_t_kernel(tc, x, hidden, W_tau, b_tau, W_r, b_r, W_h, b_h, out):
         prepare_weight(GATE, (S, V))
         weave(jobs(tau_job, 0), [lambda: quant_w(GATE)] + bring(1)[:2])
         weave(jobs(gate_job, 0), bring(1)[2:])
-        halve_hidden_columns()
-        prep_negid()
         prepare_weight(CAND, (S, S))
         for u in range(3):
             load_hidden_again(u)
@@ -377,24 +386,27 @@ def tile_ltccell_t_kernel(tc, x, hidden, W_tau, b_tau, W_r, b_r, W_h, b_h, out):
         main = [lambda u=u: softplus(u) for u in G1] + [lambda u=u: root_plain(u) for u in G1]
 
         weave(main, bring(3) + [lambda: quant_w(CAND)] + bring(4) + bring(5) + bring(6))
-        weave(cslot(0), gating(G1[-1]))
-        weave(nslot(3), fin1(0) + bring(7))
-        weave(cslot(1), gating(3))
-        weave(nslot(4), fin1(1))
-        weave(cslot(2), gating(4))
-        weave(nslot(5), fin1(2))
-        weave(nslot(6), gating(5))
+        weave(cslot(0), gating(2))
+        weave(nslot(3), [])
+        weave(cslot(1), fin1(0))
+        weave(nslot(4), gating(3) + fin1(1)[:2])
+        weave(cslot(2), fin1(1)[2:])
+        weave(nslot(5), gating(4) + bring(7)[:2])
+        weave(nslot(6), bring(7)[2:] + gating(5))
         weave(jobs(cand_job, 3) + jobs(cand_job, 4), gating(6))
         weave(nslot(7), [])
         weave(jobs(cand_job, 5), gating(7))
         weave(jobs(cand_job, 6), [])
         weave(jobs(cand_job, 7), [])
 
-
-        weave([lambda u=u: softplus(u) for u in G2], fin2(0) + fin2(1) + fin2(2))
+        weave([lambda u=u: softplus(u) for u in G2], fin2(0) + fin1(2) + fin2(1) + fin2(2))
         steps = [(u, s0) for u in G2 for s0 in (0, 2)]
-        root_tau(*steps[0])
+        for i in range(2):
+            turn_tau(*steps[i])
+            difference(*steps[i])
         for i in range(len(steps)):
-            if i + 1 < len(steps):
-                root_tau(*steps[i + 1])
+            invert_tau(*steps[i])
             finish(*steps[i])
+            if i + 2 < len(steps):
+                turn_tau(*steps[i + 2])
+                difference(*steps[i + 2])

@@ -18,15 +18,17 @@ B, I, H = 8192, 256, 256
 FLOPS = 3 * 2 * B * (I + H) * H
 ROWS = B // P
 UNITS = 8
-PAIRS = ROWS // UNITS // 2
+UROWS = ROWS // UNITS
+PAIRS = UROWS // 2
 NCOL = PAIRS * P
 UW = PACK * NCOL
 WCOL = 2 * PACK * P
 EPS = 1e-6
 TAU, GATE, CAND = 0, 1, 2
-
-GROUPS = ((0, 1, 2), (3, 4, 5, 6, 7))
+FIRST, SECOND = (0, 1, 2), (3, 4, 5, 6, 7)
 LEAD = 2
+AGAIN = 3
+
 BUFS = {"th": 2, "ht": 6, "xh": 2, "h2": 3, "xg": 1, "hg": 8, "xc": 7, "hc": 4, "dg": 1, "dc": 5, "ee": 6}
 
 
@@ -37,6 +39,7 @@ def tile_ltccell_t_kernel(tc, x, hidden, W_tau, b_tau, W_r, b_r, W_h, b_h, out):
     ov = out.rearrange("(p q) k -> p (q k)", q=ROWS)
     weights = (W_tau, W_r, W_h)
     biases = (b_tau, b_r, b_h)
+    on_scalar, on_vector = nc.scalar.copy, nc.vector.tensor_copy
 
     with ExitStack() as ctx:
         const = ctx.enter_context(tc.tile_pool(name="const", bufs=1))
@@ -46,28 +49,18 @@ def tile_ltccell_t_kernel(tc, x, hidden, W_tau, b_tau, W_r, b_r, W_h, b_h, out):
 
         ident = const.tile([P, P], F32, name="ident")
         negid = const.tile([P, P], BF16, name="negid")
-        cst = const.tile([P, 2], F32, name="cst")
         braw = const.tile([P, 3, 16], BF16, name="braw")
         bias = const.tile([P, 3 * PACK], F32, name="bias")
         wc = const.tile([P, 3 * WCOL], U32, name="wc", align_bytes=64)
         ws = const.tile([P, 3 * WCOL], U8, name="ws", align_bytes=64)
 
-        xn, hn, h2, hg, xc, xs, hc, hs = {}, {}, {}, {}, {}, {}, {}, {}
-        dc, ds, th, ee, ht, wn, xg, wg, dg, lt = {}, {}, {}, {}, {}, {}, {}, {}, {}, {}
+        xn, hn, h2, xg, hg, xc, xs, hc, hs, dc, ds = {}, {}, {}, {}, {}, {}, {}, {}, {}, {}, {}
+        wn, wg, th, dg, ee, ht, lt = {}, {}, {}, {}, {}, {}, {}
         tau_bank, diff_bank = {}, {}
 
         def chunk(t):
             return slice(t * NCOL, (t + 1) * NCOL)
 
-
-        def setup():
-            make_identity(nc, ident[:])
-            nc.vector.memset(cst[:, 0:1], 1.0)
-            nc.vector.memset(cst[:, 1:2], EPS)
-
-        def prep_negid():
-            make_identity(nc, negid[:])
-            nc.gpsimd.tensor_scalar(out=negid[:], in0=negid[:], scalar1=-1.0, scalar2=0.0, op0=ALU.mult, op1=ALU.add)
 
         def load_weight(w, zero_engine):
             wn[w] = work.tile([P, 2, 768], BF16, name="wn", tag="h2", bufs=BUFS["h2"])
@@ -94,6 +87,10 @@ def tile_ltccell_t_kernel(tc, x, hidden, W_tau, b_tau, W_r, b_r, W_h, b_h, out):
             part = wn[CAND][:, :, 256:512]
             nc.gpsimd.tensor_scalar(out=part, in0=part, scalar1=0.5, scalar2=0.0, op0=ALU.mult, op1=ALU.add)
 
+        def negate_identity():
+            make_identity(nc, negid[:])
+            nc.gpsimd.tensor_scalar(out=negid[:], in0=negid[:], scalar1=-1.0, scalar2=0.0, op0=ALU.mult, op1=ALU.add)
+
         def prepare_weight(w, copies):
             words = wn[w][:].rearrange("p c k -> p (c k)").bitcast(F32).rearrange("p (c k) -> p c k", c=2)
             dv = wg[w][:].rearrange("p (t a m u) -> p t a m u", t=PACK, a=2, m=P, u=2)
@@ -113,71 +110,87 @@ def tile_ltccell_t_kernel(tc, x, hidden, W_tau, b_tau, W_r, b_r, W_h, b_h, out):
                             in_=bank[rows, :, c, :].rearrange("p u (q t) -> p t q u", t=PACK),
                         )
 
-        def quant_w(w):
-            cols = slice(w * WCOL, (w + 1) * WCOL)
-            nc.vector.quantize_mx(out=wc[:, cols].bitcast(FP8X4), scales=ws[:, cols], in_=wg[w][:].bitcast(BF16))
+        def quantise_weight(w, t0=0, t1=PACK):
+            c0, c1 = 2 * P * t0, 2 * P * t1
+            cols = slice(w * WCOL + c0, w * WCOL + c1)
+            nc.vector.quantize_mx(
+                out=wc[:, cols].bitcast(FP8X4), scales=ws[:, cols], in_=wg[w][:].bitcast(BF16)[:, PACK * c0 : PACK * c1]
+            )
 
 
-        def load_inputs(u):
-            if u >= UNITS:
-                return
-            cols = slice(u * UW, (u + 1) * UW)
+        def open_inputs(u):
             both = work.tile([P, 2, UW], BF16, name="xh", tag="xh", bufs=BUFS["xh"], align_bytes=64)
             xn[u], hn[u] = both[:, 0, :], both[:, 1, :]
-            nc.sync.dma_start(out=xn[u], in_=xv[:, cols])
-            nc.sync.dma_start(out=hn[u], in_=hv[:, cols])
+
+        def load_rows(natural, source, u, r0, r1):
+            w = slice(r0 * I, r1 * I)
+            nc.sync.dma_start(out=natural[:, w], in_=source[:, u * UW : (u + 1) * UW][:, w])
+
+        def load_inputs(u):
+            if u < UNITS:
+                open_inputs(u)
+                load_rows(xn[u], xv, u, 0, UROWS)
+                load_rows(hn[u], hv, u, 0, UROWS)
 
         def load_hidden_again(u):
-            if u >= UNITS:
-                return
-            h2[u] = work.tile([P, UW], BF16, name="h2", tag="h2", bufs=BUFS["h2"])
-            nc.sync.dma_start(out=h2[u][:], in_=hv[:, u * UW : (u + 1) * UW])
+            if u < UNITS:
+                h2[u] = work.tile([P, UW], BF16, name="h2", tag="h2", bufs=BUFS["h2"])
+                nc.sync.dma_start(out=h2[u][:], in_=hv[:, u * UW : (u + 1) * UW])
 
-        def transpose_rows(natural, transposed, copy):
-            sv = natural.bitcast(F32).rearrange("p (s m u) -> p s m u", s=PAIRS, m=P, u=2)
-            dv = transposed[:].rearrange("p (s m u) -> p s m u", s=PAIRS, m=P, u=2)
-            banks = []
-            for s in range(0, PAIRS, 2):
-                bank = psum.tile([P, 2, 2, P], F32, name="tin", tag="bank")
-                banks.append(bank)
-                for s2 in range(2):
-                    for u in range(2):
-                        nc.tensor.transpose(bank[:, s2, u, :], sv[:, s + s2, :, u], ident[:])
-            for s in range(0, PAIRS, 2):
-                copy(out=dv[:, s : s + 2, :, :], in_=banks[s // 2][:].rearrange("p s u m -> p s m u"))
-
-        def bring_x(u, copy=nc.vector.tensor_copy):
+        def open_x(u):
             xg[u] = work.tile([P, UW // 2], F32, name="xg", tag="xg", bufs=BUFS["xg"], align_bytes=64)
             xc[u] = work.tile([P, NCOL], U32, name="xc", tag="xc", bufs=BUFS["xc"], align_bytes=64)
             xs[u] = work.tile([P, NCOL], U8, name="xs", tag="xs", bufs=BUFS["xc"], align_bytes=64)
-            transpose_rows(xn[u], xg[u], copy)
 
-        def bring_h(u, copy=nc.vector.tensor_copy):
+        def open_h(u):
             hg[u] = work.tile([P, UW // 2], F32, name="hg", tag="hg", bufs=BUFS["hg"], align_bytes=64)
             hc[u] = work.tile([P, NCOL], U32, name="hc", tag="hc", bufs=BUFS["hc"], align_bytes=64)
             hs[u] = work.tile([P, NCOL], U8, name="hs", tag="hs", bufs=BUFS["hc"], align_bytes=64)
-            transpose_rows(hn[u], hg[u], copy)
+
+        def turn_rows(natural, transposed, starts, copy):
+            words = natural.bitcast(F32).rearrange("p (s m u) -> p s m u", m=P, u=2)
+            dv = transposed[:].rearrange("p (s m u) -> p s m u", m=P, u=2)
+            banks = []
+            for s0 in starts:
+                bank = psum.tile([P, 2, 2, P], F32, name="tin", tag="bank")
+                banks.append(bank)
+                for s in range(2):
+                    for u in range(2):
+                        nc.tensor.transpose(bank[:, s, u, :], words[:, s0 + s, :, u], ident[:])
+            for s0, bank in zip(starts, banks):
+                copy(out=dv[:, s0 : s0 + 2, :, :], in_=bank[:].rearrange("p s u m -> p s m u"))
+
+        def quantise(codes, scales, values, c0, c1):
+            nc.vector.quantize_mx(
+                out=codes[:, c0:c1].bitcast(FP8X4), scales=scales[:, c0:c1], in_=values[:, PACK * c0 : PACK * c1]
+            )
+
+        def quantise_x(u, c0=0, c1=NCOL):
+            quantise(xc[u], xs[u], xg[u][:].bitcast(BF16), c0, c1)
+
+        def quantise_h(u, c0=0, c1=NCOL):
+            quantise(hc[u], hs[u], hg[u][:].bitcast(BF16), c0, c1)
+
+        def bring_x(u, copy=on_vector):
+            open_x(u)
+            turn_rows(xn[u], xg[u], (0, 2), copy)
+
+        def bring_h(u, copy=on_vector):
+            open_h(u)
+            turn_rows(hn[u], hg[u], (0, 2), copy)
             load_inputs(u + LEAD)
 
-        def quant_x(u):
-            nc.vector.quantize_mx(out=xc[u][:].bitcast(FP8X4), scales=xs[u][:], in_=xg[u][:].bitcast(BF16))
 
-        def quant_h(u):
-            nc.vector.quantize_mx(out=hc[u][:].bitcast(FP8X4), scales=hs[u][:], in_=hg[u][:].bitcast(BF16))
-
-        def bring(u):
-            return [lambda: bring_x(u), (lambda: quant_x(u),), lambda: bring_h(u), (lambda: quant_h(u),)]
-
-        def mx_group(w, t, second_codes, second_scales, u):
-            bank = psum.tile([P, NCOL], F32, name="mx", tag="bank")
+        def mx_group(w, t, second_codes, second_scales, u, c0=0, c1=NCOL):
+            bank = psum.tile([P, c1 - c0], F32, name="mx", tag="bank")
             for part, (codes, scales) in enumerate(((xc[u], xs[u]), (second_codes, second_scales))):
                 o = w * WCOL + (2 * t + part) * P
                 nc.tensor.matmul_mx(
                     out=bank[:],
                     lhsT=wc[:, o : o + P].bitcast(FP8X4),
                     lhsT_scale=ws[:, o : o + P],
-                    rhs=codes[:].bitcast(FP8X4),
-                    rhs_scale=scales[:],
+                    rhs=codes[:, c0:c1].bitcast(FP8X4),
+                    rhs_scale=scales[:, c0:c1],
                     start=(part == 0),
                     stop=(part == 1),
                 )
@@ -186,20 +199,26 @@ def tile_ltccell_t_kernel(tc, x, hidden, W_tau, b_tau, W_r, b_r, W_h, b_h, out):
         def bias_of(w, t):
             return bias[:, PACK * w + t : PACK * w + t + 1]
 
-        def tau_job(u, t):
-            if t == 0:
-                ee[u] = work.tile([P, UW], F32, name="ee", tag="ee", bufs=BUFS["ee"])
-            bank = mx_group(TAU, t, hc[u], hs[u], u)
-            nc.scalar.activation(out=ee[u][:, chunk(t)], in_=bank[:], func=ACT.Exp, bias=bias_of(TAU, t), scale=1.0)
+        def open_tau(u):
+            ee[u] = work.tile([P, UW], F32, name="ee", tag="ee", bufs=BUFS["ee"])
 
-        def gate_job(u, t):
+        def tau(u, t, c0=0, c1=NCOL):
+            bank = mx_group(TAU, t, hc[u], hs[u], u, c0, c1)
+            o = t * NCOL
+            nc.scalar.activation(out=ee[u][:, o + c0 : o + c1], in_=bank[:], func=ACT.Exp, bias=bias_of(TAU, t), scale=1.0)
+
+        def gate(u, t):
             if t == 0:
                 th[u] = work.tile([P, UW], F32, name="th", tag="th", bufs=BUFS["th"], align_bytes=64)
             bank = mx_group(GATE, t, hc[u], hs[u], u)
             nc.scalar.activation(out=th[u][:, chunk(t)], in_=bank[:], func=ACT.Tanh, bias=bias_of(GATE, t), scale=0.5)
 
-        def jobs(f, u, n=PACK):
-            return [(lambda f=f, u=u, t=t: f(u, t)) for t in range(n)]
+        def candidate(u, t):
+            if t == 0:
+                tag = "ht" if u < UNITS - 2 else "xh"
+                ht[u] = work.tile([P, UW], F32, name="ht", tag=tag, bufs=BUFS[tag], align_bytes=64)
+            bank = mx_group(CAND, t, dc[u], ds[u], u)
+            nc.scalar.activation(out=ht[u][:, chunk(t)], in_=bank[:], func=ACT.Tanh, bias=bias_of(CAND, t), scale=1.0)
 
         def gate_hidden(u, i):
             if i == 0:
@@ -217,115 +236,110 @@ def tile_ltccell_t_kernel(tc, x, hidden, W_tau, b_tau, W_r, b_r, W_h, b_h, out):
         def quantise_gated(u):
             dc[u] = work.tile([P, NCOL], U32, name="dc", tag="dc", bufs=BUFS["dc"], align_bytes=64)
             ds[u] = work.tile([P, NCOL], U8, name="ds", tag="ds", bufs=BUFS["dc"], align_bytes=64)
-            nc.vector.quantize_mx(out=dc[u][:].bitcast(FP8X4), scales=ds[u][:], in_=dg[u][:])
-
-        def gating(u):
-            return jobs(gate_hidden, u, 2) + [(lambda: quantise_gated(u),)]
+            quantise(dc[u], ds[u], dg[u], 0, NCOL)
 
         def softplus(u):
-            nc.scalar.activation(out=ee[u][:], in_=ee[u][:], func=ACT.Ln, bias=cst[:, 0:1], scale=1.0)
-
-        def root_plain(u):
-            nc.scalar.activation(out=ee[u][:], in_=ee[u][:], func=ACT.Abs_reciprocal_sqrt, bias=cst[:, 1:2], scale=1.0)
-
-        def invert_plain(u):
-            nc.scalar.activation(out=ee[u][:], in_=ee[u][:], func=ACT.Exp, scale=-1.0)
+            nc.scalar.activation(out=ee[u][:], in_=ee[u][:], func=ACT.Ln, bias=1.0, scale=1.0)
 
 
-        def turn_tau(u, s0):
-            for s in (s0, s0 + 1):
-                bank = psum.tile([P, PACK, P], F32, name="tl", tag="bank")
-                tau_bank[u, s] = bank
-                for t in range(PACK):
-                    o = t * NCOL + s * P
-                    nc.tensor.transpose(bank[:, t, :], ee[u][:, o : o + P], ident[:])
+        def root(u):
+            nc.scalar.activation(out=ee[u][:], in_=ee[u][:], func=ACT.Abs_reciprocal_sqrt, bias=EPS, scale=1.0)
 
-        def invert_tau(u, s0):
-            if s0 == 0:
-                lt[u] = work.tile([P, UW], F32, name="lt", tag="ht", bufs=BUFS["ht"], align_bytes=64)
-            for s in (s0, s0 + 1):
-                nc.scalar.activation(
-                    out=lt[u][:, chunk(s)].rearrange("p (m t) -> p m t", t=PACK),
-                    in_=tau_bank[u, s][:].rearrange("p t m -> p m t"),
-                    func=ACT.Abs_reciprocal_sqrt,
-                    bias=cst[:, 1:2],
-                    scale=1.0,
-                )
-            for s in (s0, s0 + 1):
-                nc.scalar.activation(out=lt[u][:, chunk(s)], in_=lt[u][:, chunk(s)], func=ACT.Square)
-
-        def cand_job(u, t):
-            if t == 0:
-                tag = "ht" if u < 6 else "xh"
-                ht[u] = work.tile([P, UW], F32, name="ht", tag=tag, bufs=BUFS[tag], align_bytes=64)
-            bank = mx_group(CAND, t, dc[u], ds[u], u)
-            nc.scalar.activation(out=ht[u][:, chunk(t)], in_=bank[:], func=ACT.Tanh, bias=bias_of(CAND, t), scale=1.0)
-
-        def sub(u, i):
+        def subtract(u, i):
             planes = hg[u][:].bitcast(BF16).rearrange("p (c t) -> p t c", t=PACK)[:, 2 * i : 2 * i + 2, :]
             part = ht[u][:].rearrange("p (t c) -> p t c", t=PACK)[:, 2 * i : 2 * i + 2, :]
             nc.vector.tensor_tensor(out=part, in0=part, in1=planes, op=ALU.subtract)
 
-        def mul(u, i):
+        def multiply(u, i):
             w = slice(i * 2 * NCOL, (i + 1) * 2 * NCOL)
             nc.vector.tensor_tensor(out=ht[u][:, w], in0=ht[u][:, w], in1=ee[u][:, w], op=ALU.mult)
+
+
+        def new_bank():
+            return psum.tile([P, PACK, P], F32, name="nat", tag="bank")
+
+        def turn_back(bank, planes, s, start):
+            for t in range(PACK):
+                o = t * NCOL + s * P
+                nc.tensor.matmul(
+                    out=bank[:, t, :],
+                    lhsT=planes[:, o : o + P],
+                    rhs=ident[:],
+                    is_transpose=True,
+                    start=start,
+                    stop=start or t == PACK - 1,
+                )
+
+        def in_order(bank):
+            return bank[:].rearrange("p t m -> p m t")
+
+        def row_view(ap):
+            return ap.rearrange("p (m t) -> p m t", t=PACK)
 
         def give_back(u, s0):
             banks = []
             for s in (s0, s0 + 1):
-                bank = psum.tile([P, PACK, P], F32, name="tb", tag="bank")
-                banks.append(bank)
-                for t in range(PACK):
-                    o = t * NCOL + s * P
-                    nc.tensor.transpose(bank[:, t, :], ht[u][:, o : o + P], ident[:])
+                banks.append(new_bank())
+                turn_back(banks[-1], ht[u], s, True)
             result = work.tile([P, 2 * NCOL], F32, name="oo", tag="hg", bufs=BUFS["hg"], align_bytes=64)
             for i in range(2):
-                w = slice(i * NCOL, (i + 1) * NCOL)
                 nc.vector.tensor_tensor(
-                    out=result[:, w].rearrange("p (m t) -> p m t", t=PACK),
-                    in0=banks[i][:].rearrange("p t m -> p m t"),
-                    in1=h2[u][:, chunk(s0 + i)].rearrange("p (m t) -> p m t", t=PACK),
-                    op=ALU.add,
+                    out=row_view(result[:, chunk(i)]), in0=in_order(banks[i]), in1=row_view(h2[u][:, chunk(s0 + i)]), op=ALU.add
                 )
             o = u * UW + s0 * NCOL
             nc.sync.dma_start(out=ov[:, o : o + 2 * NCOL], in_=result[:])
             if s0 + 2 == PAIRS:
-                load_hidden_again(u + 3)
+                load_hidden_again(u + AGAIN)
+
+
+        def turn_tau(u, s0):
+            for s in (s0, s0 + 1):
+                tau_bank[u, s] = new_bank()
+                turn_back(tau_bank[u, s], ee[u], s, True)
 
         def difference(u, s0):
             for s in (s0, s0 + 1):
-                bank = psum.tile([P, PACK, P], F32, name="td", tag="bank")
-                diff_bank[u, s] = bank
+                diff_bank[u, s] = new_bank()
                 nc.tensor.matmul(
-                    out=bank[:],
+                    out=diff_bank[u, s][:],
                     lhsT=negid[:],
                     rhs=h2[u][:, chunk(s)].rearrange("p (m t) -> p t m", t=PACK),
                     start=True,
                     stop=False,
                 )
             for s in (s0, s0 + 1):
-                for t in range(PACK):
-                    o = t * NCOL + s * P
-                    nc.tensor.matmul(
-                        out=diff_bank[u, s][:, t, :],
-                        lhsT=ht[u][:, o : o + P],
-                        rhs=ident[:],
-                        is_transpose=True,
-                        start=False,
-                        stop=(t == PACK - 1),
-                    )
+                turn_back(diff_bank[u, s], ht[u], s, False)
 
-        def finish(u, s0):
+        def invert_tau(u, s0):
+            if s0 == 0:
+                lt[u] = work.tile([P, UW], F32, name="lt", tag="ht", bufs=BUFS["ht"], align_bytes=64)
             for s in (s0, s0 + 1):
-                part = lt[u][:, chunk(s)].rearrange("p (m t) -> p m t", t=PACK)
-                nc.vector.tensor_tensor(out=part, in0=diff_bank[u, s][:].rearrange("p t m -> p m t"), in1=part, op=ALU.mult)
+                nc.scalar.activation(
+                    out=row_view(lt[u][:, chunk(s)]),
+                    in_=in_order(tau_bank[u, s]),
+                    func=ACT.Abs_reciprocal_sqrt,
+                    bias=EPS,
+                    scale=1.0,
+                )
             for s in (s0, s0 + 1):
-                w = chunk(s)
-                nc.vector.tensor_tensor(out=lt[u][:, w], in0=lt[u][:, w], in1=h2[u][:, w], op=ALU.add)
-            o = u * UW + s0 * NCOL
-            nc.sync.dma_start(out=ov[:, o : o + 2 * NCOL], in_=lt[u][:, s0 * NCOL : (s0 + 2) * NCOL])
-            if s0 + 2 == PAIRS:
-                load_hidden_again(u + 3)
+                nc.scalar.activation(out=lt[u][:, chunk(s)], in_=lt[u][:, chunk(s)], func=ACT.Square)
+
+        def divide(u, s0):
+            for s in (s0, s0 + 1):
+                part = row_view(lt[u][:, chunk(s)])
+                nc.vector.tensor_tensor(out=part, in0=in_order(diff_bank[u, s]), in1=part, op=ALU.mult)
+
+        def finish(u, s0, n=2):
+            w = slice(s0 * NCOL, (s0 + n) * NCOL)
+            nc.vector.tensor_tensor(out=lt[u][:, w], in0=lt[u][:, w], in1=h2[u][:, w], op=ALU.add)
+            o = u * UW
+            nc.sync.dma_start(out=ov[:, o + s0 * NCOL : o + (s0 + n) * NCOL], in_=lt[u][:, w])
+            if s0 + n == PAIRS:
+                load_hidden_again(u + AGAIN)
+
+
+        def jobs(f, u, n=PACK):
+            return [(lambda t=t: f(u, t)) for t in range(n)]
 
         late = []
 
@@ -348,65 +362,83 @@ def tile_ltccell_t_kernel(tc, x, hidden, W_tau, b_tau, W_r, b_r, W_h, b_h, out):
                 done = upto
             run(lambda: None)
 
+        def bring(u, cx=on_vector, ch=on_vector):
+            return [lambda: bring_x(u, cx), (lambda: quantise_x(u),), lambda: bring_h(u, ch), (lambda: quantise_h(u),)]
 
-        setup()
+        def gating(u):
+            return jobs(gate_hidden, u, 2) + [(lambda: quantise_gated(u),)]
+
+        def tau_and_gate(u):
+            return [lambda: open_tau(u)] + jobs(tau, u) + jobs(gate, u)
+
+        def update(u):
+            return [
+                lambda: subtract(u, 0),
+                lambda: subtract(u, 1),
+                lambda: multiply(u, 0),
+                lambda: multiply(u, 1),
+                lambda: multiply(u, 0),
+                lambda: multiply(u, 1),
+            ]
+
+        def result(u):
+            return [lambda: give_back(u, 0), lambda: give_back(u, 2)]
+
+        make_identity(nc, ident[:])
         load_weight(TAU, nc.vector)
-        load_inputs(0)
+        open_inputs(0)
+        load_rows(xn[0], xv, 0, 0, UROWS)
+        load_rows(hn[0], hv, 0, 0, UROWS)
         load_biases()
         load_weight(GATE, nc.gpsimd)
         load_weight(CAND, nc.gpsimd)
         load_inputs(1)
         halve_hidden_columns()
-        prep_negid()
-        S, V = nc.scalar.copy, nc.vector.tensor_copy
-        G1, G2 = GROUPS
-        def nslot(u):
-            return jobs(tau_job, u) + jobs(gate_job, u)
-        def cslot(u):
-            return jobs(cand_job, u)
-        def fin1(u):
-            return [lambda: sub(u, 0), lambda: sub(u, 1), lambda: mul(u, 0), lambda: mul(u, 1), lambda: mul(u, 0), lambda: mul(u, 1)]
-        def fin2(u):
-            return [lambda: give_back(u, 0), lambda: give_back(u, 2)]
-        prepare_weight(TAU, (S, V))
+        negate_identity()
+
+        prepare_weight(TAU, (on_scalar, on_vector))
         prepare_biases()
-        bring_x(0, S)
-        quant_w(TAU)
-        bring_h(0, S)
-        quant_x(0)
-        quant_h(0)
-        prepare_weight(GATE, (S, V))
-        weave(jobs(tau_job, 0), [lambda: quant_w(GATE)] + bring(1)[:2])
-        weave(jobs(gate_job, 0), bring(1)[2:])
-        prepare_weight(CAND, (S, S))
-        for u in range(3):
+        bring_x(0, on_scalar)
+        quantise_weight(TAU)
+        bring_h(0, on_scalar)
+        quantise_x(0)
+        quantise_h(0)
+        prepare_weight(GATE, (on_scalar, on_vector))
+        weave([lambda: open_tau(0)] + jobs(tau, 0), [lambda: quantise_weight(GATE)] + bring(1, on_scalar, on_scalar)[:2])
+        weave(jobs(gate, 0), bring(1, on_scalar, on_scalar)[2:])
+        prepare_weight(CAND, (on_vector, on_vector))
+        for u in range(AGAIN):
             load_hidden_again(u)
-        weave(nslot(1), bring(2) + gating(0))
-        weave(nslot(2), gating(1))
-        main = [lambda u=u: softplus(u) for u in G1] + [lambda u=u: root_plain(u) for u in G1]
+        weave(tau_and_gate(1), bring(2, on_scalar, on_scalar) + gating(0))
+        weave(tau_and_gate(2), [lambda: quantise_weight(CAND)] + gating(1))
 
-        weave(main, bring(3) + [lambda: quant_w(CAND)] + bring(4) + bring(5) + bring(6))
-        weave(cslot(0), gating(2))
-        weave(nslot(3), [])
-        weave(cslot(1), fin1(0))
-        weave(nslot(4), gating(3) + fin1(1)[:2])
-        weave(cslot(2), fin1(1)[2:])
-        weave(nslot(5), gating(4) + bring(7)[:2])
-        weave(nslot(6), bring(7)[2:] + gating(5))
-        weave(jobs(cand_job, 3) + jobs(cand_job, 4), gating(6))
-        weave(nslot(7), [])
-        weave(jobs(cand_job, 5), gating(7))
-        weave(jobs(cand_job, 6), [])
-        weave(jobs(cand_job, 7), [])
+        main = [lambda u=u: softplus(u) for u in FIRST] + [lambda u=u: root(u) for u in FIRST]
+        weave(main, bring(3) + bring(4) + bring(5) + bring(6))
 
-        weave([lambda u=u: softplus(u) for u in G2], fin2(0) + fin1(2) + fin2(1) + fin2(2))
-        steps = [(u, s0) for u in G2 for s0 in (0, 2)]
+        weave(jobs(candidate, 0), gating(2))
+        weave(tau_and_gate(3), [])
+        weave(jobs(candidate, 1), update(0))
+        weave(tau_and_gate(4), gating(3) + update(1)[:2])
+        weave(jobs(candidate, 2), update(1)[2:])
+        weave(tau_and_gate(5), gating(4) + bring(7)[:2])
+        weave(tau_and_gate(6), bring(7)[2:] + gating(5))
+        weave(jobs(candidate, 3) + jobs(candidate, 4), gating(6))
+        weave(tau_and_gate(7), [])
+        weave(jobs(candidate, 5), gating(7))
+        weave(jobs(candidate, 6), [])
+        weave(jobs(candidate, 7), [])
+
+        weave([lambda u=u: softplus(u) for u in SECOND], result(0) + update(2) + result(1) + result(2))
+
+        steps = [(u, s0) for u in SECOND for s0 in (0, 2)]
         for i in range(2):
             turn_tau(*steps[i])
             difference(*steps[i])
         for i in range(len(steps)):
             invert_tau(*steps[i])
-            finish(*steps[i])
+            divide(*steps[i])
+            for s in (0, 1):
+                finish(steps[i][0], steps[i][1] + s, 1)
             if i + 2 < len(steps):
                 turn_tau(*steps[i + 2])
                 difference(*steps[i + 2])

@@ -26,8 +26,10 @@ WCOL = 2 * PACK * P
 EPS = 1e-6
 TAU, GATE, CAND = 0, 1, 2
 FIRST, SECOND = (0, 1, 2), (3, 4, 5, 6, 7)
+SQUARED = (3,)
 LEAD = 2
 AGAIN = 3
+NEXT = {0: 3, 1: 4, 2: 7}
 
 BUFS = {"th": 2, "ht": 6, "xh": 2, "h2": 3, "xg": 1, "hg": 8, "xc": 7, "hc": 4, "dg": 1, "dc": 5, "ee": 6}
 
@@ -48,6 +50,7 @@ def tile_ltccell_t_kernel(tc, x, hidden, W_tau, b_tau, W_r, b_r, W_h, b_h, out):
         ctx.enter_context(tc.manual_schedule())
 
         ident = const.tile([P, P], F32, name="ident")
+        posid = const.tile([P, P], BF16, name="posid")
         negid = const.tile([P, P], BF16, name="negid")
         braw = const.tile([P, 3, 16], BF16, name="braw")
         bias = const.tile([P, 3 * PACK], F32, name="bias")
@@ -63,7 +66,7 @@ def tile_ltccell_t_kernel(tc, x, hidden, W_tau, b_tau, W_r, b_r, W_h, b_h, out):
 
 
         def load_weight(w, zero_engine):
-            wn[w] = work.tile([P, 2, 768], BF16, name="wn", tag="h2", bufs=BUFS["h2"])
+            wn[w] = work.tile([P, 2, 768], BF16, name="wn", tag="h2", bufs=BUFS["h2"], align_bytes=64)
             src = weights[w].rearrange("(c p) k -> p c k", p=P)
             nc.sync.dma_start(out=wn[w][:, :, 0:512], in_=src)
             nc.sync.dma_start(out=wn[w][:, :, 512:768], in_=src[:, :, 0:256])
@@ -87,7 +90,8 @@ def tile_ltccell_t_kernel(tc, x, hidden, W_tau, b_tau, W_r, b_r, W_h, b_h, out):
             part = wn[CAND][:, :, 256:512]
             nc.gpsimd.tensor_scalar(out=part, in0=part, scalar1=0.5, scalar2=0.0, op0=ALU.mult, op1=ALU.add)
 
-        def negate_identity():
+        def signed_identities():
+            make_identity(nc, posid[:])
             make_identity(nc, negid[:])
             nc.gpsimd.tensor_scalar(out=negid[:], in0=negid[:], scalar1=-1.0, scalar2=0.0, op0=ALU.mult, op1=ALU.add)
 
@@ -134,7 +138,8 @@ def tile_ltccell_t_kernel(tc, x, hidden, W_tau, b_tau, W_r, b_r, W_h, b_h, out):
 
         def load_hidden_again(u):
             if u < UNITS:
-                h2[u] = work.tile([P, UW], BF16, name="h2", tag="h2", bufs=BUFS["h2"])
+                tag = "th" if u in (5, 6) else "h2"
+                h2[u] = work.tile([P, UW], BF16, name="h2", tag=tag, bufs=BUFS[tag], align_bytes=64)
                 nc.sync.dma_start(out=h2[u][:], in_=hv[:, u * UW : (u + 1) * UW])
 
         def open_x(u):
@@ -220,15 +225,13 @@ def tile_ltccell_t_kernel(tc, x, hidden, W_tau, b_tau, W_r, b_r, W_h, b_h, out):
             bank = mx_group(CAND, t, dc[u], ds[u], u)
             nc.scalar.activation(out=ht[u][:, chunk(t)], in_=bank[:], func=ACT.Tanh, bias=bias_of(CAND, t), scale=1.0)
 
-        def gate_hidden(u, i):
-            if i == 0:
-                dg[u] = work.tile([P, UW], BF16, name="dg", tag="dg", bufs=BUFS["dg"], align_bytes=64)
-            c = slice(i * 2 * P, (i + 1) * 2 * P)
+        def gate_hidden(u):
+            dg[u] = work.tile([P, UW], BF16, name="dg", tag="dg", bufs=BUFS["dg"], align_bytes=64)
             nc.vector.scalar_tensor_tensor(
-                out=dg[u][:].rearrange("p (c t) -> p c t", t=PACK)[:, c, :],
-                in0=th[u][:].rearrange("p (t c) -> p c t", t=PACK)[:, c, :],
+                out=dg[u][:].rearrange("p (c t) -> p c t", t=PACK),
+                in0=th[u][:].rearrange("p (t c) -> p c t", t=PACK),
                 scalar=1.0,
-                in1=hg[u][:].bitcast(BF16).rearrange("p (c t) -> p c t", t=PACK)[:, c, :],
+                in1=hg[u][:].bitcast(BF16).rearrange("p (c t) -> p c t", t=PACK),
                 op0=ALU.add,
                 op1=ALU.mult,
             )
@@ -289,7 +292,38 @@ def tile_ltccell_t_kernel(tc, x, hidden, W_tau, b_tau, W_r, b_r, W_h, b_h, out):
             o = u * UW + s0 * NCOL
             nc.sync.dma_start(out=ov[:, o : o + 2 * NCOL], in_=result[:])
             if s0 + 2 == PAIRS:
-                load_hidden_again(u + AGAIN)
+                load_hidden_again(NEXT[u])
+
+
+        def square_tau(u, i):
+            w = slice(i * 2 * NCOL, (i + 1) * 2 * NCOL)
+            nc.vector.scalar_tensor_tensor(
+                out=ee[u][:, w], in0=ee[u][:, w], scalar=2 * EPS, in1=ee[u][:, w], op0=ALU.add, op1=ALU.mult
+            )
+
+
+        def invert_turned(u):
+            nc.scalar.activation(out=ee[u][:], in_=ee[u][:], func=ACT.Abs_reciprocal_sqrt, bias=EPS * EPS, scale=1.0)
+
+        def add_hidden(u, s0):
+            for s in (s0, s0 + 1):
+                diff_bank[u, s] = new_bank()
+                nc.tensor.matmul(
+                    out=diff_bank[u, s][:],
+                    lhsT=posid[:],
+                    rhs=h2[u][:, chunk(s)].rearrange("p (m t) -> p t m", t=PACK),
+                    start=True,
+                    stop=False,
+                )
+            for s in (s0, s0 + 1):
+                turn_back(diff_bank[u, s], ht[u], s, False)
+
+        def copy_out(u, s0):
+            result = work.tile([P, 2 * NCOL], F32, name="oo", tag="hg", bufs=BUFS["hg"], align_bytes=64)
+            for i in range(2):
+                nc.scalar.copy(out=row_view(result[:, chunk(i)]), in_=in_order(diff_bank[u, s0 + i]))
+            o = u * UW + s0 * NCOL
+            nc.sync.dma_start(out=ov[:, o : o + 2 * NCOL], in_=result[:])
 
 
         def turn_tau(u, s0):
@@ -318,11 +352,52 @@ def tile_ltccell_t_kernel(tc, x, hidden, W_tau, b_tau, W_r, b_r, W_h, b_h, out):
                     out=row_view(lt[u][:, chunk(s)]),
                     in_=in_order(tau_bank[u, s]),
                     func=ACT.Abs_reciprocal_sqrt,
+                    bias=EPS * EPS if u in SQUARED else EPS,
+                    scale=1.0,
+                )
+            if u in SQUARED:
+                return
+            for s in (s0, s0 + 1):
+                nc.scalar.activation(out=lt[u][:, chunk(s)], in_=lt[u][:, chunk(s)], func=ACT.Square)
+
+        def natural_root(u):
+            lt[u] = work.tile([P, UW], F32, name="lt", tag="ee", bufs=BUFS["ee"])
+            for s in range(PAIRS):
+                nc.scalar.activation(
+                    out=row_view(lt[u][:, chunk(s)]),
+                    in_=in_order(tau_bank[u, s]),
+                    func=ACT.Abs_reciprocal_sqrt,
                     bias=EPS,
                     scale=1.0,
                 )
-            for s in (s0, s0 + 1):
-                nc.scalar.activation(out=lt[u][:, chunk(s)], in_=lt[u][:, chunk(s)], func=ACT.Square)
+
+        def natural_update(u):
+            parts = {}
+
+            def first(s0):
+                difference(u, s0)
+                parts[s0] = work.tile([P, 2 * NCOL], F32, name="oo", tag="hg", bufs=BUFS["hg"], align_bytes=64)
+                for i in range(2):
+                    nc.vector.tensor_tensor(
+                        out=row_view(parts[s0][:, chunk(i)]),
+                        in0=in_order(diff_bank[u, s0 + i]),
+                        in1=row_view(lt[u][:, chunk(s0 + i)]),
+                        op=ALU.mult,
+                    )
+
+            def second(s0):
+                w = slice(s0 * NCOL, (s0 + 2) * NCOL)
+                nc.vector.tensor_tensor(out=parts[s0][:], in0=parts[s0][:], in1=lt[u][:, w], op=ALU.mult)
+
+            def third(s0):
+                w = slice(s0 * NCOL, (s0 + 2) * NCOL)
+                nc.vector.tensor_tensor(out=parts[s0][:], in0=parts[s0][:], in1=h2[u][:, w], op=ALU.add)
+                o = u * UW + s0 * NCOL
+                nc.sync.dma_start(out=ov[:, o : o + 2 * NCOL], in_=parts[s0][:])
+                if s0 + 2 == PAIRS:
+                    load_hidden_again(NEXT[u])
+
+            return [(lambda f=f, s0=s0: f(s0)) for f in (first, second, third) for s0 in (0, 2)]
 
         def divide(u, s0):
             for s in (s0, s0 + 1):
@@ -334,8 +409,6 @@ def tile_ltccell_t_kernel(tc, x, hidden, W_tau, b_tau, W_r, b_r, W_h, b_h, out):
             nc.vector.tensor_tensor(out=lt[u][:, w], in0=lt[u][:, w], in1=h2[u][:, w], op=ALU.add)
             o = u * UW
             nc.sync.dma_start(out=ov[:, o + s0 * NCOL : o + (s0 + n) * NCOL], in_=lt[u][:, w])
-            if s0 + n == PAIRS:
-                load_hidden_again(u + AGAIN)
 
 
         def jobs(f, u, n=PACK):
@@ -360,13 +433,21 @@ def tile_ltccell_t_kernel(tc, x, hidden, W_tau, b_tau, W_r, b_r, W_h, b_h, out):
                 for g in side[done:upto]:
                     run(g)
                 done = upto
+
+        def settle():
             run(lambda: None)
 
+        def settle_job():
+            return
+
         def bring(u, cx=on_vector, ch=on_vector):
+            return [lambda: bring_x(u, cx), lambda: bring_h(u, ch), lambda: quantise_x(u), lambda: quantise_h(u)]
+
+        def bring_soon(u, cx=on_vector, ch=on_vector):
             return [lambda: bring_x(u, cx), (lambda: quantise_x(u),), lambda: bring_h(u, ch), (lambda: quantise_h(u),)]
 
         def gating(u):
-            return jobs(gate_hidden, u, 2) + [(lambda: quantise_gated(u),)]
+            return [lambda: gate_hidden(u), (lambda: quantise_gated(u),)]
 
         def tau_and_gate(u):
             return [lambda: open_tau(u)] + jobs(tau, u) + jobs(gate, u)
@@ -394,7 +475,7 @@ def tile_ltccell_t_kernel(tc, x, hidden, W_tau, b_tau, W_r, b_r, W_h, b_h, out):
         load_weight(CAND, nc.gpsimd)
         load_inputs(1)
         halve_hidden_columns()
-        negate_identity()
+        signed_identities()
 
         prepare_weight(TAU, (on_scalar, on_vector))
         prepare_biases()
@@ -404,41 +485,47 @@ def tile_ltccell_t_kernel(tc, x, hidden, W_tau, b_tau, W_r, b_r, W_h, b_h, out):
         quantise_x(0)
         quantise_h(0)
         prepare_weight(GATE, (on_scalar, on_vector))
-        weave([lambda: open_tau(0)] + jobs(tau, 0), [lambda: quantise_weight(GATE)] + bring(1, on_scalar, on_scalar)[:2])
-        weave(jobs(gate, 0), bring(1, on_scalar, on_scalar)[2:])
+        weave([lambda: open_tau(0)] + jobs(tau, 0), [lambda: quantise_weight(GATE)] + bring_soon(1, on_scalar, on_scalar)[:2])
+        weave(jobs(gate, 0), bring_soon(1, on_scalar, on_scalar)[2:])
+        settle()
         prepare_weight(CAND, (on_vector, on_vector))
         for u in range(AGAIN):
             load_hidden_again(u)
-        weave(tau_and_gate(1), bring(2, on_scalar, on_scalar) + gating(0))
+        weave(tau_and_gate(1), bring_soon(2, on_scalar, on_scalar) + gating(0))
         weave(tau_and_gate(2), [lambda: quantise_weight(CAND)] + gating(1))
 
-        main = [lambda u=u: softplus(u) for u in FIRST] + [lambda u=u: root(u) for u in FIRST]
-        weave(main, bring(3) + bring(4) + bring(5) + bring(6))
+        main = [lambda u=u: softplus(u) for u in FIRST] + [lambda u=u: root(u) for u in FIRST[:2]] + [lambda: natural_root(2)]
+        weave(main, bring(3) + bring(4) + bring(5) + [lambda: turn_tau(2, 0), lambda: turn_tau(2, 2)] + bring(6))
 
         weave(jobs(candidate, 0), gating(2))
         weave(tau_and_gate(3), [])
         weave(jobs(candidate, 1), update(0))
         weave(tau_and_gate(4), gating(3) + update(1)[:2])
         weave(jobs(candidate, 2), update(1)[2:])
-        weave(tau_and_gate(5), gating(4) + bring(7)[:2])
-        weave(tau_and_gate(6), bring(7)[2:] + gating(5))
+        weave(tau_and_gate(5), gating(4) + bring(7, on_scalar, on_vector)[:2])
+        weave(tau_and_gate(6), gating(5) + bring(7, on_scalar, on_vector)[2:])
         weave(jobs(candidate, 3) + jobs(candidate, 4), gating(6))
-        weave(tau_and_gate(7), [])
+        weave(tau_and_gate(7), [settle_job])
         weave(jobs(candidate, 5), gating(7))
-        weave(jobs(candidate, 6), [])
+        weave(jobs(candidate, 6), [settle_job])
         weave(jobs(candidate, 7), [])
+        load_hidden_again(5)
+        load_hidden_again(6)
 
-        weave([lambda u=u: softplus(u) for u in SECOND], result(0) + update(2) + result(1) + result(2))
+        weave([lambda u=u: softplus(u) for u in SECOND], result(0) + result(1) + [lambda: square_tau(3, 0), lambda: square_tau(3, 1)] + natural_update(2))
 
         steps = [(u, s0) for u in SECOND for s0 in (0, 2)]
-        for i in range(2):
-            turn_tau(*steps[i])
-            difference(*steps[i])
+
+        def prepare(i):
+            if i < len(steps):
+                turn_tau(*steps[i])
+                difference(*steps[i])
+
+        prepare(0)
+        prepare(1)
         for i in range(len(steps)):
             invert_tau(*steps[i])
             divide(*steps[i])
             for s in (0, 1):
                 finish(steps[i][0], steps[i][1] + s, 1)
-            if i + 2 < len(steps):
-                turn_tau(*steps[i + 2])
-                difference(*steps[i + 2])
+            prepare(i + 2)

@@ -26,12 +26,12 @@ WCOL = 2 * PACK * P
 EPS = 1e-6
 TAU, GATE, CAND = 0, 1, 2
 FIRST, SECOND = (0, 1, 2), (3, 4, 5, 6, 7)
+LAST = 2
 SQUARED = (3,)
 LEAD = 2
-AGAIN = 3
-NEXT = {0: 3, 1: 4, 2: 7}
+AGAIN = ("h2", "h2", "h2", "hn", "h2", "xn", "xn", "hn")
 
-BUFS = {"th": 2, "ht": 6, "xh": 2, "h2": 3, "xg": 1, "hg": 8, "xc": 7, "hc": 4, "dg": 1, "dc": 5, "ee": 6}
+BUFS = {"th": 2, "ht": 6, "xn": 2, "hn": 2, "h2": 3, "xg": 1, "hg": 8, "xc": 7, "hc": 4, "dg": 1, "dc": 5, "ee": 6}
 
 
 def tile_ltccell_t_kernel(tc, x, hidden, W_tau, b_tau, W_r, b_r, W_h, b_h, out):
@@ -50,14 +50,13 @@ def tile_ltccell_t_kernel(tc, x, hidden, W_tau, b_tau, W_r, b_r, W_h, b_h, out):
         ctx.enter_context(tc.manual_schedule())
 
         ident = const.tile([P, P], F32, name="ident")
-        posid = const.tile([P, P], BF16, name="posid")
         negid = const.tile([P, P], BF16, name="negid")
         braw = const.tile([P, 3, 16], BF16, name="braw")
         bias = const.tile([P, 3 * PACK], F32, name="bias")
         wc = const.tile([P, 3 * WCOL], U32, name="wc", align_bytes=64)
         ws = const.tile([P, 3 * WCOL], U8, name="ws", align_bytes=64)
 
-        xn, hn, h2, xg, hg, xc, xs, hc, hs, dc, ds = {}, {}, {}, {}, {}, {}, {}, {}, {}, {}, {}
+        xn, hn, h2, xg, hg, xq, hq, dq = {}, {}, {}, {}, {}, {}, {}, {}
         wn, wg, th, dg, ee, ht, lt = {}, {}, {}, {}, {}, {}, {}
         tau_bank, diff_bank = {}, {}
 
@@ -90,8 +89,7 @@ def tile_ltccell_t_kernel(tc, x, hidden, W_tau, b_tau, W_r, b_r, W_h, b_h, out):
             part = wn[CAND][:, :, 256:512]
             nc.gpsimd.tensor_scalar(out=part, in0=part, scalar1=0.5, scalar2=0.0, op0=ALU.mult, op1=ALU.add)
 
-        def signed_identities():
-            make_identity(nc, posid[:])
+        def negate_identity():
             make_identity(nc, negid[:])
             nc.gpsimd.tensor_scalar(out=negid[:], in0=negid[:], scalar1=-1.0, scalar2=0.0, op0=ALU.mult, op1=ALU.add)
 
@@ -114,88 +112,75 @@ def tile_ltccell_t_kernel(tc, x, hidden, W_tau, b_tau, W_r, b_r, W_h, b_h, out):
                             in_=bank[rows, :, c, :].rearrange("p u (q t) -> p t q u", t=PACK),
                         )
 
-        def quantise_weight(w, t0=0, t1=PACK):
-            c0, c1 = 2 * P * t0, 2 * P * t1
-            cols = slice(w * WCOL + c0, w * WCOL + c1)
-            nc.vector.quantize_mx(
-                out=wc[:, cols].bitcast(FP8X4), scales=ws[:, cols], in_=wg[w][:].bitcast(BF16)[:, PACK * c0 : PACK * c1]
-            )
+        def quantise_weight(w):
+            cols = slice(w * WCOL, (w + 1) * WCOL)
+            nc.vector.quantize_mx(out=wc[:, cols].bitcast(FP8X4), scales=ws[:, cols], in_=wg[w][:].bitcast(BF16))
 
 
-        def open_inputs(u):
-            both = work.tile([P, 2, UW], BF16, name="xh", tag="xh", bufs=BUFS["xh"], align_bytes=64)
-            xn[u], hn[u] = both[:, 0, :], both[:, 1, :]
-
-        def load_rows(natural, source, u, r0, r1):
-            w = slice(r0 * I, r1 * I)
-            nc.sync.dma_start(out=natural[:, w], in_=source[:, u * UW : (u + 1) * UW][:, w])
-
-        def load_inputs(u):
+        def load_x(u):
             if u < UNITS:
-                open_inputs(u)
-                load_rows(xn[u], xv, u, 0, UROWS)
-                load_rows(hn[u], hv, u, 0, UROWS)
+                xn[u] = work.tile([P, UW], BF16, name="xn", tag="xn", bufs=BUFS["xn"], align_bytes=64)
+                nc.sync.dma_start(out=xn[u][:], in_=xv[:, u * UW : (u + 1) * UW])
+
+        def load_h(u):
+            if u < UNITS:
+                hn[u] = work.tile([P, UW], BF16, name="hn", tag="hn", bufs=BUFS["hn"], align_bytes=64)
+                nc.sync.dma_start(out=hn[u][:], in_=hv[:, u * UW : (u + 1) * UW])
 
         def load_hidden_again(u):
-            if u < UNITS:
-                tag = "th" if u in (5, 6) else "h2"
-                h2[u] = work.tile([P, UW], BF16, name="h2", tag=tag, bufs=BUFS[tag], align_bytes=64)
-                nc.sync.dma_start(out=h2[u][:], in_=hv[:, u * UW : (u + 1) * UW])
+            tag = AGAIN[u]
+            h2[u] = work.tile([P, UW], BF16, name="h2", tag=tag, bufs=BUFS[tag], align_bytes=64)
+            nc.sync.dma_start(out=h2[u][:], in_=hv[:, u * UW : (u + 1) * UW])
 
-        def open_x(u):
-            xg[u] = work.tile([P, UW // 2], F32, name="xg", tag="xg", bufs=BUFS["xg"], align_bytes=64)
-            xc[u] = work.tile([P, NCOL], U32, name="xc", tag="xc", bufs=BUFS["xc"], align_bytes=64)
-            xs[u] = work.tile([P, NCOL], U8, name="xs", tag="xs", bufs=BUFS["xc"], align_bytes=64)
-
-        def open_h(u):
-            hg[u] = work.tile([P, UW // 2], F32, name="hg", tag="hg", bufs=BUFS["hg"], align_bytes=64)
-            hc[u] = work.tile([P, NCOL], U32, name="hc", tag="hc", bufs=BUFS["hc"], align_bytes=64)
-            hs[u] = work.tile([P, NCOL], U8, name="hs", tag="hs", bufs=BUFS["hc"], align_bytes=64)
-
-        def turn_rows(natural, transposed, starts, copy):
-            words = natural.bitcast(F32).rearrange("p (s m u) -> p s m u", m=P, u=2)
+        def turn_rows(natural, transposed, copy):
+            words = natural[:].bitcast(F32).rearrange("p (s m u) -> p s m u", m=P, u=2)
             dv = transposed[:].rearrange("p (s m u) -> p s m u", m=P, u=2)
             banks = []
-            for s0 in starts:
+            for s0 in (0, 2):
                 bank = psum.tile([P, 2, 2, P], F32, name="tin", tag="bank")
                 banks.append(bank)
                 for s in range(2):
                     for u in range(2):
                         nc.tensor.transpose(bank[:, s, u, :], words[:, s0 + s, :, u], ident[:])
-            for s0, bank in zip(starts, banks):
+            for s0, bank in zip((0, 2), banks):
                 copy(out=dv[:, s0 : s0 + 2, :, :], in_=bank[:].rearrange("p s u m -> p s m u"))
 
-        def quantise(codes, scales, values, c0, c1):
-            nc.vector.quantize_mx(
-                out=codes[:, c0:c1].bitcast(FP8X4), scales=scales[:, c0:c1], in_=values[:, PACK * c0 : PACK * c1]
-            )
-
-        def quantise_x(u, c0=0, c1=NCOL):
-            quantise(xc[u], xs[u], xg[u][:].bitcast(BF16), c0, c1)
-
-        def quantise_h(u, c0=0, c1=NCOL):
-            quantise(hc[u], hs[u], hg[u][:].bitcast(BF16), c0, c1)
-
         def bring_x(u, copy=on_vector):
-            open_x(u)
-            turn_rows(xn[u], xg[u], (0, 2), copy)
+            xg[u] = work.tile([P, UW // 2], F32, name="xg", tag="xg", bufs=BUFS["xg"], align_bytes=64)
+            turn_rows(xn[u], xg[u], copy)
+            load_x(u + LEAD)
 
         def bring_h(u, copy=on_vector):
-            open_h(u)
-            turn_rows(hn[u], hg[u], (0, 2), copy)
-            load_inputs(u + LEAD)
+            hg[u] = work.tile([P, UW // 2], F32, name="hg", tag="hg", bufs=BUFS["hg"], align_bytes=64)
+            turn_rows(hn[u], hg[u], copy)
+            load_h(u + LEAD)
+
+        def quantise(tag, values):
+            codes = work.tile([P, NCOL], U32, name="codes", tag=tag, bufs=BUFS[tag], align_bytes=64)
+            scales = work.tile([P, NCOL], U8, name="scales", tag=tag + "s", bufs=BUFS[tag], align_bytes=64)
+            nc.vector.quantize_mx(out=codes[:].bitcast(FP8X4), scales=scales[:], in_=values)
+            return codes, scales
+
+        def quantise_x(u):
+            xq[u] = quantise("xc", xg[u][:].bitcast(BF16))
+
+        def quantise_h(u):
+            hq[u] = quantise("hc", hg[u][:].bitcast(BF16))
+
+        def quantise_gated(u):
+            dq[u] = quantise("dc", dg[u][:])
 
 
-        def mx_group(w, t, second_codes, second_scales, u, c0=0, c1=NCOL):
-            bank = psum.tile([P, c1 - c0], F32, name="mx", tag="bank")
-            for part, (codes, scales) in enumerate(((xc[u], xs[u]), (second_codes, second_scales))):
+        def mx_group(w, t, first, second):
+            bank = psum.tile([P, NCOL], F32, name="mx", tag="bank")
+            for part, (codes, scales) in enumerate((first, second)):
                 o = w * WCOL + (2 * t + part) * P
                 nc.tensor.matmul_mx(
                     out=bank[:],
                     lhsT=wc[:, o : o + P].bitcast(FP8X4),
                     lhsT_scale=ws[:, o : o + P],
-                    rhs=codes[:, c0:c1].bitcast(FP8X4),
-                    rhs_scale=scales[:, c0:c1],
+                    rhs=codes[:].bitcast(FP8X4),
+                    rhs_scale=scales[:],
                     start=(part == 0),
                     stop=(part == 1),
                 )
@@ -204,25 +189,23 @@ def tile_ltccell_t_kernel(tc, x, hidden, W_tau, b_tau, W_r, b_r, W_h, b_h, out):
         def bias_of(w, t):
             return bias[:, PACK * w + t : PACK * w + t + 1]
 
-        def open_tau(u):
-            ee[u] = work.tile([P, UW], F32, name="ee", tag="ee", bufs=BUFS["ee"])
-
-        def tau(u, t, c0=0, c1=NCOL):
-            bank = mx_group(TAU, t, hc[u], hs[u], u, c0, c1)
-            o = t * NCOL
-            nc.scalar.activation(out=ee[u][:, o + c0 : o + c1], in_=bank[:], func=ACT.Exp, bias=bias_of(TAU, t), scale=1.0)
+        def tau(u, t):
+            if t == 0:
+                ee[u] = work.tile([P, UW], F32, name="ee", tag="ee", bufs=BUFS["ee"])
+            bank = mx_group(TAU, t, xq[u], hq[u])
+            nc.scalar.activation(out=ee[u][:, chunk(t)], in_=bank[:], func=ACT.Exp, bias=bias_of(TAU, t), scale=1.0)
 
         def gate(u, t):
             if t == 0:
                 th[u] = work.tile([P, UW], F32, name="th", tag="th", bufs=BUFS["th"], align_bytes=64)
-            bank = mx_group(GATE, t, hc[u], hs[u], u)
+            bank = mx_group(GATE, t, xq[u], hq[u])
             nc.scalar.activation(out=th[u][:, chunk(t)], in_=bank[:], func=ACT.Tanh, bias=bias_of(GATE, t), scale=0.5)
 
         def candidate(u, t):
             if t == 0:
-                tag = "ht" if u < UNITS - 2 else "xh"
+                tag = "ht" if u < UNITS - 2 else "th"
                 ht[u] = work.tile([P, UW], F32, name="ht", tag=tag, bufs=BUFS[tag], align_bytes=64)
-            bank = mx_group(CAND, t, dc[u], ds[u], u)
+            bank = mx_group(CAND, t, xq[u], dq[u])
             nc.scalar.activation(out=ht[u][:, chunk(t)], in_=bank[:], func=ACT.Tanh, bias=bias_of(CAND, t), scale=1.0)
 
         def gate_hidden(u):
@@ -235,11 +218,6 @@ def tile_ltccell_t_kernel(tc, x, hidden, W_tau, b_tau, W_r, b_r, W_h, b_h, out):
                 op0=ALU.add,
                 op1=ALU.mult,
             )
-
-        def quantise_gated(u):
-            dc[u] = work.tile([P, NCOL], U32, name="dc", tag="dc", bufs=BUFS["dc"], align_bytes=64)
-            ds[u] = work.tile([P, NCOL], U8, name="ds", tag="ds", bufs=BUFS["dc"], align_bytes=64)
-            quantise(dc[u], ds[u], dg[u], 0, NCOL)
 
         def softplus(u):
             nc.scalar.activation(out=ee[u][:], in_=ee[u][:], func=ACT.Ln, bias=1.0, scale=1.0)
@@ -287,12 +265,13 @@ def tile_ltccell_t_kernel(tc, x, hidden, W_tau, b_tau, W_r, b_r, W_h, b_h, out):
             result = work.tile([P, 2 * NCOL], F32, name="oo", tag="hg", bufs=BUFS["hg"], align_bytes=64)
             for i in range(2):
                 nc.vector.tensor_tensor(
-                    out=row_view(result[:, chunk(i)]), in0=in_order(banks[i]), in1=row_view(h2[u][:, chunk(s0 + i)]), op=ALU.add
+                    out=row_view(result[:, chunk(i)]),
+                    in0=in_order(banks[i]),
+                    in1=row_view(h2[u][:, chunk(s0 + i)]),
+                    op=ALU.add,
                 )
             o = u * UW + s0 * NCOL
             nc.sync.dma_start(out=ov[:, o : o + 2 * NCOL], in_=result[:])
-            if s0 + 2 == PAIRS:
-                load_hidden_again(NEXT[u])
 
 
         def square_tau(u, i):
@@ -300,31 +279,6 @@ def tile_ltccell_t_kernel(tc, x, hidden, W_tau, b_tau, W_r, b_r, W_h, b_h, out):
             nc.vector.scalar_tensor_tensor(
                 out=ee[u][:, w], in0=ee[u][:, w], scalar=2 * EPS, in1=ee[u][:, w], op0=ALU.add, op1=ALU.mult
             )
-
-
-        def invert_turned(u):
-            nc.scalar.activation(out=ee[u][:], in_=ee[u][:], func=ACT.Abs_reciprocal_sqrt, bias=EPS * EPS, scale=1.0)
-
-        def add_hidden(u, s0):
-            for s in (s0, s0 + 1):
-                diff_bank[u, s] = new_bank()
-                nc.tensor.matmul(
-                    out=diff_bank[u, s][:],
-                    lhsT=posid[:],
-                    rhs=h2[u][:, chunk(s)].rearrange("p (m t) -> p t m", t=PACK),
-                    start=True,
-                    stop=False,
-                )
-            for s in (s0, s0 + 1):
-                turn_back(diff_bank[u, s], ht[u], s, False)
-
-        def copy_out(u, s0):
-            result = work.tile([P, 2 * NCOL], F32, name="oo", tag="hg", bufs=BUFS["hg"], align_bytes=64)
-            for i in range(2):
-                nc.scalar.copy(out=row_view(result[:, chunk(i)]), in_=in_order(diff_bank[u, s0 + i]))
-            o = u * UW + s0 * NCOL
-            nc.sync.dma_start(out=ov[:, o : o + 2 * NCOL], in_=result[:])
-
 
         def turn_tau(u, s0):
             for s in (s0, s0 + 1):
@@ -344,71 +298,63 @@ def tile_ltccell_t_kernel(tc, x, hidden, W_tau, b_tau, W_r, b_r, W_h, b_h, out):
             for s in (s0, s0 + 1):
                 turn_back(diff_bank[u, s], ht[u], s, False)
 
+        def natural_root(u, s, eps):
+            nc.scalar.activation(
+                out=row_view(lt[u][:, chunk(s)]),
+                in_=in_order(tau_bank[u, s]),
+                func=ACT.Abs_reciprocal_sqrt,
+                bias=eps,
+                scale=1.0,
+            )
+
+        def divide(u, s, result):
+            nc.vector.tensor_tensor(
+                out=row_view(result), in0=in_order(diff_bank[u, s]), in1=row_view(lt[u][:, chunk(s)]), op=ALU.mult
+            )
+
+        def store(u, s0, n, result, engine=nc.vector):
+            w = slice(s0 * NCOL, (s0 + n) * NCOL)
+            engine.tensor_tensor(out=result, in0=result, in1=h2[u][:, w], op=ALU.add)
+            o = u * UW
+            nc.sync.dma_start(out=ov[:, o + s0 * NCOL : o + (s0 + n) * NCOL], in_=result)
+
+        def last_roots():
+            lt[LAST] = work.tile([P, UW], F32, name="lt", tag="ee", bufs=BUFS["ee"])
+            for s in range(PAIRS):
+                natural_root(LAST, s, EPS)
+
+        def last_update():
+            results = {}
+
+            def first(s0):
+                difference(LAST, s0)
+                results[s0] = work.tile([P, 2 * NCOL], F32, name="oo", tag="hg", bufs=BUFS["hg"], align_bytes=64)
+                for i in range(2):
+                    divide(LAST, s0 + i, results[s0][:, chunk(i)])
+
+            def second(s0):
+                w = slice(s0 * NCOL, (s0 + 2) * NCOL)
+                nc.vector.tensor_tensor(out=results[s0][:], in0=results[s0][:], in1=lt[LAST][:, w], op=ALU.mult)
+
+            def third(s0):
+                store(LAST, s0, 2, results[s0][:])
+
+            return [(lambda f=f, s0=s0: f(s0)) for f in (first, second, third) for s0 in (0, 2)]
+
         def invert_tau(u, s0):
             if s0 == 0:
                 lt[u] = work.tile([P, UW], F32, name="lt", tag="ht", bufs=BUFS["ht"], align_bytes=64)
             for s in (s0, s0 + 1):
-                nc.scalar.activation(
-                    out=row_view(lt[u][:, chunk(s)]),
-                    in_=in_order(tau_bank[u, s]),
-                    func=ACT.Abs_reciprocal_sqrt,
-                    bias=EPS * EPS if u in SQUARED else EPS,
-                    scale=1.0,
-                )
-            if u in SQUARED:
-                return
+                natural_root(u, s, EPS * EPS if u in SQUARED else EPS)
+            if u not in SQUARED:
+                for s in (s0, s0 + 1):
+                    nc.scalar.activation(out=lt[u][:, chunk(s)], in_=lt[u][:, chunk(s)], func=ACT.Square)
+
+        def finish(u, s0):
             for s in (s0, s0 + 1):
-                nc.scalar.activation(out=lt[u][:, chunk(s)], in_=lt[u][:, chunk(s)], func=ACT.Square)
-
-        def natural_root(u):
-            lt[u] = work.tile([P, UW], F32, name="lt", tag="ee", bufs=BUFS["ee"])
-            for s in range(PAIRS):
-                nc.scalar.activation(
-                    out=row_view(lt[u][:, chunk(s)]),
-                    in_=in_order(tau_bank[u, s]),
-                    func=ACT.Abs_reciprocal_sqrt,
-                    bias=EPS,
-                    scale=1.0,
-                )
-
-        def natural_update(u):
-            parts = {}
-
-            def first(s0):
-                difference(u, s0)
-                parts[s0] = work.tile([P, 2 * NCOL], F32, name="oo", tag="hg", bufs=BUFS["hg"], align_bytes=64)
-                for i in range(2):
-                    nc.vector.tensor_tensor(
-                        out=row_view(parts[s0][:, chunk(i)]),
-                        in0=in_order(diff_bank[u, s0 + i]),
-                        in1=row_view(lt[u][:, chunk(s0 + i)]),
-                        op=ALU.mult,
-                    )
-
-            def second(s0):
-                w = slice(s0 * NCOL, (s0 + 2) * NCOL)
-                nc.vector.tensor_tensor(out=parts[s0][:], in0=parts[s0][:], in1=lt[u][:, w], op=ALU.mult)
-
-            def third(s0):
-                w = slice(s0 * NCOL, (s0 + 2) * NCOL)
-                nc.vector.tensor_tensor(out=parts[s0][:], in0=parts[s0][:], in1=h2[u][:, w], op=ALU.add)
-                o = u * UW + s0 * NCOL
-                nc.sync.dma_start(out=ov[:, o : o + 2 * NCOL], in_=parts[s0][:])
-                if s0 + 2 == PAIRS:
-                    load_hidden_again(NEXT[u])
-
-            return [(lambda f=f, s0=s0: f(s0)) for f in (first, second, third) for s0 in (0, 2)]
-
-        def divide(u, s0):
-            for s in (s0, s0 + 1):
-                part = row_view(lt[u][:, chunk(s)])
-                nc.vector.tensor_tensor(out=part, in0=in_order(diff_bank[u, s]), in1=part, op=ALU.mult)
-
-        def finish(u, s0, n=2):
-            w = slice(s0 * NCOL, (s0 + n) * NCOL)
-            nc.vector.tensor_tensor(out=lt[u][:, w], in0=lt[u][:, w], in1=h2[u][:, w], op=ALU.add)
-            o = u * UW
-            nc.sync.dma_start(out=ov[:, o + s0 * NCOL : o + (s0 + n) * NCOL], in_=lt[u][:, w])
+                divide(u, s, lt[u][:, chunk(s)])
+            store(u, s0, 1, lt[u][:, chunk(s0)])
+            store(u, s0 + 1, 1, lt[u][:, chunk(s0 + 1)], nc.gpsimd if u < 5 else nc.vector)
 
 
         def jobs(f, u, n=PACK):
@@ -437,20 +383,22 @@ def tile_ltccell_t_kernel(tc, x, hidden, W_tau, b_tau, W_r, b_r, W_h, b_h, out):
         def settle():
             run(lambda: None)
 
-        def settle_job():
-            return
+        def bring(u, x_by=on_vector, h_by=on_vector):
+            return [lambda: bring_x(u, x_by), lambda: bring_h(u, h_by), lambda: quantise_x(u), lambda: quantise_h(u)]
 
-        def bring(u, cx=on_vector, ch=on_vector):
-            return [lambda: bring_x(u, cx), lambda: bring_h(u, ch), lambda: quantise_x(u), lambda: quantise_h(u)]
-
-        def bring_soon(u, cx=on_vector, ch=on_vector):
-            return [lambda: bring_x(u, cx), (lambda: quantise_x(u),), lambda: bring_h(u, ch), (lambda: quantise_h(u),)]
+        def bring_by_scalar(u):
+            return [
+                lambda: bring_x(u, on_scalar),
+                (lambda: quantise_x(u),),
+                lambda: bring_h(u, on_scalar),
+                (lambda: quantise_h(u),),
+            ]
 
         def gating(u):
             return [lambda: gate_hidden(u), (lambda: quantise_gated(u),)]
 
         def tau_and_gate(u):
-            return [lambda: open_tau(u)] + jobs(tau, u) + jobs(gate, u)
+            return jobs(tau, u) + jobs(gate, u)
 
         def update(u):
             return [
@@ -465,17 +413,18 @@ def tile_ltccell_t_kernel(tc, x, hidden, W_tau, b_tau, W_r, b_r, W_h, b_h, out):
         def result(u):
             return [lambda: give_back(u, 0), lambda: give_back(u, 2)]
 
+
         make_identity(nc, ident[:])
         load_weight(TAU, nc.vector)
-        open_inputs(0)
-        load_rows(xn[0], xv, 0, 0, UROWS)
-        load_rows(hn[0], hv, 0, 0, UROWS)
+        load_x(0)
+        load_h(0)
         load_biases()
         load_weight(GATE, nc.gpsimd)
         load_weight(CAND, nc.gpsimd)
-        load_inputs(1)
+        load_x(1)
+        load_h(1)
         halve_hidden_columns()
-        signed_identities()
+        negate_identity()
 
         prepare_weight(TAU, (on_scalar, on_vector))
         prepare_biases()
@@ -485,17 +434,19 @@ def tile_ltccell_t_kernel(tc, x, hidden, W_tau, b_tau, W_r, b_r, W_h, b_h, out):
         quantise_x(0)
         quantise_h(0)
         prepare_weight(GATE, (on_scalar, on_vector))
-        weave([lambda: open_tau(0)] + jobs(tau, 0), [lambda: quantise_weight(GATE)] + bring_soon(1, on_scalar, on_scalar)[:2])
-        weave(jobs(gate, 0), bring_soon(1, on_scalar, on_scalar)[2:])
+        weave(jobs(tau, 0), [lambda: quantise_weight(GATE)] + bring_by_scalar(1)[:2])
+        weave(jobs(gate, 0), bring_by_scalar(1)[2:])
         settle()
         prepare_weight(CAND, (on_vector, on_vector))
-        for u in range(AGAIN):
+        for u in FIRST:
             load_hidden_again(u)
-        weave(tau_and_gate(1), bring_soon(2, on_scalar, on_scalar) + gating(0))
+        weave(tau_and_gate(1), bring_by_scalar(2) + gating(0))
         weave(tau_and_gate(2), [lambda: quantise_weight(CAND)] + gating(1))
 
-        main = [lambda u=u: softplus(u) for u in FIRST] + [lambda u=u: root(u) for u in FIRST[:2]] + [lambda: natural_root(2)]
-        weave(main, bring(3) + bring(4) + bring(5) + [lambda: turn_tau(2, 0), lambda: turn_tau(2, 2)] + bring(6))
+        main = [lambda u=u: softplus(u) for u in FIRST] + [lambda: root(0), lambda: root(1), last_roots]
+        turn_last = [lambda: turn_tau(LAST, 0), lambda: turn_tau(LAST, 2)]
+        weave(main, bring(3) + bring(4) + bring(5) + turn_last + bring(6))
+
 
         weave(jobs(candidate, 0), gating(2))
         weave(tau_and_gate(3), [])
@@ -504,15 +455,17 @@ def tile_ltccell_t_kernel(tc, x, hidden, W_tau, b_tau, W_r, b_r, W_h, b_h, out):
         weave(jobs(candidate, 2), update(1)[2:])
         weave(tau_and_gate(5), gating(4) + bring(7, on_scalar, on_vector)[:2])
         weave(tau_and_gate(6), gating(5) + bring(7, on_scalar, on_vector)[2:])
+        for u in (5, 6, 3, 7):
+            load_hidden_again(u)
         weave(jobs(candidate, 3) + jobs(candidate, 4), gating(6))
-        weave(tau_and_gate(7), [settle_job])
+        weave(tau_and_gate(7), [lambda: None])
         weave(jobs(candidate, 5), gating(7))
-        weave(jobs(candidate, 6), [settle_job])
+        weave(jobs(candidate, 6), [lambda: None])
         weave(jobs(candidate, 7), [])
-        load_hidden_again(5)
-        load_hidden_again(6)
 
-        weave([lambda u=u: softplus(u) for u in SECOND], result(0) + result(1) + [lambda: square_tau(3, 0), lambda: square_tau(3, 1)] + natural_update(2))
+        squares = [(lambda u=u, i=i: square_tau(u, i)) for u in SQUARED for i in range(2)]
+        side = result(0) + [lambda: load_hidden_again(4)] + result(1) + squares + last_update()
+        weave([lambda u=u: softplus(u) for u in SECOND], side)
 
         steps = [(u, s0) for u in SECOND for s0 in (0, 2)]
 
@@ -525,7 +478,5 @@ def tile_ltccell_t_kernel(tc, x, hidden, W_tau, b_tau, W_r, b_r, W_h, b_h, out):
         prepare(1)
         for i in range(len(steps)):
             invert_tau(*steps[i])
-            divide(*steps[i])
-            for s in (0, 1):
-                finish(steps[i][0], steps[i][1] + s, 1)
+            finish(*steps[i])
             prepare(i + 2)

from contextlib import ExitStack

import concourse.mybir as mybir
from concourse.masks import make_identity

F32 = mybir.dt.float32
BF16 = mybir.dt.bfloat16
U32 = mybir.dt.uint32
U8 = mybir.dt.uint8
FP8X4 = mybir.dt.float8_e4m3fn_x4
ACT = mybir.ActivationFunctionType
ALU = mybir.AluOpType

P = 128
HALF = P // 2
PACK = 4
B, I, H = 8192, 256, 256
FLOPS = 3 * 2 * B * (I + H) * H
ROWS = B // P
UNITS = 8
UROWS = ROWS // UNITS
PAIRS = UROWS // 2
NCOL = PAIRS * P
UW = PACK * NCOL
WCOL = 2 * PACK * P
EPS = 1e-6
TAU, GATE, CAND = 0, 1, 2
FIRST, SECOND = (0, 1, 2), (3, 4, 5, 6, 7)
LAST = 2
SQUARED = (3,)
LEAD = 2
AGAIN = ("h2", "h2", "h2", "hn", "h2", "xn", "xn", "hn")

BUFS = {"th": 2, "ht": 6, "xn": 2, "hn": 2, "h2": 3, "xg": 1, "hg": 8, "xc": 7, "hc": 4, "dg": 1, "dc": 5, "ee": 6}


def tile_ltccell_t_kernel(tc, x, hidden, W_tau, b_tau, W_r, b_r, W_h, b_h, out):
    nc = tc.nc
    xv = x.rearrange("(p q) k -> p (q k)", q=ROWS)
    hv = hidden.rearrange("(p q) k -> p (q k)", q=ROWS)
    ov = out.rearrange("(p q) k -> p (q k)", q=ROWS)
    weights = (W_tau, W_r, W_h)
    biases = (b_tau, b_r, b_h)
    on_scalar, on_vector = nc.scalar.copy, nc.vector.tensor_copy

    with ExitStack() as ctx:
        const = ctx.enter_context(tc.tile_pool(name="const", bufs=1))
        work = ctx.enter_context(tc.tile_pool(name="work", bufs=2))
        psum = ctx.enter_context(tc.psum_pool(name="psum", bufs=8))
        ctx.enter_context(tc.manual_schedule())

        ident = const.tile([P, P], F32, name="ident")
        negid = const.tile([P, P], BF16, name="negid")
        braw = const.tile([P, 3, 16], BF16, name="braw")
        bias = const.tile([P, 3 * PACK], F32, name="bias")
        wc = const.tile([P, 3 * WCOL], U32, name="wc", align_bytes=64)
        ws = const.tile([P, 3 * WCOL], U8, name="ws", align_bytes=64)

        xn, hn, h2, xg, hg, xq, hq, dq = {}, {}, {}, {}, {}, {}, {}, {}
        wn, wg, th, dg, ee, ht, lt = {}, {}, {}, {}, {}, {}, {}
        tau_bank, diff_bank = {}, {}

        def chunk(t):
            return slice(t * NCOL, (t + 1) * NCOL)


        def load_weight(w, zero_engine):
            wn[w] = work.tile([P, 2, 768], BF16, name="wn", tag="h2", bufs=BUFS["h2"], align_bytes=64)
            src = weights[w].rearrange("(c p) k -> p c k", p=P)
            nc.sync.dma_start(out=wn[w][:, :, 0:512], in_=src)
            nc.sync.dma_start(out=wn[w][:, :, 512:768], in_=src[:, :, 0:256])
            wg[w] = work.tile([P, 2 * WCOL], F32, name="wg", tag="ht", bufs=BUFS["ht"], align_bytes=64)
            z = wg[w][:].rearrange("p (a m u) -> p a m u", a=2 * PACK, m=P, u=2)
            zero_engine.memset(z[0:HALF, :, HALF:P, :], 0.0)
            zero_engine.memset(z[HALF:P, :, 0:HALF, :], 0.0)

        def load_biases():
            for w in range(3):
                src = biases[w].rearrange("(j t) -> j t", t=PACK)
                nc.sync.dma_start(out=braw[0:HALF, w, 0:PACK], in_=src)
                nc.sync.dma_start(out=braw[HALF:P, w, 0:PACK], in_=src)

        def prepare_biases():
            nc.vector.tensor_copy(out=bias[:].rearrange("p (w t) -> p w t", w=3), in_=braw[:, :, 0:PACK])
            gate_bias = bias[:, PACK * GATE : PACK * GATE + PACK]
            nc.vector.tensor_scalar(out=gate_bias, in0=gate_bias, scalar1=0.5, scalar2=None, op0=ALU.mult)

        def halve_hidden_columns():
            part = wn[CAND][:, :, 256:512]
            nc.gpsimd.tensor_scalar(out=part, in0=part, scalar1=0.5, scalar2=0.0, op0=ALU.mult, op1=ALU.add)

        def negate_identity():
            make_identity(nc, negid[:])
            nc.gpsimd.tensor_scalar(out=negid[:], in0=negid[:], scalar1=-1.0, scalar2=0.0, op0=ALU.mult, op1=ALU.add)

        def prepare_weight(w, copies):
            words = wn[w][:].rearrange("p c k -> p (c k)").bitcast(F32).rearrange("p (c k) -> p c k", c=2)
            dv = wg[w][:].rearrange("p (t a m u) -> p t a m u", t=PACK, a=2, m=P, u=2)
            for order in range(2):
                bank = psum.tile([P, 2, 2, P], F32, name="wt", tag="bank")
                for c in range(2):
                    sv = words[:, c, P * order : P * order + 2 * P].rearrange("p (m u) -> p m u", u=2)
                    for u in range(2):
                        nc.tensor.transpose(bank[:, u, c, :], sv[:, :, u], ident[:])
                for half in range(2):
                    rows = slice(HALF * half, HALF * half + HALF)
                    part = (order + half) % 2
                    for c in range(2):
                        m0 = HALF * half + 32 * c
                        copies[order](
                            out=dv[rows, :, part, m0 : m0 + 32, :],
                            in_=bank[rows, :, c, :].rearrange("p u (q t) -> p t q u", t=PACK),
                        )

        def quantise_weight(w):
            cols = slice(w * WCOL, (w + 1) * WCOL)
            nc.vector.quantize_mx(out=wc[:, cols].bitcast(FP8X4), scales=ws[:, cols], in_=wg[w][:].bitcast(BF16))


        def load_x(u):
            if u < UNITS:
                xn[u] = work.tile([P, UW], BF16, name="xn", tag="xn", bufs=BUFS["xn"], align_bytes=64)
                nc.sync.dma_start(out=xn[u][:], in_=xv[:, u * UW : (u + 1) * UW])

        def load_h(u):
            if u < UNITS:
                hn[u] = work.tile([P, UW], BF16, name="hn", tag="hn", bufs=BUFS["hn"], align_bytes=64)
                nc.sync.dma_start(out=hn[u][:], in_=hv[:, u * UW : (u + 1) * UW])

        def load_hidden_again(u):
            tag = AGAIN[u]
            h2[u] = work.tile([P, UW], BF16, name="h2", tag=tag, bufs=BUFS[tag], align_bytes=64)
            nc.sync.dma_start(out=h2[u][:], in_=hv[:, u * UW : (u + 1) * UW])

        def turn_rows(natural, transposed, copy):
            words = natural[:].bitcast(F32).rearrange("p (s m u) -> p s m u", m=P, u=2)
            dv = transposed[:].rearrange("p (s m u) -> p s m u", m=P, u=2)
            banks = []
            for s0 in (0, 2):
                bank = psum.tile([P, 2, 2, P], F32, name="tin", tag="bank")
                banks.append(bank)
                for s in range(2):
                    for u in range(2):
                        nc.tensor.transpose(bank[:, s, u, :], words[:, s0 + s, :, u], ident[:])
            for s0, bank in zip((0, 2), banks):
                copy(out=dv[:, s0 : s0 + 2, :, :], in_=bank[:].rearrange("p s u m -> p s m u"))

        def bring_x(u, copy=on_vector):
            xg[u] = work.tile([P, UW // 2], F32, name="xg", tag="xg", bufs=BUFS["xg"], align_bytes=64)
            turn_rows(xn[u], xg[u], copy)
            load_x(u + LEAD)

        def bring_h(u, copy=on_vector):
            hg[u] = work.tile([P, UW // 2], F32, name="hg", tag="hg", bufs=BUFS["hg"], align_bytes=64)
            turn_rows(hn[u], hg[u], copy)
            load_h(u + LEAD)

        def quantise(tag, values):
            codes = work.tile([P, NCOL], U32, name="codes", tag=tag, bufs=BUFS[tag], align_bytes=64)
            scales = work.tile([P, NCOL], U8, name="scales", tag=tag + "s", bufs=BUFS[tag], align_bytes=64)
            nc.vector.quantize_mx(out=codes[:].bitcast(FP8X4), scales=scales[:], in_=values)
            return codes, scales

        def quantise_x(u):
            xq[u] = quantise("xc", xg[u][:].bitcast(BF16))

        def quantise_h(u):
            hq[u] = quantise("hc", hg[u][:].bitcast(BF16))

        def quantise_gated(u):
            dq[u] = quantise("dc", dg[u][:])


        def mx_group(w, t, first, second):
            bank = psum.tile([P, NCOL], F32, name="mx", tag="bank")
            for part, (codes, scales) in enumerate((first, second)):
                o = w * WCOL + (2 * t + part) * P
                nc.tensor.matmul_mx(
                    out=bank[:],
                    lhsT=wc[:, o : o + P].bitcast(FP8X4),
                    lhsT_scale=ws[:, o : o + P],
                    rhs=codes[:].bitcast(FP8X4),
                    rhs_scale=scales[:],
                    start=(part == 0),
                    stop=(part == 1),
                )
            return bank

        def bias_of(w, t):
            return bias[:, PACK * w + t : PACK * w + t + 1]

        def tau(u, t):
            if t == 0:
                ee[u] = work.tile([P, UW], F32, name="ee", tag="ee", bufs=BUFS["ee"])
            bank = mx_group(TAU, t, xq[u], hq[u])
            nc.scalar.activation(out=ee[u][:, chunk(t)], in_=bank[:], func=ACT.Exp, bias=bias_of(TAU, t), scale=1.0)

        def gate(u, t):
            if t == 0:
                th[u] = work.tile([P, UW], F32, name="th", tag="th", bufs=BUFS["th"], align_bytes=64)
            bank = mx_group(GATE, t, xq[u], hq[u])
            nc.scalar.activation(out=th[u][:, chunk(t)], in_=bank[:], func=ACT.Tanh, bias=bias_of(GATE, t), scale=0.5)

        def candidate(u, t):
            if t == 0:
                tag = "ht" if u < UNITS - 2 else "th"
                ht[u] = work.tile([P, UW], F32, name="ht", tag=tag, bufs=BUFS[tag], align_bytes=64)
            bank = mx_group(CAND, t, xq[u], dq[u])
            nc.scalar.activation(out=ht[u][:, chunk(t)], in_=bank[:], func=ACT.Tanh, bias=bias_of(CAND, t), scale=1.0)

        def gate_hidden(u):
            dg[u] = work.tile([P, UW], BF16, name="dg", tag="dg", bufs=BUFS["dg"], align_bytes=64)
            nc.vector.scalar_tensor_tensor(
                out=dg[u][:].rearrange("p (c t) -> p c t", t=PACK),
                in0=th[u][:].rearrange("p (t c) -> p c t", t=PACK),
                scalar=1.0,
                in1=hg[u][:].bitcast(BF16).rearrange("p (c t) -> p c t", t=PACK),
                op0=ALU.add,
                op1=ALU.mult,
            )

        def softplus(u):
            nc.scalar.activation(out=ee[u][:], in_=ee[u][:], func=ACT.Ln, bias=1.0, scale=1.0)


        def root(u):
            nc.scalar.activation(out=ee[u][:], in_=ee[u][:], func=ACT.Abs_reciprocal_sqrt, bias=EPS, scale=1.0)

        def subtract(u, i):
            planes = hg[u][:].bitcast(BF16).rearrange("p (c t) -> p t c", t=PACK)[:, 2 * i : 2 * i + 2, :]
            part = ht[u][:].rearrange("p (t c) -> p t c", t=PACK)[:, 2 * i : 2 * i + 2, :]
            nc.vector.tensor_tensor(out=part, in0=part, in1=planes, op=ALU.subtract)

        def multiply(u, i):
            w = slice(i * 2 * NCOL, (i + 1) * 2 * NCOL)
            nc.vector.tensor_tensor(out=ht[u][:, w], in0=ht[u][:, w], in1=ee[u][:, w], op=ALU.mult)


        def new_bank():
            return psum.tile([P, PACK, P], F32, name="nat", tag="bank")

        def turn_back(bank, planes, s, start):
            for t in range(PACK):
                o = t * NCOL + s * P
                nc.tensor.matmul(
                    out=bank[:, t, :],
                    lhsT=planes[:, o : o + P],
                    rhs=ident[:],
                    is_transpose=True,
                    start=start,
                    stop=start or t == PACK - 1,
                )

        def in_order(bank):
            return bank[:].rearrange("p t m -> p m t")

        def row_view(ap):
            return ap.rearrange("p (m t) -> p m t", t=PACK)

        def give_back(u, s0):
            banks = []
            for s in (s0, s0 + 1):
                banks.append(new_bank())
                turn_back(banks[-1], ht[u], s, True)
            result = work.tile([P, 2 * NCOL], F32, name="oo", tag="hg", bufs=BUFS["hg"], align_bytes=64)
            for i in range(2):
                nc.vector.tensor_tensor(
                    out=row_view(result[:, chunk(i)]),
                    in0=in_order(banks[i]),
                    in1=row_view(h2[u][:, chunk(s0 + i)]),
                    op=ALU.add,
                )
            o = u * UW + s0 * NCOL
            nc.sync.dma_start(out=ov[:, o : o + 2 * NCOL], in_=result[:])


        def square_tau(u, i):
            w = slice(i * 2 * NCOL, (i + 1) * 2 * NCOL)
            nc.vector.scalar_tensor_tensor(
                out=ee[u][:, w], in0=ee[u][:, w], scalar=2 * EPS, in1=ee[u][:, w], op0=ALU.add, op1=ALU.mult
            )

        def turn_tau(u, s0):
            for s in (s0, s0 + 1):
                tau_bank[u, s] = new_bank()
                turn_back(tau_bank[u, s], ee[u], s, True)

        def difference(u, s0):
            for s in (s0, s0 + 1):
                diff_bank[u, s] = new_bank()
                nc.tensor.matmul(
                    out=diff_bank[u, s][:],
                    lhsT=negid[:],
                    rhs=h2[u][:, chunk(s)].rearrange("p (m t) -> p t m", t=PACK),
                    start=True,
                    stop=False,
                )
            for s in (s0, s0 + 1):
                turn_back(diff_bank[u, s], ht[u], s, False)

        def natural_root(u, s, eps):
            nc.scalar.activation(
                out=row_view(lt[u][:, chunk(s)]),
                in_=in_order(tau_bank[u, s]),
                func=ACT.Abs_reciprocal_sqrt,
                bias=eps,
                scale=1.0,
            )

        def divide(u, s, result):
            nc.vector.tensor_tensor(
                out=row_view(result), in0=in_order(diff_bank[u, s]), in1=row_view(lt[u][:, chunk(s)]), op=ALU.mult
            )

        def store(u, s0, n, result, engine=nc.vector):
            w = slice(s0 * NCOL, (s0 + n) * NCOL)
            engine.tensor_tensor(out=result, in0=result, in1=h2[u][:, w], op=ALU.add)
            o = u * UW
            nc.sync.dma_start(out=ov[:, o + s0 * NCOL : o + (s0 + n) * NCOL], in_=result)

        def last_roots():
            lt[LAST] = work.tile([P, UW], F32, name="lt", tag="ee", bufs=BUFS["ee"])
            for s in range(PAIRS):
                natural_root(LAST, s, EPS)

        def last_update():
            results = {}

            def first(s0):
                difference(LAST, s0)
                results[s0] = work.tile([P, 2 * NCOL], F32, name="oo", tag="hg", bufs=BUFS["hg"], align_bytes=64)
                for i in range(2):
                    divide(LAST, s0 + i, results[s0][:, chunk(i)])

            def second(s0):
                w = slice(s0 * NCOL, (s0 + 2) * NCOL)
                nc.vector.tensor_tensor(out=results[s0][:], in0=results[s0][:], in1=lt[LAST][:, w], op=ALU.mult)

            def third(s0):
                store(LAST, s0, 2, results[s0][:])

            return [(lambda f=f, s0=s0: f(s0)) for f in (first, second, third) for s0 in (0, 2)]

        def invert_tau(u, s0):
            if s0 == 0:
                lt[u] = work.tile([P, UW], F32, name="lt", tag="ht", bufs=BUFS["ht"], align_bytes=64)
            for s in (s0, s0 + 1):
                natural_root(u, s, EPS * EPS if u in SQUARED else EPS)
            if u not in SQUARED:
                for s in (s0, s0 + 1):
                    nc.scalar.activation(out=lt[u][:, chunk(s)], in_=lt[u][:, chunk(s)], func=ACT.Square)

        def finish(u, s0):
            for s in (s0, s0 + 1):
                divide(u, s, lt[u][:, chunk(s)])
            store(u, s0, 1, lt[u][:, chunk(s0)])
            store(u, s0 + 1, 1, lt[u][:, chunk(s0 + 1)], nc.gpsimd if u < 5 else nc.vector)


        def jobs(f, u, n=PACK):
            return [(lambda t=t: f(u, t)) for t in range(n)]

        late = []

        def run(f):
            if isinstance(f, tuple):
                late.append(f[0])
                return
            f()
            for g in late:
                g()
            late.clear()

        def weave(main, side):
            done = 0
            for i, f in enumerate(main):
                f()
                upto = (i + 1) * len(side) // len(main)
                for g in side[done:upto]:
                    run(g)
                done = upto

        def settle():
            run(lambda: None)

        def bring(u, x_by=on_vector, h_by=on_vector):
            return [lambda: bring_x(u, x_by), lambda: bring_h(u, h_by), lambda: quantise_x(u), lambda: quantise_h(u)]

        def bring_by_scalar(u):
            return [
                lambda: bring_x(u, on_scalar),
                (lambda: quantise_x(u),),
                lambda: bring_h(u, on_scalar),
                (lambda: quantise_h(u),),
            ]

        def gating(u):
            return [lambda: gate_hidden(u), (lambda: quantise_gated(u),)]

        def tau_and_gate(u):
            return jobs(tau, u) + jobs(gate, u)

        def update(u):
            return [
                lambda: subtract(u, 0),
                lambda: subtract(u, 1),
                lambda: multiply(u, 0),
                lambda: multiply(u, 1),
                lambda: multiply(u, 0),
                lambda: multiply(u, 1),
            ]

        def result(u):
            return [lambda: give_back(u, 0), lambda: give_back(u, 2)]


        make_identity(nc, ident[:])
        load_weight(TAU, nc.vector)
        load_x(0)
        load_h(0)
        load_biases()
        load_weight(GATE, nc.gpsimd)
        load_weight(CAND, nc.gpsimd)
        load_x(1)
        load_h(1)
        halve_hidden_columns()
        negate_identity()

        prepare_weight(TAU, (on_scalar, on_vector))
        prepare_biases()
        bring_x(0, on_scalar)
        quantise_weight(TAU)
        bring_h(0, on_scalar)
        quantise_x(0)
        quantise_h(0)
        prepare_weight(GATE, (on_scalar, on_vector))
        weave(jobs(tau, 0), [lambda: quantise_weight(GATE)] + bring_by_scalar(1)[:2])
        weave(jobs(gate, 0), bring_by_scalar(1)[2:])
        settle()
        prepare_weight(CAND, (on_vector, on_vector))
        for u in FIRST:
            load_hidden_again(u)
        weave(tau_and_gate(1), bring_by_scalar(2) + gating(0))
        weave(tau_and_gate(2), [lambda: quantise_weight(CAND)] + gating(1))

        main = [lambda u=u: softplus(u) for u in FIRST] + [lambda: root(0), lambda: root(1), last_roots]
        turn_last = [lambda: turn_tau(LAST, 0), lambda: turn_tau(LAST, 2)]
        weave(main, bring(3) + bring(4) + bring(5) + turn_last + bring(6))


        weave(jobs(candidate, 0), gating(2))
        weave(tau_and_gate(3), [])
        weave(jobs(candidate, 1), update(0))
        weave(tau_and_gate(4), gating(3) + update(1)[:2])
        weave(jobs(candidate, 2), update(1)[2:])
        weave(tau_and_gate(5), gating(4) + bring(7, on_scalar, on_vector)[:2])
        weave(tau_and_gate(6), gating(5) + bring(7, on_scalar, on_vector)[2:])
        for u in (5, 6, 3, 7):
            load_hidden_again(u)
        weave(jobs(candidate, 3) + jobs(candidate, 4), gating(6))
        weave(tau_and_gate(7), [lambda: None])
        weave(jobs(candidate, 5), gating(7))
        weave(jobs(candidate, 6), [lambda: None])
        weave(jobs(candidate, 7), [])

        squares = [(lambda u=u, i=i: square_tau(u, i)) for u in SQUARED for i in range(2)]
        side = result(0) + [lambda: load_hidden_again(4)] + result(1) + squares + last_update()
        weave([lambda u=u: softplus(u) for u in SECOND], side)

        steps = [(u, s0) for u in SECOND for s0 in (0, 2)]

        def prepare(i):
            if i < len(steps):
                turn_tau(*steps[i])
                difference(*steps[i])

        prepare(0)
        prepare(1)
        for i in range(len(steps)):
            invert_tau(*steps[i])
            finish(*steps[i])
            prepare(i + 2)
